import numpy as np
import ml_dtypes


def mxq(x, axis, fmt="e4m3"):
    dtype, down = {"e4m3": (ml_dtypes.float8_e4m3fn, 7), "e5m2": (ml_dtypes.float8_e5m2, 14)}[fmt]
    v = np.moveaxis(np.asarray(x, np.float32).astype(ml_dtypes.bfloat16).astype(np.float64), axis, -1)
    blocks = v.reshape(v.shape[:-1] + (-1, 32))
    amax = np.abs(blocks).max(-1, keepdims=True)
    byte = np.maximum(np.where(amax > 0, np.frexp(amax)[1] - 1 + 127, 0) - down, 1)
    scale = np.exp2(byte - 127.0)
    codes = (blocks / scale).astype(np.float32).astype(dtype).astype(np.float64)
    return np.moveaxis((codes * scale).reshape(v.shape), -1, axis)


WIDE = False


def mx_kscale(k):
    if not WIDE:
        return np.ones(k)
    levels = np.array([10, -10, 5, -5, 0])
    a = np.random.permutation(np.resize(levels, k // 512 * 4)).reshape(k // 512, 4)
    idx = np.arange(k)
    return np.exp2(a[idx // 512, idx % 128 // 32])


BF16 = ml_dtypes.bfloat16


def bf(x):
    return np.asarray(x, np.float32).astype(BF16)


def f64(x):
    return np.asarray(x).astype(np.float64)


B, L, X, E, Y = 1, 1024, 4, 128, 4
XS = X - 1
PAIRS = [(x, y) for x in range(1, X) for y in range(min(x + 1, Y))]
P = len(PAIRS)
SCALE = 1.0 / np.sqrt(E)


def setup_inputs():
    a = np.log2(mx_kscale(L))
    a = a - a.max()
    g = np.where(a < 0, 0.25, 1.0) * np.exp2(-a)
    q = np.random.standard_normal((B, L, XS, E))
    q[..., 0] = 1.0
    k = np.random.standard_normal((B, P, L, E))
    r = np.random.standard_normal((B, P, L, E)) * 6.0 / np.sqrt(L)
    for p, (_, y) in enumerate(PAIRS):
        if y == 0:
            k[:, p, :, 0] += a * np.log(2.0) / SCALE
            r[:, p] *= g[:, None]
    return {"q_plus": bf(q), "key_plus": bf(k), "retrieval": bf(r)}


def reference(q_plus, key_plus, retrieval):
    q, k, r = f64(q_plus), f64(key_plus), f64(retrieval)
    heads = []
    for x in range(1, X):
        ps = [p for p, (i, _) in enumerate(PAIRS) if i == x]
        s = [(q[:, :, x - 1, :] @ k[:, p].transpose(0, 2, 1)) * SCALE for p in ps]
        top = np.maximum.reduce(s)
        e = [np.exp(v - top) for v in s]
        den = sum(e)
        heads.append(sum((mxq(ei / den, 2, "e4m3") @ mxq(r[:, p], 1, "e4m3")) for ei, p in zip(e, ps)))
    return np.stack(heads, 2)

@@ -1,0 +1,275 @@
+import math
+
+import concourse.masks as masks
+import concourse.mybir as mybir
+
+F32 = mybir.dt.float32
+BF16 = mybir.dt.bfloat16
+U32 = mybir.dt.uint32
+U8 = mybir.dt.uint8
+FP8X4 = mybir.dt.float8_e4m3fn_x4
+ACT = mybir.ActivationFunctionType
+ALU = mybir.AluOpType
+
+P = 128
+PACK = 4
+L = 1024
+E = 128
+PASSES = L // (P * PACK)
+CHUNKS = L // P
+SCALE = 1.0 / math.sqrt(E)
+PAIRS = 9
+NEGATED_PAIR = 1
+
+BLOCK_CHUNKS = 2
+STEPS = BLOCK_CHUNKS * PASSES
+BLOCKS = CHUNKS // BLOCK_CHUNKS
+SCORE_BANKS = 7
+
+LN_AT = STEPS
+RECIPROCAL_AT = LN_AT + 1
+MULTIPLY_AT = RECIPROCAL_AT + 1
+QUANTISE_AT = MULTIPLY_AT + 1
+
+FLOPS = 2 * 2 * PAIRS * L * L * E
+
+
+def first_pair(x):
+    return x * (x + 1) // 2 - 1
+
+
+def tile_anomalyattention_pa_kernel(tc, q_plus, key_plus, retrieval, out):
+    nc = tc.nc
+    q_view = q_plus[0].rearrange("(p c) x e -> p c x e", c=CHUNKS)
+    out_view = out[0].rearrange("(p c) x e -> p c x e", c=CHUNKS)
+
+    with tc.manual_schedule(), tc.tile_pool(name="keep", bufs=1) as keep, tc.tile_pool(
+        name="mx", bufs=2
+    ) as mx, tc.psum_pool(name="psum", bufs=1) as psum:
+        ident = keep.tile([P, P], BF16)
+        masks.make_identity(nc, ident[:])
+        q_t = keep.tile([P, 3, CHUNKS, P], BF16)
+        k_t = keep.tile([P, PAIRS, PASSES, PACK, P], BF16)
+        r_codes = keep.tile([P, PAIRS, PASSES, E], U32, align_bytes=64)
+        r_scales = keep.tile([P, PAIRS, PASSES, E], U8, align_bytes=64)
+
+        def score_bank(name):
+            return psum.tile([P, PACK, P], F32, tag="bank", bufs=SCORE_BANKS, name=name)
+
+        def by_query(bank):
+            return bank[:].rearrange("p t l -> p l t")
+
+        def new_codes(x):
+            codes = mx.tile([P, x + 1, STEPS, P], U32, tag="codes", name="codes", align_bytes=64)
+            scales = mx.tile([P, x + 1, STEPS, P], U8, tag="scales", name="scales", align_bytes=64)
+            return codes, scales
+
+        def quantise_series(series, codes, scales, y):
+            nc.vector.quantize_mx(
+                out=codes[:, y, :, :].rearrange("p j l -> p (j l)").bitcast(FP8X4),
+                scales=scales[:, y, :, :].rearrange("p j l -> p (j l)"),
+                in_=series[:].rearrange("p j l t -> p (j l t)"),
+            )
+
+        def multiply_by_values(x, codes, scales):
+            acc = psum.tile([P, BLOCK_CHUNKS, E], F32, tag="acc", name="acc")
+            terms = [(g, y) for g in range(PASSES) for y in range(x + 1)]
+            for c in range(BLOCK_CHUNKS):
+                for g, y in terms:
+                    nc.tensor.matmul_mx(
+                        out=acc[:, c, :],
+                        lhsT=codes[:, y, c * PASSES + g, :].bitcast(FP8X4),
+                        lhsT_scale=scales[:, y, c * PASSES + g, :],
+                        rhs=r_codes[:, first_pair(x) + y, g, :].bitcast(FP8X4),
+                        rhs_scale=r_scales[:, first_pair(x) + y, g, :],
+                        start=((g, y) == terms[0]),
+                        stop=((g, y) == terms[-1]),
+                    )
+            return acc
+
+        def store_rows(x, block, acc, copy_out):
+            result = mx.tile([P, BLOCK_CHUNKS, E], F32, name="result")
+            copy_out(out=result[:], in_=acc[:])
+            chunks = slice(block * BLOCK_CHUNKS, (block + 1) * BLOCK_CHUNKS)
+            nc.sync.dma_start(out=out_view[:, chunks, x - 1, :], in_=result[:])
+
+        with tc.tile_pool(name="raw", bufs=1) as raw:
+            q_raw = raw.tile([P, CHUNKS, 3, E], BF16)
+            nc.sync.dma_start(out=q_raw[:], in_=q_view)
+            k_raw = []
+            r_raw = []
+            for pair in range(PAIRS):
+                k_raw.append(raw.tile([P, PASSES, PACK, E], BF16, name="k_raw%d" % pair))
+                r_raw.append(raw.tile([P, PASSES, PACK, E], BF16, name="r_raw%d" % pair))
+                nc.sync.dma_start(
+                    out=k_raw[pair][:], in_=key_plus[0, pair].rearrange("(g p t) e -> p g t e", g=PASSES, t=PACK)
+                )
+                nc.sync.dma_start(
+                    out=r_raw[pair][:], in_=retrieval[0, pair].rearrange("(g p t) e -> p g t e", g=PASSES, t=PACK)
+                )
+
+            def transpose_queries(x):
+                for half in range(CHUNKS // PACK):
+                    flipped = psum.tile([P, PACK, P], BF16, tag="bank", bufs=SCORE_BANKS, name="flipped")
+                    for i in range(PACK):
+                        nc.tensor.transpose(flipped[:, i, :], q_raw[:, half * PACK + i, x - 1, :], ident[:])
+                    nc.scalar.copy(out=q_t[:, x - 1, half * PACK : (half + 1) * PACK, :], in_=flipped[:])
+
+            def transpose_keys(pair):
+                for g in range(PASSES):
+                    flipped = psum.tile([P, PACK, P], BF16, tag="bank", bufs=SCORE_BANKS, name="flipped")
+                    for t in range(PACK):
+                        nc.tensor.transpose(flipped[:, t, :], k_raw[pair][:, g, t, :], ident[:])
+                    if pair == NEGATED_PAIR:
+                        nc.vector.tensor_scalar_mul(out=k_t[:, pair, g, :, :], in0=flipped[:], scalar1=-1.0)
+                    else:
+                        nc.vector.tensor_copy(out=k_t[:, pair, g, :, :], in_=flipped[:])
+
+            def quantise_values(pairs):
+                grouped = {}
+                for pair in pairs:
+                    grouped[pair] = raw.tile(
+                        [P, PASSES, E, PACK], BF16, tag="grouped", bufs=4, name="grouped", align_bytes=64
+                    )
+                    nc.vector.tensor_copy(out=grouped[pair][:], in_=r_raw[pair][:].rearrange("p g t e -> p g e t"))
+                for pair in pairs:
+                    nc.vector.quantize_mx(
+                        out=r_codes[:, pair, :, :].rearrange("p g e -> p (g e)").bitcast(FP8X4),
+                        scales=r_scales[:, pair, :, :].rearrange("p g e -> p (g e)"),
+                        in_=grouped[pair][:].rearrange("p g e t -> p (g e t)"),
+                    )
+
+            def head_one_series(block):
+                series = [
+                    raw.tile([P, STEPS, P, PACK], BF16, tag="series1", bufs=4, name="series1", align_bytes=64)
+                    for y in range(2)
+                ]
+                for j in range(STEPS):
+                    c = block * BLOCK_CHUNKS + j // PASSES
+                    g = j % PASSES
+                    bank = score_bank("difference")
+                    for t in range(PACK):
+                        nc.tensor.matmul(bank[:, t, :], lhsT=k_t[:, 0, g, t, :], rhs=q_t[:, 0, c, :], start=True, stop=False)
+                        nc.tensor.matmul(bank[:, t, :], lhsT=k_t[:, 1, g, t, :], rhs=q_t[:, 0, c, :], start=False, stop=True)
+                    nc.scalar.activation(out=series[0][:, j, :, :], in_=by_query(bank), func=ACT.Sigmoid, scale=SCALE)
+                    nc.scalar.activation(out=series[1][:, j, :, :], in_=by_query(bank), func=ACT.Sigmoid, scale=-SCALE)
+                return series
+
+            for x in (1, 2, 3):
+                transpose_queries(x)
+            transpose_keys(0)
+            transpose_keys(1)
+            quantise_values([0, 1])
+            series_of = {0: head_one_series(0)}
+            for block in range(BLOCKS):
+                if block + 1 < BLOCKS:
+                    series_of[block + 1] = head_one_series(block + 1)
+                later = [pair for pair in (2 + 2 * block, 3 + 2 * block) if pair < PAIRS]
+                for pair in later:
+                    transpose_keys(pair)
+                quantise_values(later)
+                codes, scales = new_codes(1)
+                for y in range(2):
+                    quantise_series(series_of[block][y], codes, scales, y)
+                store_rows(1, block, multiply_by_values(1, codes, scales), nc.vector.tensor_copy)
+
+        with tc.tile_pool(name="work", bufs=2) as work:
+            blocks = [(x, block) for x in (2, 3) for block in range(BLOCKS)]
+            n_steps = len(blocks) * STEPS
+            banks = {}
+            rounded = {}
+            top = {}
+            expo = {}
+            den = {}
+            series = {}
+            packed = {}
+
+            def heads(step):
+                return blocks[step // STEPS][0] + 1
+
+            def make_scores(step):
+                x, block = blocks[step // STEPS]
+                j = step % STEPS
+                c = block * BLOCK_CHUNKS + j // PASSES
+                g = j % PASSES
+                banks[step] = []
+                rounded[step] = work.tile([P, x + 1, P, PACK], BF16, tag="rounded", bufs=3, name="rounded")
+                for y in range(x + 1):
+                    bank = score_bank("scores")
+                    for t in range(PACK):
+                        nc.tensor.matmul(
+                            bank[:, t, :], lhsT=k_t[:, first_pair(x) + y, g, t, :], rhs=q_t[:, x - 1, c, :], start=True, stop=True
+                        )
+                    nc.scalar.copy(out=rounded[step][:, y, :, :], in_=by_query(bank))
+                    banks[step].append(bank)
+
+            def max_link(step, y):
+                if y == 1:
+                    top[step] = work.tile([P, P, PACK], BF16, tag="top", name="top")
+                nc.vector.tensor_tensor(
+                    out=top[step][:],
+                    in0=(rounded[step][:, 0, :, :] if y == 1 else top[step][:]),
+                    in1=rounded[step][:, y, :, :],
+                    op=ALU.max,
+                )
+
+            def add_link(step, y):
+                kb = step // STEPS
+                j = step % STEPS
+                if y == 1 and j == 0:
+                    den[kb] = work.tile([P, STEPS, P, PACK], F32, tag="den", bufs=3, name="den")
+                nc.vector.tensor_tensor(
+                    out=den[kb][:, j, :, :],
+                    in0=(expo[kb, 0][:, j, :, :] if y == 1 else den[kb][:, j, :, :]),
+                    in1=expo[kb, y][:, j, :, :],
+                    op=ALU.add,
+                )
+
+            def shifted_exponentials(step):
+                kb = step // STEPS
+                j = step % STEPS
+                for y in range(heads(step)):
+                    if j == 0:
+                        expo[kb, y] = work.tile([P, STEPS, P, PACK], F32, tag="expo", bufs=10, name="expo")
+                    nc.vector.tensor_tensor(
+                        out=expo[kb, y][:, j, :, :], in0=by_query(banks[step][y]), in1=top[step][:], op=ALU.subtract
+                    )
+                for y in range(heads(step)):
+                    nc.scalar.activation(out=expo[kb, y][:, j, :, :], in_=expo[kb, y][:, j, :, :], func=ACT.Exp, scale=SCALE)
+
+            make_scores(0)
+            last_slot = (len(blocks) - 1) * STEPS + QUANTISE_AT + blocks[-1][0] + 1
+            for slot in range(last_slot + 1):
+                ages = [(kb, x, block, slot - kb * STEPS) for kb, (x, block) in enumerate(blocks)]
+                if slot + 1 < n_steps:
+                    make_scores(slot + 1)
+                sums = {}
+                for kb, x, block, age in ages:
+                    if age == QUANTISE_AT + x + 1:
+                        sums[kb] = multiply_by_values(x, packed[kb][0], packed[kb][1])
+                for y in range(1, 4):
+                    if slot < n_steps and y < heads(slot):
+                        max_link(slot, y)
+                    if 0 <= slot - 1 < n_steps and y < heads(slot - 1):
+                        add_link(slot - 1, y)
+                if slot < n_steps:
+                    shifted_exponentials(slot)
+                for kb, x, block, age in ages:
+                    if age == LN_AT:
+                        nc.scalar.activation(out=den[kb][:], in_=den[kb][:], func=ACT.Ln)
+                    if age == RECIPROCAL_AT:
+                        nc.scalar.activation(out=den[kb][:], in_=den[kb][:], func=ACT.Exp, scale=-1.0)
+                for kb, x, block, age in ages:
+                    y = age - QUANTISE_AT
+                    if 0 <= y <= x:
+                        if y == 0:
+                            packed[kb] = new_codes(x)
+                        quantise_series(series[kb, y], packed[kb][0], packed[kb][1], y)
+                for kb, x, block, age in ages:
+                    y = age - MULTIPLY_AT
+                    if 0 <= y <= x:
+                        series[kb, y] = work.tile([P, STEPS, P, PACK], BF16, tag="series", name="series", align_bytes=64)
+                        nc.vector.tensor_tensor(out=series[kb, y][:], in0=expo[kb, y][:], in1=den[kb][:], op=ALU.mult)
+                for kb, x, block, age in ages:
+                    if kb in sums:
+                        store_rows(x, block, sums[kb], nc.scalar.copy)

@@ -23,13 +23,16 @@ NEGATED_PAIR = 1
 
 BLOCK_CHUNKS = 2
 STEPS = BLOCK_CHUNKS * PASSES
-BLOCKS = CHUNKS // BLOCK_CHUNKS
+HEAD_STEPS = CHUNKS * PASSES
 SCORE_BANKS = 7
 
-LN_AT = STEPS
+AHEAD = 3
+ADD_LAG = 1
+LN_AT = STEPS - 1 + ADD_LAG
 RECIPROCAL_AT = LN_AT + 1
-MULTIPLY_AT = RECIPROCAL_AT + 1
-QUANTISE_AT = MULTIPLY_AT + 1
+MULTIPLY_LAG = RECIPROCAL_AT + 1
+QUANTISE_LAG = MULTIPLY_LAG + 1
+PRODUCT_AT = STEPS - 1 + QUANTISE_LAG + 1
 
 FLOPS = 2 * 2 * PAIRS * L * L * E
 
@@ -44,14 +47,32 @@ def tile_anomalyattention_pa_kernel(tc, q_plus, key_plus, retrieval, out):
     out_view = out[0].rearrange("(p c) x e -> p c x e", c=CHUNKS)
 
     with tc.manual_schedule(), tc.tile_pool(name="keep", bufs=1) as keep, tc.tile_pool(
-        name="mx", bufs=2
-    ) as mx, tc.psum_pool(name="psum", bufs=1) as psum:
-        ident = keep.tile([P, P], BF16)
+        name="work", bufs=2
+    ) as work, tc.psum_pool(name="psum", bufs=1) as psum:
+        ident = keep.tile([P, P], BF16, name="ident")
         masks.make_identity(nc, ident[:])
-        q_t = keep.tile([P, 3, CHUNKS, P], BF16)
-        k_t = keep.tile([P, PAIRS, PASSES, PACK, P], BF16)
-        r_codes = keep.tile([P, PAIRS, PASSES, E], U32, align_bytes=64)
-        r_scales = keep.tile([P, PAIRS, PASSES, E], U8, align_bytes=64)
+        q_raw = keep.tile([P, CHUNKS, 3, E], BF16, name="q_raw")
+        k_raw = [keep.tile([P, PASSES, PACK, E], BF16, name="k_raw%d" % pair) for pair in range(PAIRS)]
+        r_raw = [keep.tile([P, PASSES, PACK, E], BF16, name="r_raw%d" % pair) for pair in range(PAIRS)]
+        q_t = keep.tile([P, 3, CHUNKS, P], BF16, name="q_t")
+        k_t = keep.tile([P, PAIRS, PASSES, PACK, P], BF16, name="k_t")
+        r_codes = keep.tile([P, PAIRS, PASSES, E], U32, name="r_codes", align_bytes=64)
+        r_scales = keep.tile([P, PAIRS, PASSES, E], U8, name="r_scales", align_bytes=64)
+
+        def load_keys(pair):
+            nc.sync.dma_start(out=k_raw[pair][:], in_=key_plus[0, pair].rearrange("(g p t) e -> p g t e", g=PASSES, t=PACK))
+
+        def load_values(pair):
+            nc.sync.dma_start(out=r_raw[pair][:], in_=retrieval[0, pair].rearrange("(g p t) e -> p g t e", g=PASSES, t=PACK))
+
+        nc.sync.dma_start(out=q_raw[:], in_=q_view)
+        load_keys(0)
+        load_keys(1)
+        load_values(0)
+        load_values(1)
+        for pair in range(2, PAIRS):
+            load_keys(pair)
+            load_values(pair)
 
         def score_bank(name):
             return psum.tile([P, PACK, P], F32, tag="bank", bufs=SCORE_BANKS, name=name)
@@ -59,17 +80,68 @@ def tile_anomalyattention_pa_kernel(tc, q_plus, key_plus, retrieval, out):
         def by_query(bank):
             return bank[:].rearrange("p t l -> p l t")
 
-        def new_codes(x):
-            codes = mx.tile([P, x + 1, STEPS, P], U32, tag="codes", name="codes", align_bytes=64)
-            scales = mx.tile([P, x + 1, STEPS, P], U8, tag="scales", name="scales", align_bytes=64)
+        def transposed(sources):
+            flipped = psum.tile([P, PACK, P], BF16, tag="bank", bufs=SCORE_BANKS, name="flipped")
+            for i, source in enumerate(sources):
+                nc.tensor.transpose(flipped[:, i, :], source, ident[:])
+            return flipped
+
+        def transpose_queries(x, half, copy_out=nc.vector.tensor_copy):
+            chunks = range(half * PACK, (half + 1) * PACK)
+            flipped = transposed([q_raw[:, c, x - 1, :] for c in chunks])
+            copy_out(out=q_t[:, x - 1, half * PACK : (half + 1) * PACK, :], in_=flipped[:])
+
+        def transpose_keys(pair, g):
+            flipped = transposed([k_raw[pair][:, g, t, :] for t in range(PACK)])
+            if pair == NEGATED_PAIR:
+                nc.vector.tensor_scalar_mul(out=k_t[:, pair, g, :, :], in0=flipped[:], scalar1=-1.0)
+            else:
+                nc.vector.tensor_copy(out=k_t[:, pair, g, :, :], in_=flipped[:])
+
+        grouped = {}
+
+        def group_values(pair):
+            grouped[pair] = work.tile([P, PASSES, E, PACK], BF16, tag="grouped", name="grouped", align_bytes=64)
+            nc.vector.tensor_copy(out=grouped[pair][:], in_=r_raw[pair][:].rearrange("p g t e -> p g e t"))
+
+        def quantise_values(pair):
+            nc.vector.quantize_mx(
+                out=r_codes[:, pair, :, :].rearrange("p g e -> p (g e)").bitcast(FP8X4),
+                scales=r_scales[:, pair, :, :].rearrange("p g e -> p (g e)"),
+                in_=grouped[pair][:].rearrange("p g e t -> p (g e t)"),
+            )
+
+        def prepare_pair(pair, g):
+            transpose_keys(pair, g)
+            if g == 0:
+                group_values(pair)
+            else:
+                quantise_values(pair)
+
+        def operands_of(x):
+            pairs = range(first_pair(x), first_pair(x) + x + 1)
+            return [(transpose_queries, x, half) for half in range(CHUNKS // PACK)] + [
+                (prepare_pair, pair, g) for pair in pairs for g in range(PASSES)
+            ]
+
+        def new_series(n):
+            return work.tile([P, n, P, PACK], BF16, tag="series", bufs=4, name="series", align_bytes=64)
+
+        def new_codes(n):
+            codes = work.tile([P, STEPS, n, P], U32, tag="codes", name="codes", align_bytes=64)
+            scales = work.tile([P, STEPS, n, P], U8, tag="scales", name="scales", align_bytes=64)
             return codes, scales
 
-        def quantise_series(series, codes, scales, y):
-            nc.vector.quantize_mx(
-                out=codes[:, y, :, :].rearrange("p j l -> p (j l)").bitcast(FP8X4),
-                scales=scales[:, y, :, :].rearrange("p j l -> p (j l)"),
-                in_=series[:].rearrange("p j l t -> p (j l t)"),
-            )
+        def quantise_series(series, n, codes, scales, j):
+            y = 0
+            for run in (4, 2, 1):
+                if n - y >= run:
+                    nc.vector.quantize_mx(
+                        out=codes[:, j, y : y + run, :].rearrange("p y l -> p (y l)").bitcast(FP8X4),
+                        scales=scales[:, j, y : y + run, :].rearrange("p y l -> p (y l)"),
+                        in_=series[:, y : y + run, :, :].rearrange("p y l t -> p (y l t)"),
+                    )
+                    y += run
 
         def multiply_by_values(x, codes, scales):
             acc = psum.tile([P, BLOCK_CHUNKS, E], F32, tag="acc", name="acc")
@@ -78,8 +150,8 @@ def tile_anomalyattention_pa_kernel(tc, q_plus, key_plus, retrieval, out):
                 for g, y in terms:
                     nc.tensor.matmul_mx(
                         out=acc[:, c, :],
-                        lhsT=codes[:, y, c * PASSES + g, :].bitcast(FP8X4),
-                        lhsT_scale=scales[:, y, c * PASSES + g, :],
+                        lhsT=codes[:, c * PASSES + g, y, :].bitcast(FP8X4),
+                        lhsT_scale=scales[:, c * PASSES + g, y, :],
                         rhs=r_codes[:, first_pair(x) + y, g, :].bitcast(FP8X4),
                         rhs_scale=r_scales[:, first_pair(x) + y, g, :],
                         start=((g, y) == terms[0]),
@@ -88,188 +160,146 @@ def tile_anomalyattention_pa_kernel(tc, q_plus, key_plus, retrieval, out):
             return acc
 
         def store_rows(x, block, acc, copy_out):
-            result = mx.tile([P, BLOCK_CHUNKS, E], F32, name="result")
+            result = work.tile([P, BLOCK_CHUNKS, E], F32, name="result")
             copy_out(out=result[:], in_=acc[:])
             chunks = slice(block * BLOCK_CHUNKS, (block + 1) * BLOCK_CHUNKS)
             nc.sync.dma_start(out=out_view[:, chunks, x - 1, :], in_=result[:])
 
-        with tc.tile_pool(name="raw", bufs=1) as raw:
-            q_raw = raw.tile([P, CHUNKS, 3, E], BF16)
-            nc.sync.dma_start(out=q_raw[:], in_=q_view)
-            k_raw = []
-            r_raw = []
-            for pair in range(PAIRS):
-                k_raw.append(raw.tile([P, PASSES, PACK, E], BF16, name="k_raw%d" % pair))
-                r_raw.append(raw.tile([P, PASSES, PACK, E], BF16, name="r_raw%d" % pair))
-                nc.sync.dma_start(
-                    out=k_raw[pair][:], in_=key_plus[0, pair].rearrange("(g p t) e -> p g t e", g=PASSES, t=PACK)
-                )
-                nc.sync.dma_start(
-                    out=r_raw[pair][:], in_=retrieval[0, pair].rearrange("(g p t) e -> p g t e", g=PASSES, t=PACK)
-                )
+        difference = {}
+        series = {}
+        packed = {}
+        sums = {}
 
-            def transpose_queries(x):
-                for half in range(CHUNKS // PACK):
-                    flipped = psum.tile([P, PACK, P], BF16, tag="bank", bufs=SCORE_BANKS, name="flipped")
-                    for i in range(PACK):
-                        nc.tensor.transpose(flipped[:, i, :], q_raw[:, half * PACK + i, x - 1, :], ident[:])
-                    nc.scalar.copy(out=q_t[:, x - 1, half * PACK : (half + 1) * PACK, :], in_=flipped[:])
+        def head_one_scores(step):
+            c, g = divmod(step, PASSES)
+            difference[step] = score_bank("difference")
+            for t in range(PACK):
+                nc.tensor.matmul(difference[step][:, t, :], lhsT=k_t[:, 0, g, t, :], rhs=q_t[:, 0, c, :], start=True, stop=False)
+                nc.tensor.matmul(difference[step][:, t, :], lhsT=k_t[:, 1, g, t, :], rhs=q_t[:, 0, c, :], start=False, stop=True)
 
-            def transpose_keys(pair):
-                for g in range(PASSES):
-                    flipped = psum.tile([P, PACK, P], BF16, tag="bank", bufs=SCORE_BANKS, name="flipped")
-                    for t in range(PACK):
-                        nc.tensor.transpose(flipped[:, t, :], k_raw[pair][:, g, t, :], ident[:])
-                    if pair == NEGATED_PAIR:
-                        nc.vector.tensor_scalar_mul(out=k_t[:, pair, g, :, :], in0=flipped[:], scalar1=-1.0)
-                    else:
-                        nc.vector.tensor_copy(out=k_t[:, pair, g, :, :], in_=flipped[:])
+        def head_one_series(step):
+            series[step] = new_series(2)
+            nc.scalar.activation(out=series[step][:, 0, :, :], in_=by_query(difference[step]), func=ACT.Sigmoid, scale=SCALE)
+            nc.scalar.activation(out=series[step][:, 1, :, :], in_=by_query(difference[step]), func=ACT.Sigmoid, scale=-SCALE)
 
-            def quantise_values(pairs):
-                grouped = {}
-                for pair in pairs:
-                    grouped[pair] = raw.tile(
-                        [P, PASSES, E, PACK], BF16, tag="grouped", bufs=4, name="grouped", align_bytes=64
+        for half in range(CHUNKS // PACK):
+            transpose_queries(1, half, nc.scalar.copy)
+        for pair in (0, 1):
+            for g in range(PASSES):
+                transpose_keys(pair, g)
+        for pair in (0, 1):
+            group_values(pair)
+        for pair in (0, 1):
+            quantise_values(pair)
+        for step in range(AHEAD):
+            head_one_scores(step)
+        for step in range(HEAD_STEPS + 3):
+            block, j = divmod(step, STEPS)
+            if j == 1 and block >= 1:
+                sums[block - 1] = multiply_by_values(1, packed[block - 1][0], packed[block - 1][1])
+            if step + AHEAD < HEAD_STEPS:
+                head_one_scores(step + AHEAD)
+            if step < HEAD_STEPS:
+                head_one_series(step)
+            if step < len(operands_of(2)):
+                job, first, second = operands_of(2)[step]
+                job(first, second)
+            if 1 <= step <= HEAD_STEPS:
+                if (step - 1) % STEPS == 0:
+                    packed[(step - 1) // STEPS] = new_codes(2)
+                codes, scales = packed[(step - 1) // STEPS]
+                quantise_series(series[step - 1], 2, codes, scales, (step - 1) % STEPS)
+            if j == 2 and block >= 1:
+                store_rows(1, block - 1, sums[block - 1], nc.vector.tensor_copy)
+
+        steps = [(x, c, g) for x in (2, 3) for c in range(CHUNKS) for g in range(PASSES)]
+        n_steps = len(steps)
+        banks = {}
+        top = {}
+        expo = {}
+        den = {}
+        series = {}
+        packed = {}
+
+        def heads(step):
+            return steps[step][0] + 1
+
+        def make_scores(step):
+            x, c, g = steps[step]
+            banks[step] = [score_bank("scores") for y in range(x + 1)]
+            top[step] = work.tile([P, P, PACK], F32, tag="top", bufs=3, name="top")
+            for y in range(x + 1):
+                for t in range(PACK):
+                    nc.tensor.matmul(
+                        banks[step][y][:, t, :], lhsT=k_t[:, first_pair(x) + y, g, t, :], rhs=q_t[:, x - 1, c, :], start=True, stop=True
                     )
-                    nc.vector.tensor_copy(out=grouped[pair][:], in_=r_raw[pair][:].rearrange("p g t e -> p g e t"))
-                for pair in pairs:
-                    nc.vector.quantize_mx(
-                        out=r_codes[:, pair, :, :].rearrange("p g e -> p (g e)").bitcast(FP8X4),
-                        scales=r_scales[:, pair, :, :].rearrange("p g e -> p (g e)"),
-                        in_=grouped[pair][:].rearrange("p g e t -> p (g e t)"),
-                    )
+            nc.scalar.copy(out=top[step][:], in_=by_query(banks[step][0]))
 
-            def head_one_series(block):
-                series = [
-                    raw.tile([P, STEPS, P, PACK], BF16, tag="series1", bufs=4, name="series1", align_bytes=64)
-                    for y in range(2)
-                ]
-                for j in range(STEPS):
-                    c = block * BLOCK_CHUNKS + j // PASSES
-                    g = j % PASSES
-                    bank = score_bank("difference")
-                    for t in range(PACK):
-                        nc.tensor.matmul(bank[:, t, :], lhsT=k_t[:, 0, g, t, :], rhs=q_t[:, 0, c, :], start=True, stop=False)
-                        nc.tensor.matmul(bank[:, t, :], lhsT=k_t[:, 1, g, t, :], rhs=q_t[:, 0, c, :], start=False, stop=True)
-                    nc.scalar.activation(out=series[0][:, j, :, :], in_=by_query(bank), func=ACT.Sigmoid, scale=SCALE)
-                    nc.scalar.activation(out=series[1][:, j, :, :], in_=by_query(bank), func=ACT.Sigmoid, scale=-SCALE)
-                return series
+        def raise_top(step, y):
+            nc.vector.tensor_tensor(out=top[step][:], in0=by_query(banks[step][y]), in1=top[step][:], op=ALU.max)
 
-            for x in (1, 2, 3):
-                transpose_queries(x)
-            transpose_keys(0)
-            transpose_keys(1)
-            quantise_values([0, 1])
-            series_of = {0: head_one_series(0)}
-            for block in range(BLOCKS):
-                if block + 1 < BLOCKS:
-                    series_of[block + 1] = head_one_series(block + 1)
-                later = [pair for pair in (2 + 2 * block, 3 + 2 * block) if pair < PAIRS]
-                for pair in later:
-                    transpose_keys(pair)
-                quantise_values(later)
-                codes, scales = new_codes(1)
-                for y in range(2):
-                    quantise_series(series_of[block][y], codes, scales, y)
-                store_rows(1, block, multiply_by_values(1, codes, scales), nc.vector.tensor_copy)
+        def subtract_top(step, y):
+            if y == 0:
+                expo[step] = work.tile([P, heads(step), P, PACK], F32, tag="expo", bufs=MULTIPLY_LAG + 2, name="expo")
+            nc.vector.tensor_tensor(out=expo[step][:, y, :, :], in0=by_query(banks[step][y]), in1=top[step][:], op=ALU.subtract)
 
-        with tc.tile_pool(name="work", bufs=2) as work:
-            blocks = [(x, block) for x in (2, 3) for block in range(BLOCKS)]
-            n_steps = len(blocks) * STEPS
-            banks = {}
-            rounded = {}
-            top = {}
-            expo = {}
-            den = {}
-            series = {}
-            packed = {}
+        def add_up(step):
+            block, j = divmod(step, STEPS)
+            if j == 0:
+                den[block] = work.tile([P, STEPS, P, PACK], F32, tag="den", bufs=3, name="den")
+            nc.gpsimd.tensor_tensor(out=den[block][:, j, :, :], in0=expo[step][:, 0, :, :], in1=expo[step][:, 1, :, :], op=ALU.add)
+            for y in range(2, heads(step)):
+                nc.gpsimd.tensor_tensor(out=den[block][:, j, :, :], in0=den[block][:, j, :, :], in1=expo[step][:, y, :, :], op=ALU.add)
 
-            def heads(step):
-                return blocks[step // STEPS][0] + 1
+        def multiply(step):
+            block, j = divmod(step, STEPS)
+            n = heads(step)
+            series[step] = new_series(n)
+            nc.vector.tensor_tensor(
+                out=series[step][:],
+                in0=expo[step][:],
+                in1=den[block][:, j, :, :].unsqueeze(1).to_broadcast([P, n, P, PACK]),
+                op=ALU.mult,
+            )
 
-            def make_scores(step):
-                x, block = blocks[step // STEPS]
-                j = step % STEPS
-                c = block * BLOCK_CHUNKS + j // PASSES
-                g = j % PASSES
-                banks[step] = []
-                rounded[step] = work.tile([P, x + 1, P, PACK], BF16, tag="rounded", bufs=3, name="rounded")
-                for y in range(x + 1):
-                    bank = score_bank("scores")
-                    for t in range(PACK):
-                        nc.tensor.matmul(
-                            bank[:, t, :], lhsT=k_t[:, first_pair(x) + y, g, t, :], rhs=q_t[:, x - 1, c, :], start=True, stop=True
-                        )
-                    nc.scalar.copy(out=rounded[step][:, y, :, :], in_=by_query(bank))
-                    banks[step].append(bank)
-
-            def max_link(step, y):
-                if y == 1:
-                    top[step] = work.tile([P, P, PACK], BF16, tag="top", name="top")
-                nc.vector.tensor_tensor(
-                    out=top[step][:],
-                    in0=(rounded[step][:, 0, :, :] if y == 1 else top[step][:]),
-                    in1=rounded[step][:, y, :, :],
-                    op=ALU.max,
-                )
-
-            def add_link(step, y):
-                kb = step // STEPS
-                j = step % STEPS
-                if y == 1 and j == 0:
-                    den[kb] = work.tile([P, STEPS, P, PACK], F32, tag="den", bufs=3, name="den")
-                nc.vector.tensor_tensor(
-                    out=den[kb][:, j, :, :],
-                    in0=(expo[kb, 0][:, j, :, :] if y == 1 else den[kb][:, j, :, :]),
-                    in1=expo[kb, y][:, j, :, :],
-                    op=ALU.add,
-                )
-
-            def shifted_exponentials(step):
-                kb = step // STEPS
-                j = step % STEPS
-                for y in range(heads(step)):
-                    if j == 0:
-                        expo[kb, y] = work.tile([P, STEPS, P, PACK], F32, tag="expo", bufs=10, name="expo")
-                    nc.vector.tensor_tensor(
-                        out=expo[kb, y][:, j, :, :], in0=by_query(banks[step][y]), in1=top[step][:], op=ALU.subtract
-                    )
-                for y in range(heads(step)):
-                    nc.scalar.activation(out=expo[kb, y][:, j, :, :], in_=expo[kb, y][:, j, :, :], func=ACT.Exp, scale=SCALE)
-
-            make_scores(0)
-            last_slot = (len(blocks) - 1) * STEPS + QUANTISE_AT + blocks[-1][0] + 1
-            for slot in range(last_slot + 1):
-                ages = [(kb, x, block, slot - kb * STEPS) for kb, (x, block) in enumerate(blocks)]
-                if slot + 1 < n_steps:
-                    make_scores(slot + 1)
-                sums = {}
-                for kb, x, block, age in ages:
-                    if age == QUANTISE_AT + x + 1:
-                        sums[kb] = multiply_by_values(x, packed[kb][0], packed[kb][1])
-                for y in range(1, 4):
-                    if slot < n_steps and y < heads(slot):
-                        max_link(slot, y)
-                    if 0 <= slot - 1 < n_steps and y < heads(slot - 1):
-                        add_link(slot - 1, y)
-                if slot < n_steps:
-                    shifted_exponentials(slot)
-                for kb, x, block, age in ages:
-                    if age == LN_AT:
-                        nc.scalar.activation(out=den[kb][:], in_=den[kb][:], func=ACT.Ln)
-                    if age == RECIPROCAL_AT:
-                        nc.scalar.activation(out=den[kb][:], in_=den[kb][:], func=ACT.Exp, scale=-1.0)
-                for kb, x, block, age in ages:
-                    y = age - QUANTISE_AT
-                    if 0 <= y <= x:
-                        if y == 0:
-                            packed[kb] = new_codes(x)
-                        quantise_series(series[kb, y], packed[kb][0], packed[kb][1], y)
-                for kb, x, block, age in ages:
-                    y = age - MULTIPLY_AT
-                    if 0 <= y <= x:
-                        series[kb, y] = work.tile([P, STEPS, P, PACK], BF16, tag="series", name="series", align_bytes=64)
-                        nc.vector.tensor_tensor(out=series[kb, y][:], in0=expo[kb, y][:], in1=den[kb][:], op=ALU.mult)
-                for kb, x, block, age in ages:
-                    if kb in sums:
-                        store_rows(x, block, sums[kb], nc.scalar.copy)
+        make_scores(0)
+        make_scores(1)
+        for y in range(1, heads(0)):
+            raise_top(0, y)
+        for slot in range(n_steps - STEPS + PRODUCT_AT + 1):
+            block, age = divmod(slot - PRODUCT_AT, STEPS)
+            product_due = age == 0 and block >= 0
+            if product_due:
+                x = steps[block * STEPS][0]
+                sums[block] = multiply_by_values(x, packed[block][0], packed[block][1])
+            if slot + 2 < n_steps:
+                make_scores(slot + 2)
+            if 0 <= slot - ADD_LAG < n_steps:
+                add_up(slot - ADD_LAG)
+            for y in range(PACK):
+                if slot + 1 < n_steps and y + 1 < heads(slot + 1):
+                    raise_top(slot + 1, y + 1)
+                if slot < n_steps and y < heads(slot):
+                    subtract_top(slot, y)
+            if slot < n_steps:
+                nc.scalar.activation(out=expo[slot][:], in_=expo[slot][:], func=ACT.Exp, scale=SCALE)
+            block, age = divmod(slot - LN_AT, STEPS)
+            if age == 0 and 0 <= block < n_steps // STEPS:
+                nc.scalar.activation(out=den[block][:], in_=den[block][:], func=ACT.Ln)
+            block, age = divmod(slot - RECIPROCAL_AT, STEPS)
+            if age == 0 and 0 <= block < n_steps // STEPS:
+                nc.scalar.activation(out=den[block][:], in_=den[block][:], func=ACT.Exp, scale=-1.0)
+            if slot < len(operands_of(3)):
+                job, first, second = operands_of(3)[slot]
+                job(first, second)
+            if 0 <= slot - QUANTISE_LAG < n_steps:
+                block, j = divmod(slot - QUANTISE_LAG, STEPS)
+                if j == 0:
+                    packed[block] = new_codes(heads(slot - QUANTISE_LAG))
+                quantise_series(series[slot - QUANTISE_LAG], heads(slot - QUANTISE_LAG), packed[block][0], packed[block][1], j)
+            if 0 <= slot - MULTIPLY_LAG < n_steps:
+                multiply(slot - MULTIPLY_LAG)
+            if product_due:
+                block = (slot - PRODUCT_AT) // STEPS
+                x, c, g = steps[block * STEPS]
+                store_rows(x, c // BLOCK_CHUNKS, sums[block], nc.scalar.copy)

@@ -30,7 +30,8 @@ AHEAD = 3
 ADD_LAG = 1
 LN_AT = STEPS - 1 + ADD_LAG
 RECIPROCAL_AT = LN_AT + 1
-MULTIPLY_LAG = RECIPROCAL_AT + 1
+SPARE = 2
+MULTIPLY_LAG = RECIPROCAL_AT + 1 + SPARE
 QUANTISE_LAG = MULTIPLY_LAG + 1
 PRODUCT_AT = STEPS - 1 + QUANTISE_LAG + 1
 
@@ -52,8 +53,8 @@ def tile_anomalyattention_pa_kernel(tc, q_plus, key_plus, retrieval, out):
         ident = keep.tile([P, P], BF16, name="ident")
         masks.make_identity(nc, ident[:])
         q_raw = keep.tile([P, CHUNKS, 3, E], BF16, name="q_raw")
-        k_raw = [keep.tile([P, PASSES, PACK, E], BF16, name="k_raw%d" % pair) for pair in range(PAIRS)]
-        r_raw = [keep.tile([P, PASSES, PACK, E], BF16, name="r_raw%d" % pair) for pair in range(PAIRS)]
+        k_raw = [keep.tile([P, PASSES, PACK, E], BF16, tag="k_raw", bufs=5, name="k_raw") for pair in range(PAIRS)]
+        r_raw = [keep.tile([P, PASSES, PACK, E], BF16, tag="r_raw", bufs=5, name="r_raw") for pair in range(PAIRS)]
         q_t = keep.tile([P, 3, CHUNKS, P], BF16, name="q_t")
         k_t = keep.tile([P, PAIRS, PASSES, PACK, P], BF16, name="k_t")
         r_codes = keep.tile([P, PAIRS, PASSES, E], U32, name="r_codes", align_bytes=64)
@@ -86,13 +87,16 @@ def tile_anomalyattention_pa_kernel(tc, q_plus, key_plus, retrieval, out):
                 nc.tensor.transpose(flipped[:, i, :], source, ident[:])
             return flipped
 
-        def transpose_queries(x, half, copy_out=nc.vector.tensor_copy):
-            chunks = range(half * PACK, (half + 1) * PACK)
-            flipped = transposed([q_raw[:, c, x - 1, :] for c in chunks])
+        def flip_queries(x, half):
+            return transposed([q_raw[:, c, x - 1, :] for c in range(half * PACK, (half + 1) * PACK)])
+
+        def keep_queries(x, half, flipped, copy_out=nc.vector.tensor_copy):
             copy_out(out=q_t[:, x - 1, half * PACK : (half + 1) * PACK, :], in_=flipped[:])
 
-        def transpose_keys(pair, g):
-            flipped = transposed([k_raw[pair][:, g, t, :] for t in range(PACK)])
+        def flip_keys(pair, g):
+            return transposed([k_raw[pair][:, g, t, :] for t in range(PACK)])
+
+        def keep_keys(pair, g, flipped):
             if pair == NEGATED_PAIR:
                 nc.vector.tensor_scalar_mul(out=k_t[:, pair, g, :, :], in0=flipped[:], scalar1=-1.0)
             else:
@@ -111,8 +115,8 @@ def tile_anomalyattention_pa_kernel(tc, q_plus, key_plus, retrieval, out):
                 in_=grouped[pair][:].rearrange("p g e t -> p (g e t)"),
             )
 
-        def prepare_pair(pair, g):
-            transpose_keys(pair, g)
+        def keep_pair(pair, g, flipped):
+            keep_keys(pair, g, flipped)
             if g == 0:
                 group_values(pair)
             else:
@@ -120,9 +124,19 @@ def tile_anomalyattention_pa_kernel(tc, q_plus, key_plus, retrieval, out):
 
         def operands_of(x):
             pairs = range(first_pair(x), first_pair(x) + x + 1)
-            return [(transpose_queries, x, half) for half in range(CHUNKS // PACK)] + [
-                (prepare_pair, pair, g) for pair in pairs for g in range(PASSES)
+            return [(flip_queries, keep_queries, x, half) for half in range(CHUNKS // PACK)] + [
+                (flip_keys, keep_pair, pair, g) for pair in pairs for g in range(PASSES)
             ]
+
+        flipped_for = {}
+
+        def one_job(jobs, turn):
+            if 1 <= turn <= len(jobs):
+                flip, finish, first, second = jobs[turn - 1]
+                finish(first, second, flipped_for[turn - 1])
+            if turn < len(jobs):
+                flip, finish, first, second = jobs[turn]
+                flipped_for[turn] = flip(first, second)
 
         def new_series(n):
             return work.tile([P, n, P, PACK], BF16, tag="series", bufs=4, name="series", align_bytes=64)
@@ -183,10 +197,10 @@ def tile_anomalyattention_pa_kernel(tc, q_plus, key_plus, retrieval, out):
             nc.scalar.activation(out=series[step][:, 1, :, :], in_=by_query(difference[step]), func=ACT.Sigmoid, scale=-SCALE)
 
         for half in range(CHUNKS // PACK):
-            transpose_queries(1, half, nc.scalar.copy)
+            keep_queries(1, half, flip_queries(1, half), nc.scalar.copy)
         for pair in (0, 1):
             for g in range(PASSES):
-                transpose_keys(pair, g)
+                keep_keys(pair, g, flip_keys(pair, g))
         for pair in (0, 1):
             group_values(pair)
         for pair in (0, 1):
@@ -201,9 +215,7 @@ def tile_anomalyattention_pa_kernel(tc, q_plus, key_plus, retrieval, out):
                 head_one_scores(step + AHEAD)
             if step < HEAD_STEPS:
                 head_one_series(step)
-            if step < len(operands_of(2)):
-                job, first, second = operands_of(2)[step]
-                job(first, second)
+            one_job(operands_of(2), step)
             if 1 <= step <= HEAD_STEPS:
                 if (step - 1) % STEPS == 0:
                     packed[(step - 1) // STEPS] = new_codes(2)
@@ -247,9 +259,13 @@ def tile_anomalyattention_pa_kernel(tc, q_plus, key_plus, retrieval, out):
             block, j = divmod(step, STEPS)
             if j == 0:
                 den[block] = work.tile([P, STEPS, P, PACK], F32, tag="den", bufs=3, name="den")
-            nc.gpsimd.tensor_tensor(out=den[block][:, j, :, :], in0=expo[step][:, 0, :, :], in1=expo[step][:, 1, :, :], op=ALU.add)
-            for y in range(2, heads(step)):
-                nc.gpsimd.tensor_tensor(out=den[block][:, j, :, :], in0=den[block][:, j, :, :], in1=expo[step][:, y, :, :], op=ALU.add)
+            if heads(step) == 4:
+                half_sums = work.tile([P, 2, P, PACK], F32, name="half_sums")
+                nc.gpsimd.tensor_tensor(out=half_sums[:], in0=expo[step][:, 0:2, :, :], in1=expo[step][:, 2:4, :, :], op=ALU.add)
+                nc.gpsimd.tensor_tensor(out=den[block][:, j, :, :], in0=half_sums[:, 0, :, :], in1=half_sums[:, 1, :, :], op=ALU.add)
+            else:
+                nc.gpsimd.tensor_tensor(out=den[block][:, j, :, :], in0=expo[step][:, 0, :, :], in1=expo[step][:, 1, :, :], op=ALU.add)
+                nc.gpsimd.tensor_tensor(out=den[block][:, j, :, :], in0=den[block][:, j, :, :], in1=expo[step][:, 2, :, :], op=ALU.add)
 
         def multiply(step):
             block, j = divmod(step, STEPS)
@@ -267,6 +283,7 @@ def tile_anomalyattention_pa_kernel(tc, q_plus, key_plus, retrieval, out):
         for y in range(1, heads(0)):
             raise_top(0, y)
         for slot in range(n_steps - STEPS + PRODUCT_AT + 1):
+            one_job(operands_of(3), slot)
             block, age = divmod(slot - PRODUCT_AT, STEPS)
             product_due = age == 0 and block >= 0
             if product_due:
@@ -289,9 +306,6 @@ def tile_anomalyattention_pa_kernel(tc, q_plus, key_plus, retrieval, out):
             block, age = divmod(slot - RECIPROCAL_AT, STEPS)
             if age == 0 and 0 <= block < n_steps // STEPS:
                 nc.scalar.activation(out=den[block][:], in_=den[block][:], func=ACT.Exp, scale=-1.0)
-            if slot < len(operands_of(3)):
-                job, first, second = operands_of(3)[slot]
-                job(first, second)
             if 0 <= slot - QUANTISE_LAG < n_steps:
                 block, j = divmod(slot - QUANTISE_LAG, STEPS)
                 if j == 0:

@@ -256,16 +256,17 @@ def tile_anomalyattention_pa_kernel(tc, q_plus, key_plus, retrieval, out):
             nc.vector.tensor_tensor(out=expo[step][:, y, :, :], in0=by_query(banks[step][y]), in1=top[step][:], op=ALU.subtract)
 
         def add_up(step):
+            adder = nc.gpsimd if step + 1 < n_steps else nc.vector
             block, j = divmod(step, STEPS)
             if j == 0:
                 den[block] = work.tile([P, STEPS, P, PACK], F32, tag="den", bufs=3, name="den")
             if heads(step) == 4:
                 half_sums = work.tile([P, 2, P, PACK], F32, name="half_sums")
-                nc.gpsimd.tensor_tensor(out=half_sums[:], in0=expo[step][:, 0:2, :, :], in1=expo[step][:, 2:4, :, :], op=ALU.add)
-                nc.gpsimd.tensor_tensor(out=den[block][:, j, :, :], in0=half_sums[:, 0, :, :], in1=half_sums[:, 1, :, :], op=ALU.add)
+                adder.tensor_tensor(out=half_sums[:], in0=expo[step][:, 0:2, :, :], in1=expo[step][:, 2:4, :, :], op=ALU.add)
+                adder.tensor_tensor(out=den[block][:, j, :, :], in0=half_sums[:, 0, :, :], in1=half_sums[:, 1, :, :], op=ALU.add)
             else:
-                nc.gpsimd.tensor_tensor(out=den[block][:, j, :, :], in0=expo[step][:, 0, :, :], in1=expo[step][:, 1, :, :], op=ALU.add)
-                nc.gpsimd.tensor_tensor(out=den[block][:, j, :, :], in0=den[block][:, j, :, :], in1=expo[step][:, 2, :, :], op=ALU.add)
+                adder.tensor_tensor(out=den[block][:, j, :, :], in0=expo[step][:, 0, :, :], in1=expo[step][:, 1, :, :], op=ALU.add)
+                adder.tensor_tensor(out=den[block][:, j, :, :], in0=den[block][:, j, :, :], in1=expo[step][:, 2, :, :], op=ALU.add)
 
         def multiply(step):
             block, j = divmod(step, STEPS)

@@ -24,9 +24,9 @@ NEGATED_PAIR = 1
 BLOCK_CHUNKS = 2
 STEPS = BLOCK_CHUNKS * PASSES
 HEAD_STEPS = CHUNKS * PASSES
-SCORE_BANKS = 7
+BANKS = 8
+RAW_ROOMS = 5
 
-AHEAD = 3
 ADD_LAG = 1
 LN_AT = STEPS - 1 + ADD_LAG
 RECIPROCAL_AT = LN_AT + 1
@@ -34,12 +34,22 @@ SPARE = 2
 MULTIPLY_LAG = RECIPROCAL_AT + 1 + SPARE
 QUANTISE_LAG = MULTIPLY_LAG + 1
 PRODUCT_AT = STEPS - 1 + QUANTISE_LAG + 1
+LAST_BLOCK = 2 * HEAD_STEPS - STEPS
+DRAIN_AT = LAST_BLOCK + RECIPROCAL_AT + 1
+
+AHEAD = 5
+BEHIND = 3
+TURNS_A_SLOT = 3
 
 FLOPS = 2 * 2 * PAIRS * L * L * E
 
 
 def first_pair(x):
     return x * (x + 1) // 2 - 1
+
+
+def pairs_of(x):
+    return range(first_pair(x), first_pair(x) + x + 1)
 
 
 def tile_anomalyattention_pa_kernel(tc, q_plus, key_plus, retrieval, out):
@@ -49,40 +59,30 @@ def tile_anomalyattention_pa_kernel(tc, q_plus, key_plus, retrieval, out):
 
     with tc.manual_schedule(), tc.tile_pool(name="keep", bufs=1) as keep, tc.tile_pool(
         name="work", bufs=2
-    ) as work, tc.psum_pool(name="psum", bufs=1) as psum:
+    ) as work, tc.psum_pool(name="psum", bufs=BANKS) as psum:
         ident = keep.tile([P, P], BF16, name="ident")
         masks.make_identity(nc, ident[:])
-        q_raw = keep.tile([P, CHUNKS, 3, E], BF16, name="q_raw")
-        k_raw = [keep.tile([P, PASSES, PACK, E], BF16, tag="k_raw", bufs=5, name="k_raw") for pair in range(PAIRS)]
-        r_raw = [keep.tile([P, PASSES, PACK, E], BF16, tag="r_raw", bufs=5, name="r_raw") for pair in range(PAIRS)]
         q_t = keep.tile([P, 3, CHUNKS, P], BF16, name="q_t")
         k_t = keep.tile([P, PAIRS, PASSES, PACK, P], BF16, name="k_t")
         r_codes = keep.tile([P, PAIRS, PASSES, E], U32, name="r_codes", align_bytes=64)
         r_scales = keep.tile([P, PAIRS, PASSES, E], U8, name="r_scales", align_bytes=64)
 
-        def load_keys(pair):
-            nc.sync.dma_start(out=k_raw[pair][:], in_=key_plus[0, pair].rearrange("(g p t) e -> p g t e", g=PASSES, t=PACK))
-
-        def load_values(pair):
-            nc.sync.dma_start(out=r_raw[pair][:], in_=retrieval[0, pair].rearrange("(g p t) e -> p g t e", g=PASSES, t=PACK))
-
+        q_raw = keep.tile([P, CHUNKS, 3, E], BF16, name="q_raw")
         nc.sync.dma_start(out=q_raw[:], in_=q_view)
-        load_keys(0)
-        load_keys(1)
-        load_values(0)
-        load_values(1)
-        for pair in range(2, PAIRS):
-            load_keys(pair)
-            load_values(pair)
+        k_raw = {}
+        r_raw = {}
+        for x in (2, 3, 1):
+            for pair in pairs_of(x):
+                k_raw[pair] = keep.tile([P, PASSES, PACK, E], BF16, tag="k_raw", bufs=RAW_ROOMS, name="k_raw")
+                r_raw[pair] = keep.tile([P, PASSES, PACK, E], BF16, tag="r_raw", bufs=RAW_ROOMS, name="r_raw")
+                nc.sync.dma_start(out=k_raw[pair][:], in_=key_plus[0, pair].rearrange("(g p t) e -> p g t e", g=PASSES, t=PACK))
+                nc.sync.dma_start(out=r_raw[pair][:], in_=retrieval[0, pair].rearrange("(g p t) e -> p g t e", g=PASSES, t=PACK))
 
-        def score_bank(name):
-            return psum.tile([P, PACK, P], F32, tag="bank", bufs=SCORE_BANKS, name=name)
-
-        def by_query(bank):
-            return bank[:].rearrange("p t l -> p l t")
+        def bank(shape, dtype, name):
+            return psum.tile(shape, dtype, tag="bank", name=name)
 
         def transposed(sources):
-            flipped = psum.tile([P, PACK, P], BF16, tag="bank", bufs=SCORE_BANKS, name="flipped")
+            flipped = bank([P, PACK, P], BF16, "flipped")
             for i, source in enumerate(sources):
                 nc.tensor.transpose(flipped[:, i, :], source, ident[:])
             return flipped
@@ -90,42 +90,32 @@ def tile_anomalyattention_pa_kernel(tc, q_plus, key_plus, retrieval, out):
         def flip_queries(x, half):
             return transposed([q_raw[:, c, x - 1, :] for c in range(half * PACK, (half + 1) * PACK)])
 
-        def keep_queries(x, half, flipped, copy_out=nc.vector.tensor_copy):
-            copy_out(out=q_t[:, x - 1, half * PACK : (half + 1) * PACK, :], in_=flipped[:])
+        def keep_queries(x, half, flipped):
+            nc.vector.tensor_copy(out=q_t[:, x - 1, half * PACK : (half + 1) * PACK, :], in_=flipped[:])
 
         def flip_keys(pair, g):
             return transposed([k_raw[pair][:, g, t, :] for t in range(PACK)])
 
-        def keep_keys(pair, g, flipped):
+        grouped = {}
+
+        def keep_pair(pair, g, flipped):
             if pair == NEGATED_PAIR:
                 nc.vector.tensor_scalar_mul(out=k_t[:, pair, g, :, :], in0=flipped[:], scalar1=-1.0)
             else:
                 nc.vector.tensor_copy(out=k_t[:, pair, g, :, :], in_=flipped[:])
-
-        grouped = {}
-
-        def group_values(pair):
-            grouped[pair] = work.tile([P, PASSES, E, PACK], BF16, tag="grouped", name="grouped", align_bytes=64)
-            nc.vector.tensor_copy(out=grouped[pair][:], in_=r_raw[pair][:].rearrange("p g t e -> p g e t"))
-
-        def quantise_values(pair):
-            nc.vector.quantize_mx(
-                out=r_codes[:, pair, :, :].rearrange("p g e -> p (g e)").bitcast(FP8X4),
-                scales=r_scales[:, pair, :, :].rearrange("p g e -> p (g e)"),
-                in_=grouped[pair][:].rearrange("p g e t -> p (g e t)"),
-            )
-
-        def keep_pair(pair, g, flipped):
-            keep_keys(pair, g, flipped)
             if g == 0:
-                group_values(pair)
+                grouped[pair] = work.tile([P, PASSES, E, PACK], BF16, tag="grouped", name="grouped", align_bytes=64)
+                nc.vector.tensor_copy(out=grouped[pair][:], in_=r_raw[pair][:].rearrange("p g t e -> p g e t"))
             else:
-                quantise_values(pair)
+                nc.vector.quantize_mx(
+                    out=r_codes[:, pair, :, :].rearrange("p g e -> p (g e)").bitcast(FP8X4),
+                    scales=r_scales[:, pair, :, :].rearrange("p g e -> p (g e)"),
+                    in_=grouped[pair][:].rearrange("p g e t -> p (g e t)"),
+                )
 
         def operands_of(x):
-            pairs = range(first_pair(x), first_pair(x) + x + 1)
             return [(flip_queries, keep_queries, x, half) for half in range(CHUNKS // PACK)] + [
-                (flip_keys, keep_pair, pair, g) for pair in pairs for g in range(PASSES)
+                (flip_keys, keep_pair, pair, g) for pair in pairs_of(x) for g in range(PASSES)
             ]
 
         flipped_for = {}
@@ -138,8 +128,8 @@ def tile_anomalyattention_pa_kernel(tc, q_plus, key_plus, retrieval, out):
                 flip, finish, first, second = jobs[turn]
                 flipped_for[turn] = flip(first, second)
 
-        def new_series(n):
-            return work.tile([P, n, P, PACK], BF16, tag="series", bufs=4, name="series", align_bytes=64)
+        def by_query(scores):
+            return scores[:].rearrange("p t l -> p l t")
 
         def new_codes(n):
             codes = work.tile([P, STEPS, n, P], U32, tag="codes", name="codes", align_bytes=64)
@@ -158,7 +148,7 @@ def tile_anomalyattention_pa_kernel(tc, q_plus, key_plus, retrieval, out):
                     y += run
 
         def multiply_by_values(x, codes, scales):
-            acc = psum.tile([P, BLOCK_CHUNKS, E], F32, tag="acc", name="acc")
+            acc = bank([P, BLOCK_CHUNKS, E], F32, "acc")
             terms = [(g, y) for g in range(PASSES) for y in range(x + 1)]
             for c in range(BLOCK_CHUNKS):
                 for g, y in terms:
@@ -180,49 +170,38 @@ def tile_anomalyattention_pa_kernel(tc, q_plus, key_plus, retrieval, out):
             nc.sync.dma_start(out=out_view[:, chunks, x - 1, :], in_=result[:])
 
         difference = {}
-        series = {}
-        packed = {}
-        sums = {}
+        series_one = {}
+        packed_one = {}
+        sums_one = {}
 
         def head_one_scores(step):
             c, g = divmod(step, PASSES)
-            difference[step] = score_bank("difference")
+            difference[step] = bank([P, PACK, P], F32, "difference")
             for t in range(PACK):
                 nc.tensor.matmul(difference[step][:, t, :], lhsT=k_t[:, 0, g, t, :], rhs=q_t[:, 0, c, :], start=True, stop=False)
                 nc.tensor.matmul(difference[step][:, t, :], lhsT=k_t[:, 1, g, t, :], rhs=q_t[:, 0, c, :], start=False, stop=True)
 
         def head_one_series(step):
-            series[step] = new_series(2)
-            nc.scalar.activation(out=series[step][:, 0, :, :], in_=by_query(difference[step]), func=ACT.Sigmoid, scale=SCALE)
-            nc.scalar.activation(out=series[step][:, 1, :, :], in_=by_query(difference[step]), func=ACT.Sigmoid, scale=-SCALE)
+            series_one[step] = work.tile([P, 2, P, PACK], BF16, tag="series_one", bufs=3, name="series_one", align_bytes=64)
+            nc.scalar.activation(out=series_one[step][:, 0, :, :], in_=by_query(difference[step]), func=ACT.Sigmoid, scale=SCALE)
+            nc.scalar.activation(out=series_one[step][:, 1, :, :], in_=by_query(difference[step]), func=ACT.Sigmoid, scale=-SCALE)
 
-        for half in range(CHUNKS // PACK):
-            keep_queries(1, half, flip_queries(1, half), nc.scalar.copy)
-        for pair in (0, 1):
-            for g in range(PASSES):
-                keep_keys(pair, g, flip_keys(pair, g))
-        for pair in (0, 1):
-            group_values(pair)
-        for pair in (0, 1):
-            quantise_values(pair)
-        for step in range(AHEAD):
-            head_one_scores(step)
-        for step in range(HEAD_STEPS + 3):
-            block, j = divmod(step, STEPS)
-            if j == 1 and block >= 1:
-                sums[block - 1] = multiply_by_values(1, packed[block - 1][0], packed[block - 1][1])
-            if step + AHEAD < HEAD_STEPS:
-                head_one_scores(step + AHEAD)
-            if step < HEAD_STEPS:
-                head_one_series(step)
-            one_job(operands_of(2), step)
-            if 1 <= step <= HEAD_STEPS:
-                if (step - 1) % STEPS == 0:
-                    packed[(step - 1) // STEPS] = new_codes(2)
-                codes, scales = packed[(step - 1) // STEPS]
-                quantise_series(series[step - 1], 2, codes, scales, (step - 1) % STEPS)
-            if j == 2 and block >= 1:
-                store_rows(1, block - 1, sums[block - 1], nc.vector.tensor_copy)
+        def head_one_turn(turn):
+            if turn - 2 >= 0 and (turn - 2) % STEPS == STEPS - 1:
+                block = (turn - 2) // STEPS
+                sums_one[block] = multiply_by_values(1, packed_one[block][0], packed_one[block][1])
+            if turn + AHEAD < HEAD_STEPS:
+                head_one_scores(turn + AHEAD)
+            if 0 <= turn < HEAD_STEPS:
+                head_one_series(turn)
+            if 0 <= turn - 1 < HEAD_STEPS:
+                block, j = divmod(turn - 1, STEPS)
+                if j == 0:
+                    packed_one[block] = new_codes(2)
+                quantise_series(series_one[turn - 1], 2, packed_one[block][0], packed_one[block][1], j)
+            if turn - BEHIND >= 0 and (turn - BEHIND) % STEPS == STEPS - 1:
+                block = (turn - BEHIND) // STEPS
+                store_rows(1, block, sums_one[block], nc.vector.tensor_copy)
 
         steps = [(x, c, g) for x in (2, 3) for c in range(CHUNKS) for g in range(PASSES)]
         n_steps = len(steps)
@@ -232,13 +211,14 @@ def tile_anomalyattention_pa_kernel(tc, q_plus, key_plus, retrieval, out):
         den = {}
         series = {}
         packed = {}
+        sums = {}
 
         def heads(step):
             return steps[step][0] + 1
 
         def make_scores(step):
             x, c, g = steps[step]
-            banks[step] = [score_bank("scores") for y in range(x + 1)]
+            banks[step] = [bank([P, PACK, P], F32, "scores") for y in range(x + 1)]
             top[step] = work.tile([P, P, PACK], F32, tag="top", bufs=3, name="top")
             for y in range(x + 1):
                 for t in range(PACK):
@@ -271,7 +251,7 @@ def tile_anomalyattention_pa_kernel(tc, q_plus, key_plus, retrieval, out):
         def multiply(step):
             block, j = divmod(step, STEPS)
             n = heads(step)
-            series[step] = new_series(n)
+            series[step] = work.tile([P, n, P, PACK], BF16, tag="series", bufs=3, name="series", align_bytes=64)
             nc.vector.tensor_tensor(
                 out=series[step][:],
                 in0=expo[step][:],
@@ -279,14 +259,18 @@ def tile_anomalyattention_pa_kernel(tc, q_plus, key_plus, retrieval, out):
                 op=ALU.mult,
             )
 
+        for turn in range(len(operands_of(2)) + 1):
+            one_job(operands_of(2), turn)
         make_scores(0)
         make_scores(1)
         for y in range(1, heads(0)):
             raise_top(0, y)
-        for slot in range(n_steps - STEPS + PRODUCT_AT + 1):
-            one_job(operands_of(3), slot)
+        later_operands = operands_of(3) + operands_of(1)
+        head_one_turns = AHEAD + HEAD_STEPS + BEHIND
+        for slot in range(max(LAST_BLOCK + PRODUCT_AT + 1, DRAIN_AT + (head_one_turns + TURNS_A_SLOT - 1) // TURNS_A_SLOT)):
+            one_job(later_operands, slot)
             block, age = divmod(slot - PRODUCT_AT, STEPS)
-            product_due = age == 0 and block >= 0
+            product_due = age == 0 and 0 <= block < n_steps // STEPS
             if product_due:
                 x = steps[block * STEPS][0]
                 sums[block] = multiply_by_values(x, packed[block][0], packed[block][1])
@@ -318,3 +302,7 @@ def tile_anomalyattention_pa_kernel(tc, q_plus, key_plus, retrieval, out):
                 block = (slot - PRODUCT_AT) // STEPS
                 x, c, g = steps[block * STEPS]
                 store_rows(x, c // BLOCK_CHUNKS, sums[block], nc.scalar.copy)
+            if slot >= DRAIN_AT:
+                for turn in range(TURNS_A_SLOT * (slot - DRAIN_AT), TURNS_A_SLOT * (slot - DRAIN_AT + 1)):
+                    if turn < head_one_turns:
+                        head_one_turn(turn - AHEAD)

@@ -19,37 +19,20 @@ PASSES = L // (P * PACK)
 CHUNKS = L // P
 SCALE = 1.0 / math.sqrt(E)
 PAIRS = 9
-NEGATED_PAIR = 1
+NEGATED_PAIRS = (1, 3)
+TINY = 2.0**-62
 
 BLOCK_CHUNKS = 2
 STEPS = BLOCK_CHUNKS * PASSES
 HEAD_STEPS = CHUNKS * PASSES
-BANKS = 8
-RAW_ROOMS = 5
-
-ADD_LAG = 1
-LN_AT = STEPS - 1 + ADD_LAG
-RECIPROCAL_AT = LN_AT + 1
-SPARE = 2
-MULTIPLY_LAG = RECIPROCAL_AT + 1 + SPARE
-QUANTISE_LAG = MULTIPLY_LAG + 1
-PRODUCT_AT = STEPS - 1 + QUANTISE_LAG + 1
-LAST_BLOCK = 2 * HEAD_STEPS - STEPS
-DRAIN_AT = LAST_BLOCK + RECIPROCAL_AT + 1
-
-AHEAD = 5
-BEHIND = 3
-TURNS_A_SLOT = 3
+BLOCKS = HEAD_STEPS // STEPS
+LONG_CHUNK = 6
 
 FLOPS = 2 * 2 * PAIRS * L * L * E
 
 
 def first_pair(x):
     return x * (x + 1) // 2 - 1
-
-
-def pairs_of(x):
-    return range(first_pair(x), first_pair(x) + x + 1)
 
 
 def tile_anomalyattention_pa_kernel(tc, q_plus, key_plus, retrieval, out):
@@ -59,7 +42,7 @@ def tile_anomalyattention_pa_kernel(tc, q_plus, key_plus, retrieval, out):
 
     with tc.manual_schedule(), tc.tile_pool(name="keep", bufs=1) as keep, tc.tile_pool(
         name="work", bufs=2
-    ) as work, tc.psum_pool(name="psum", bufs=BANKS) as psum:
+    ) as work, tc.psum_pool(name="psum", bufs=1) as psum:
         ident = keep.tile([P, P], BF16, name="ident")
         masks.make_identity(nc, ident[:])
         q_t = keep.tile([P, 3, CHUNKS, P], BF16, name="q_t")
@@ -67,76 +50,99 @@ def tile_anomalyattention_pa_kernel(tc, q_plus, key_plus, retrieval, out):
         r_codes = keep.tile([P, PAIRS, PASSES, E], U32, name="r_codes", align_bytes=64)
         r_scales = keep.tile([P, PAIRS, PASSES, E], U8, name="r_scales", align_bytes=64)
 
-        q_raw = keep.tile([P, CHUNKS, 3, E], BF16, name="q_raw")
+        def raw(tag, bufs, pairs, source):
+            room = work.tile([P, len(pairs), PASSES, PACK, E], BF16, tag=tag, bufs=bufs, name="raw", align_bytes=64)
+            return {pair: (room[:, i, :, :, :], source[0, pair].rearrange("(g p t) e -> p g t e", g=PASSES, t=PACK)) for i, pair in enumerate(pairs)}
+
+        q_raw = work.tile([P, CHUNKS, 3, E], BF16, tag="codes3", bufs=1, name="q_raw", align_bytes=64)
         nc.sync.dma_start(out=q_raw[:], in_=q_view)
         k_raw = {}
         r_raw = {}
-        for x in (2, 3, 1):
-            for pair in pairs_of(x):
-                k_raw[pair] = keep.tile([P, PASSES, PACK, E], BF16, tag="k_raw", bufs=RAW_ROOMS, name="k_raw")
-                r_raw[pair] = keep.tile([P, PASSES, PACK, E], BF16, tag="r_raw", bufs=RAW_ROOMS, name="r_raw")
-                nc.sync.dma_start(out=k_raw[pair][:], in_=key_plus[0, pair].rearrange("(g p t) e -> p g t e", g=PASSES, t=PACK))
-                nc.sync.dma_start(out=r_raw[pair][:], in_=retrieval[0, pair].rearrange("(g p t) e -> p g t e", g=PASSES, t=PACK))
+        for pair in range(5, 9):
+            k_raw.update(raw("three_series", 4, (pair,), key_plus))
+        k_raw.update(raw("codes2", 1, (2, 3, 4), key_plus))
+        k_raw.update(raw("four_series", 2, (0, 1), key_plus))
+        r_raw.update(raw("four_series", 2, (5, 6), retrieval))
+        for pair in (5, 6, 7, 8, 3, 4, 2, 0, 1):
+            nc.sync.dma_start(out=k_raw[pair][0], in_=k_raw[pair][1])
+        value_order = (5, 6, 7, 8, 2, 3, 4, 0, 1)
+        for pair in value_order:
+            if pair not in r_raw:
+                r_raw.update(raw("r_raw", 3, (pair,), retrieval))
+            nc.sync.dma_start(out=r_raw[pair][0], in_=r_raw[pair][1])
 
-        def bank(shape, dtype, name):
-            return psum.tile(shape, dtype, tag="bank", name=name)
+        def four_bank(shape, dtype, name):
+            return psum.tile(shape, dtype, tag="four", bufs=5, name=name)
 
-        def transposed(sources):
+        def pair_bank(shape, dtype, name):
+            return psum.tile(shape, dtype, tag="pair", bufs=2, name=name)
+
+        def late_bank(shape, dtype, name):
+            return psum.tile(shape, dtype, tag="late", bufs=1, name=name)
+
+        def flip(sources, bank):
             flipped = bank([P, PACK, P], BF16, "flipped")
             for i, source in enumerate(sources):
                 nc.tensor.transpose(flipped[:, i, :], source, ident[:])
             return flipped
 
-        def flip_queries(x, half):
-            return transposed([q_raw[:, c, x - 1, :] for c in range(half * PACK, (half + 1) * PACK)])
+        def ready_queries(x, half, bank, copy):
+            flipped = flip([q_raw[:, c, x - 1, :] for c in range(half * PACK, (half + 1) * PACK)], bank)
+            copy(out=q_t[:, x - 1, half * PACK : (half + 1) * PACK, :], in_=flipped[:])
 
-        def keep_queries(x, half, flipped):
-            nc.vector.tensor_copy(out=q_t[:, x - 1, half * PACK : (half + 1) * PACK, :], in_=flipped[:])
-
-        def flip_keys(pair, g):
-            return transposed([k_raw[pair][:, g, t, :] for t in range(PACK)])
+        def ready_keys(pair, g, bank, copy):
+            flipped = flip([k_raw[pair][0][:, g, t, :] for t in range(PACK)], bank)
+            if pair in NEGATED_PAIRS:
+                nc.scalar.activation(out=k_t[:, pair, g, :, :], in_=flipped[:], func=ACT.Copy, scale=-1.0)
+            else:
+                copy(out=k_t[:, pair, g, :, :], in_=flipped[:])
 
         grouped = {}
 
-        def keep_pair(pair, g, flipped):
-            if pair == NEGATED_PAIR:
-                nc.vector.tensor_scalar_mul(out=k_t[:, pair, g, :, :], in0=flipped[:], scalar1=-1.0)
-            else:
-                nc.vector.tensor_copy(out=k_t[:, pair, g, :, :], in_=flipped[:])
-            if g == 0:
-                grouped[pair] = work.tile([P, PASSES, E, PACK], BF16, tag="grouped", name="grouped", align_bytes=64)
-                nc.vector.tensor_copy(out=grouped[pair][:], in_=r_raw[pair][:].rearrange("p g t e -> p g e t"))
-            else:
-                nc.vector.quantize_mx(
-                    out=r_codes[:, pair, :, :].rearrange("p g e -> p (g e)").bitcast(FP8X4),
-                    scales=r_scales[:, pair, :, :].rearrange("p g e -> p (g e)"),
-                    in_=grouped[pair][:].rearrange("p g e t -> p (g e t)"),
-                )
+        def group_values(pair):
+            grouped[pair] = work.tile([P, PASSES, E, PACK], BF16, tag="grouped", name="grouped", align_bytes=64)
+            nc.gpsimd.tensor_scalar(
+                out=grouped[pair][:],
+                in0=r_raw[pair][0].rearrange("p g t e -> p g e t"),
+                scalar1=1.0,
+                scalar2=0.0,
+                op0=ALU.mult,
+                op1=ALU.add,
+            )
 
-        def operands_of(x):
-            return [(flip_queries, keep_queries, x, half) for half in range(CHUNKS // PACK)] + [
-                (flip_keys, keep_pair, pair, g) for pair in pairs_of(x) for g in range(PASSES)
-            ]
-
-        flipped_for = {}
-
-        def one_job(jobs, turn):
-            if 1 <= turn <= len(jobs):
-                flip, finish, first, second = jobs[turn - 1]
-                finish(first, second, flipped_for[turn - 1])
-            if turn < len(jobs):
-                flip, finish, first, second = jobs[turn]
-                flipped_for[turn] = flip(first, second)
+        def quantise_values(pair):
+            nc.vector.quantize_mx(
+                out=r_codes[:, pair, :, :].rearrange("p g e -> p (g e)").bitcast(FP8X4),
+                scales=r_scales[:, pair, :, :].rearrange("p g e -> p (g e)"),
+                in_=grouped[pair][:].rearrange("p g e t -> p (g e t)"),
+            )
 
         def by_query(scores):
             return scores[:].rearrange("p t l -> p l t")
 
-        def new_codes(n):
-            codes = work.tile([P, STEPS, n, P], U32, tag="codes", name="codes", align_bytes=64)
-            scales = work.tile([P, STEPS, n, P], U8, tag="scales", name="scales", align_bytes=64)
-            return codes, scales
+        def score(bank, x, step, pairs):
+            c, g = divmod(step, PASSES)
+            for t in range(PACK):
+                for pair in pairs:
+                    nc.tensor.matmul(
+                        bank[:, t, :],
+                        lhsT=k_t[:, pair, g, t, :],
+                        rhs=q_t[:, x - 1, c, :],
+                        start=(pair == pairs[0]),
+                        stop=(pair == pairs[-1]),
+                    )
 
-        def quantise_series(series, n, codes, scales, j):
+        packed = {}
+
+        def quantise(x, step, series):
+            block, j = divmod(step, STEPS)
+            n = x + 1
+            if (x, block) not in packed:
+                packed[x, block] = (
+                    work.tile([P, STEPS, n, P], U32, tag="codes%d" % x, bufs=1, name="codes", align_bytes=64),
+                    work.tile([P, STEPS, n, P], U8, tag="scales%d" % x, bufs=1, name="scales", align_bytes=64),
+                )
+            codes, scales = packed[x, block]
             y = 0
             for run in (4, 2, 1):
                 if n - y >= run:
@@ -147,8 +153,12 @@ def tile_anomalyattention_pa_kernel(tc, q_plus, key_plus, retrieval, out):
                     )
                     y += run
 
-        def multiply_by_values(x, codes, scales):
-            acc = bank([P, BLOCK_CHUNKS, E], F32, "acc")
+        sums = {}
+
+        def product(x, block):
+            codes, scales = packed[x, block]
+            acc = late_bank([P, BLOCK_CHUNKS, E], F32, "acc")
+            sums[x] = acc
             terms = [(g, y) for g in range(PASSES) for y in range(x + 1)]
             for c in range(BLOCK_CHUNKS):
                 for g, y in terms:
@@ -161,148 +171,345 @@ def tile_anomalyattention_pa_kernel(tc, q_plus, key_plus, retrieval, out):
                         start=((g, y) == terms[0]),
                         stop=((g, y) == terms[-1]),
                     )
-            return acc
 
-        def store_rows(x, block, acc, copy_out):
+        def store(x, block, copy):
             result = work.tile([P, BLOCK_CHUNKS, E], F32, name="result")
-            copy_out(out=result[:], in_=acc[:])
+            copy(out=result[:], in_=sums[x][:])
             chunks = slice(block * BLOCK_CHUNKS, (block + 1) * BLOCK_CHUNKS)
             nc.sync.dma_start(out=out_view[:, chunks, x - 1, :], in_=result[:])
 
-        difference = {}
-        series_one = {}
-        packed_one = {}
-        sums_one = {}
+        two_series = {}
 
-        def head_one_scores(step):
-            c, g = divmod(step, PASSES)
-            difference[step] = bank([P, PACK, P], F32, "difference")
-            for t in range(PACK):
-                nc.tensor.matmul(difference[step][:, t, :], lhsT=k_t[:, 0, g, t, :], rhs=q_t[:, 0, c, :], start=True, stop=False)
-                nc.tensor.matmul(difference[step][:, t, :], lhsT=k_t[:, 1, g, t, :], rhs=q_t[:, 0, c, :], start=False, stop=True)
+        def two_sigmoids(step):
+            difference = pair_bank([P, PACK, P], F32, "difference")
+            score(difference, 1, step, (0, 1))
+            two_series[step] = work.tile([P, 2, P, PACK], BF16, tag="two_series", bufs=4, name="two_series", align_bytes=64)
+            nc.scalar.activation(out=two_series[step][:, 0, :, :], in_=by_query(difference), func=ACT.Sigmoid, scale=SCALE)
+            nc.scalar.activation(out=two_series[step][:, 1, :, :], in_=by_query(difference), func=ACT.Sigmoid, scale=-SCALE)
 
-        def head_one_series(step):
-            series_one[step] = work.tile([P, 2, P, PACK], BF16, tag="series_one", bufs=3, name="series_one", align_bytes=64)
-            nc.scalar.activation(out=series_one[step][:, 0, :, :], in_=by_query(difference[step]), func=ACT.Sigmoid, scale=SCALE)
-            nc.scalar.activation(out=series_one[step][:, 1, :, :], in_=by_query(difference[step]), func=ACT.Sigmoid, scale=-SCALE)
+        lower = {}
+        minus_one = {}
+        halves = {}
+        odds = {}
+        three_series = {}
 
-        def head_one_turn(turn):
-            if turn - 2 >= 0 and (turn - 2) % STEPS == STEPS - 1:
-                block = (turn - 2) // STEPS
-                sums_one[block] = multiply_by_values(1, packed_one[block][0], packed_one[block][1])
-            if turn + AHEAD < HEAD_STEPS:
-                head_one_scores(turn + AHEAD)
-            if 0 <= turn < HEAD_STEPS:
-                head_one_series(turn)
-            if 0 <= turn - 1 < HEAD_STEPS:
-                block, j = divmod(turn - 1, STEPS)
-                if j == 0:
-                    packed_one[block] = new_codes(2)
-                quantise_series(series_one[turn - 1], 2, packed_one[block][0], packed_one[block][1], j)
-            if turn - BEHIND >= 0 and (turn - BEHIND) % STEPS == STEPS - 1:
-                block = (turn - BEHIND) // STEPS
-                store_rows(1, block, sums_one[block], nc.vector.tensor_copy)
+        def is_long(step):
+            return step // PASSES == LONG_CHUNK
 
-        steps = [(x, c, g) for x in (2, 3) for c in range(CHUNKS) for g in range(PASSES)]
-        n_steps = len(steps)
-        banks = {}
-        top = {}
-        expo = {}
-        den = {}
-        series = {}
-        packed = {}
-        sums = {}
+        def long_one(step):
+            one = late_bank([P, PACK, P], F32, "one")
+            score(one, 2, step, (3,))
+            minus_one[step] = work.tile([P, P, PACK], F32, tag="plane", bufs=14, name="minus_one")
+            nc.scalar.copy(out=minus_one[step][:], in_=by_query(one))
 
-        def heads(step):
-            return steps[step][0] + 1
+        def long_two(step):
+            two = late_bank([P, PACK, P], F32, "two")
+            score(two, 2, step, (4,))
+            lower[step] = work.tile([P, P, PACK], F32, tag="plane", bufs=14, name="lower")
+            nc.vector.tensor_tensor(out=lower[step][:], in0=by_query(two), in1=minus_one[step][:], op=ALU.add)
 
-        def make_scores(step):
-            x, c, g = steps[step]
-            banks[step] = [bank([P, PACK, P], F32, "scores") for y in range(x + 1)]
-            top[step] = work.tile([P, P, PACK], F32, tag="top", bufs=3, name="top")
-            for y in range(x + 1):
-                for t in range(PACK):
-                    nc.tensor.matmul(
-                        banks[step][y][:, t, :], lhsT=k_t[:, first_pair(x) + y, g, t, :], rhs=q_t[:, x - 1, c, :], start=True, stop=True
-                    )
-            nc.scalar.copy(out=top[step][:], in_=by_query(banks[step][0]))
-
-        def raise_top(step, y):
-            nc.vector.tensor_tensor(out=top[step][:], in0=by_query(banks[step][y]), in1=top[step][:], op=ALU.max)
-
-        def subtract_top(step, y):
-            if y == 0:
-                expo[step] = work.tile([P, heads(step), P, PACK], F32, tag="expo", bufs=MULTIPLY_LAG + 2, name="expo")
-            nc.vector.tensor_tensor(out=expo[step][:, y, :, :], in0=by_query(banks[step][y]), in1=top[step][:], op=ALU.subtract)
-
-        def add_up(step):
-            adder = nc.gpsimd if step + 1 < n_steps else nc.vector
-            block, j = divmod(step, STEPS)
-            if j == 0:
-                den[block] = work.tile([P, STEPS, P, PACK], F32, tag="den", bufs=3, name="den")
-            if heads(step) == 4:
-                half_sums = work.tile([P, 2, P, PACK], F32, name="half_sums")
-                adder.tensor_tensor(out=half_sums[:], in0=expo[step][:, 0:2, :, :], in1=expo[step][:, 2:4, :, :], op=ALU.add)
-                adder.tensor_tensor(out=den[block][:, j, :, :], in0=half_sums[:, 0, :, :], in1=half_sums[:, 1, :, :], op=ALU.add)
+        def three_sigmoids(step):
+            halves[step] = work.tile([P, 2, P, PACK], F32, tag="halves", bufs=8, name="halves")
+            if is_long(step):
+                source = lower[step][:]
             else:
-                adder.tensor_tensor(out=den[block][:, j, :, :], in0=expo[step][:, 0, :, :], in1=expo[step][:, 1, :, :], op=ALU.add)
-                adder.tensor_tensor(out=den[block][:, j, :, :], in0=den[block][:, j, :, :], in1=expo[step][:, 2, :, :], op=ALU.add)
+                difference = pair_bank([P, PACK, P], F32, "difference")
+                score(difference, 2, step, (4, 3))
+                source = by_query(difference)
+            nc.scalar.activation(out=halves[step][:, 0, :, :], in_=source, func=ACT.Sigmoid, scale=-SCALE)
+            nc.scalar.activation(out=halves[step][:, 1, :, :], in_=source, func=ACT.Sigmoid, scale=SCALE)
+            if not is_long(step):
+                lower[step] = work.tile([P, P, PACK], F32, tag="plane", bufs=14, name="lower")
+                nc.scalar.copy(out=lower[step][:], in_=source)
 
-        def multiply(step):
-            block, j = divmod(step, STEPS)
-            n = heads(step)
-            series[step] = work.tile([P, n, P, PACK], BF16, tag="series", bufs=3, name="series", align_bytes=64)
+        def three_ln(step):
+            odds[step] = work.tile([P, P, PACK], F32, tag="plane", bufs=14, name="odds")
+            nc.scalar.activation(out=odds[step][:], in_=halves[step][:, 0, :, :], func=ACT.Ln, bias=tiny[:])
+
+        def three_guard(step):
+            nc.vector.scalar_tensor_tensor(
+                out=odds[step][:], in0=lower[step][:], scalar=-SCALE, in1=odds[step][:], op0=ALU.mult, op1=ALU.min
+            )
+
+        def three_z(step):
+            bank = pair_bank([P, PACK, P], F32, "upper")
+            if is_long(step):
+                score(bank, 2, step, (2,))
+                nc.vector.tensor_tensor(out=minus_one[step][:], in0=by_query(bank), in1=minus_one[step][:], op=ALU.add)
+                source = minus_one[step][:]
+            else:
+                score(bank, 2, step, (2, 3))
+                source = by_query(bank)
+            nc.vector.scalar_tensor_tensor(out=odds[step][:], in0=source, scalar=SCALE, in1=odds[step][:], op0=ALU.mult, op1=ALU.add)
+
+        def three_split(step):
+            three_series[step] = work.tile([P, 3, P, PACK], BF16, tag="three_series", bufs=4, name="three_series", align_bytes=64)
+            nc.scalar.activation(out=three_series[step][:, 0, :, :], in_=odds[step][:], func=ACT.Sigmoid)
+            nc.scalar.activation(out=odds[step][:], in_=odds[step][:], func=ACT.Sigmoid, scale=-1.0)
+
+        def three_multiply(step):
             nc.vector.tensor_tensor(
-                out=series[step][:],
-                in0=expo[step][:],
-                in1=den[block][:, j, :, :].unsqueeze(1).to_broadcast([P, n, P, PACK]),
+                out=three_series[step][:, 1:3, :, :],
+                in0=halves[step][:],
+                in1=odds[step][:].unsqueeze(1).to_broadcast([P, 2, P, PACK]),
                 op=ALU.mult,
             )
 
-        for turn in range(len(operands_of(2)) + 1):
-            one_job(operands_of(2), turn)
-        make_scores(0)
-        make_scores(1)
-        for y in range(1, heads(0)):
-            raise_top(0, y)
-        later_operands = operands_of(3) + operands_of(1)
-        head_one_turns = AHEAD + HEAD_STEPS + BEHIND
-        for slot in range(max(LAST_BLOCK + PRODUCT_AT + 1, DRAIN_AT + (head_one_turns + TURNS_A_SLOT - 1) // TURNS_A_SLOT)):
-            one_job(later_operands, slot)
-            block, age = divmod(slot - PRODUCT_AT, STEPS)
-            product_due = age == 0 and 0 <= block < n_steps // STEPS
-            if product_due:
-                x = steps[block * STEPS][0]
-                sums[block] = multiply_by_values(x, packed[block][0], packed[block][1])
-            if slot + 2 < n_steps:
-                make_scores(slot + 2)
-            if 0 <= slot - ADD_LAG < n_steps:
-                add_up(slot - ADD_LAG)
-            for y in range(PACK):
-                if slot + 1 < n_steps and y + 1 < heads(slot + 1):
-                    raise_top(slot + 1, y + 1)
-                if slot < n_steps and y < heads(slot):
-                    subtract_top(slot, y)
-            if slot < n_steps:
-                nc.scalar.activation(out=expo[slot][:], in_=expo[slot][:], func=ACT.Exp, scale=SCALE)
-            block, age = divmod(slot - LN_AT, STEPS)
-            if age == 0 and 0 <= block < n_steps // STEPS:
-                nc.scalar.activation(out=den[block][:], in_=den[block][:], func=ACT.Ln)
-            block, age = divmod(slot - RECIPROCAL_AT, STEPS)
-            if age == 0 and 0 <= block < n_steps // STEPS:
-                nc.scalar.activation(out=den[block][:], in_=den[block][:], func=ACT.Exp, scale=-1.0)
-            if 0 <= slot - QUANTISE_LAG < n_steps:
-                block, j = divmod(slot - QUANTISE_LAG, STEPS)
-                if j == 0:
-                    packed[block] = new_codes(heads(slot - QUANTISE_LAG))
-                quantise_series(series[slot - QUANTISE_LAG], heads(slot - QUANTISE_LAG), packed[block][0], packed[block][1], j)
-            if 0 <= slot - MULTIPLY_LAG < n_steps:
-                multiply(slot - MULTIPLY_LAG)
-            if product_due:
-                block = (slot - PRODUCT_AT) // STEPS
-                x, c, g = steps[block * STEPS]
-                store_rows(x, c // BLOCK_CHUNKS, sums[block], nc.scalar.copy)
-            if slot >= DRAIN_AT:
-                for turn in range(TURNS_A_SLOT * (slot - DRAIN_AT), TURNS_A_SLOT * (slot - DRAIN_AT + 1)):
-                    if turn < head_one_turns:
-                        head_one_turn(turn - AHEAD)
+        banks = {}
+        top = {}
+        expo = {}
+        den = keep.tile([P, STEPS, P, PACK], F32, name="den")
+        four_series = {}
+
+        def four_score(step, y):
+            if step < HEAD_STEPS:
+                banks[step, y] = four_bank([P, PACK, P], F32, "scores")
+                score(banks[step, y], 3, step, (first_pair(3) + y,))
+
+        def four_copy(step):
+            if step < HEAD_STEPS:
+                top[step] = work.tile([P, P, PACK], F32, tag="plane", bufs=14, name="top")
+                nc.scalar.copy(out=top[step][:], in_=by_query(banks[step, 0]))
+
+        def raise_top(step, y):
+            if step < HEAD_STEPS:
+                nc.vector.tensor_tensor(out=top[step][:], in0=by_query(banks[step, y]), in1=top[step][:], op=ALU.max)
+
+        def subtract_top(step, y):
+            if y == 0:
+                expo[step] = work.tile([P, 4, P, PACK], F32, tag="expo", bufs=8, name="expo")
+            nc.vector.tensor_tensor(out=expo[step][:, y, :, :], in0=by_query(banks[step, y]), in1=top[step][:], op=ALU.subtract)
+
+        def four_unit(step, fill=()):
+            subtract_top(step, 0)
+            four_score(step + 1, 1)
+            for job in fill[0:1]:
+                job()
+            subtract_top(step, 1)
+            raise_top(step + 1, 1)
+            four_score(step + 1, 2)
+            for job in fill[1:2]:
+                job()
+            subtract_top(step, 2)
+            raise_top(step + 1, 2)
+            four_score(step + 1, 3)
+            for job in fill[2:3]:
+                job()
+            subtract_top(step, 3)
+            raise_top(step + 1, 3)
+            four_score(step + 2, 0)
+            four_copy(step + 2)
+            for job in fill[3:]:
+                job()
+
+        def four_exp(step):
+            nc.scalar.activation(out=expo[step][:], in_=expo[step][:], func=ACT.Exp, scale=SCALE)
+
+        def four_add(step):
+            adder = nc.gpsimd if step < HEAD_STEPS - STEPS else nc.vector
+            here = den[:, step % STEPS, :, :]
+            half_sum = work.tile([P, P, PACK], F32, tag="plane", bufs=14, name="half_sum")
+            adder.tensor_tensor(out=here, in0=expo[step][:, 0, :, :], in1=expo[step][:, 1, :, :], op=ALU.add)
+            adder.tensor_tensor(out=half_sum[:], in0=expo[step][:, 2, :, :], in1=expo[step][:, 3, :, :], op=ALU.add)
+            adder.tensor_tensor(out=here, in0=here, in1=half_sum[:], op=ALU.add)
+
+        def four_ln(block):
+            nc.scalar.activation(out=den[:], in_=den[:], func=ACT.Ln)
+
+        def four_reciprocal(block):
+            nc.scalar.activation(out=den[:], in_=den[:], func=ACT.Exp, scale=-1.0)
+
+        def four_multiply(step):
+            block, j = divmod(step, STEPS)
+            four_series[step] = work.tile([P, 4, P, PACK], BF16, tag="four_series", bufs=2, name="four_series", align_bytes=64)
+            nc.vector.tensor_tensor(
+                out=four_series[step][:],
+                in0=expo[step][:],
+                in1=den[:, j, :, :].unsqueeze(1).to_broadcast([P, 4, P, PACK]),
+                op=ALU.mult,
+            )
+
+        tiny = keep.tile([P, 1], F32, name="tiny")
+        nc.vector.memset(tiny[:], TINY)
+
+        vcopy = nc.vector.tensor_copy
+        scopy = nc.scalar.copy
+        ready_queries(3, 0, four_bank, vcopy)
+        for pair in range(5, 9):
+            ready_keys(pair, 0, four_bank, vcopy)
+        for y in range(4):
+            four_score(0, y)
+        four_copy(0)
+        for pair, y in zip(range(5, 9), (1, 2, 3, 4)):
+            ready_keys(pair, 1, late_bank, vcopy)
+            if y < 4:
+                raise_top(0, y)
+        four_score(1, 0)
+        four_copy(1)
+
+        def queries(x, half):
+            return lambda: ready_queries(x, half, pair_bank, scopy)
+
+        def keys(pair, g):
+            return lambda: ready_keys(pair, g, pair_bank, scopy)
+
+        def two(step):
+            return lambda: two_sigmoids(step)
+
+        def three(step):
+            return lambda: three_sigmoids(step)
+
+        def split(step):
+            return lambda: three_split(step)
+
+        def steps_of(block):
+            return range(block * STEPS, (block + 1) * STEPS) if 0 <= block < BLOCKS else range(0)
+
+        def at(block, j):
+            return steps_of(block)[j : j + 1] if j >= 0 else ()
+
+        def blocks(block):
+            return (block,) if 0 <= block < BLOCKS else ()
+
+        values_ready = []
+
+        def next_values():
+            if values_ready:
+                quantise_values(values_ready[-1])
+            if len(values_ready) < PAIRS:
+                values_ready.append(value_order[len(values_ready)])
+                group_values(values_ready[-1])
+
+        next_values()
+        flips = [
+            [queries(2, 0), keys(3, 0), keys(4, 0)],
+            [keys(3, 1), keys(4, 1)],
+            [keys(2, 0), keys(2, 1)],
+            [queries(1, 0), keys(0, 0), keys(1, 0)],
+        ]
+        for step in range(STEPS):
+            four_unit(step, flips[step])
+            next_values()
+            four_exp(step)
+            four_add(step)
+
+        for w in range(BLOCKS):
+            long = [step for step in steps_of(w) if is_long(step)]
+            twos = {1: (0,), 2: (1,)}.get(w, ())
+            for block in blocks(w - 1):
+                four_reciprocal(block)
+            for step in steps_of(w - 1):
+                three_guard(step)
+            for block in blocks(w - 2):
+                store(2, block, vcopy)
+            for step in steps_of(w - 1):
+                three_z(step)
+            for step in steps_of(w) if w else ():
+                four_exp(step)
+            fills = {row: [] for row in range(STEPS)}
+            for j in range(STEPS):
+                fills[1 + j // 2] += [split(step) for step in at(w - 1, j)]
+                for block in twos:
+                    fills[1 + j // 2] += [two(step) for step in at(block, j)]
+                if w:
+                    fills[3] += [three(step) for step in at(w, j)]
+                else:
+                    fills[j // 2] += [three(step) for step in at(w, j)]
+            if w == 0:
+                fills[1] += [queries(3, 1)]
+                fills[2] = [keys(0, 1), keys(1, 1)]
+                fills[3] = [queries(2, 1), queries(1, 1)]
+            for row in range(STEPS):
+                for step in at(w - 1, row - 1):
+                    quantise(3, step, four_series[step])
+                for step in at(w - 1, row):
+                    four_multiply(step)
+                for step in at(w, row) if w else ():
+                    four_add(step)
+                if row == 2 and long:
+                    long_two(long[0])
+                    long_one(long[1])
+                if row == 3 and long:
+                    long_two(long[1])
+                for step in at(w + 1, row):
+                    four_unit(step, fills[row])
+                if w + 1 >= BLOCKS:
+                    for job in fills[row]:
+                        job()
+                if row == 0 and long:
+                    long_one(long[0])
+                if w == 0:
+                    next_values()
+            for step in steps_of(w):
+                three_ln(step)
+            for block in blocks(w):
+                four_ln(block)
+            if w == 0:
+                next_values()
+            for step in at(w - 1, STEPS - 1):
+                quantise(3, step, four_series[step])
+            for block in blocks(w - 1):
+                product(3, block)
+            for j in range(STEPS):
+                for step in at(w - 1, j):
+                    three_multiply(step)
+                for block in twos:
+                    for step in at(block, j):
+                        quantise(1, step, two_series[step])
+                for step in at(w - 1, j - 1):
+                    quantise(2, step, three_series[step])
+                if j == 1:
+                    for block in blocks(w - 1):
+                        store(3, block, vcopy)
+            for step in at(w - 1, STEPS - 1):
+                quantise(2, step, three_series[step])
+            for block in twos:
+                product(1, block)
+                store(1, block, vcopy)
+            for block in blocks(w - 1):
+                product(2, block)
+
+        last = BLOCKS - 1
+        four_reciprocal(last)
+        for step in steps_of(last):
+            three_guard(step)
+        store(2, last - 1, vcopy)
+        for step in steps_of(last):
+            three_z(step)
+        for step in steps_of(last):
+            three_split(step)
+        for block in (2, 3):
+            for step in steps_of(block):
+                two_sigmoids(step)
+        four_multiply(12)
+        four_multiply(13)
+        quantise(3, 12, four_series[12])
+        three_multiply(12)
+        quantise(3, 13, four_series[13])
+        four_multiply(14)
+        quantise(2, 12, three_series[12])
+        three_multiply(13)
+        quantise(3, 14, four_series[14])
+        quantise(1, 8, two_series[8])
+        four_multiply(15)
+        quantise(2, 13, three_series[13])
+        quantise(1, 9, two_series[9])
+        three_multiply(14)
+        quantise(3, 15, four_series[15])
+        product(3, last)
+        quantise(1, 10, two_series[10])
+        quantise(1, 11, two_series[11])
+        three_multiply(15)
+        quantise(2, 14, three_series[14])
+        store(3, last, vcopy)
+        product(1, 2)
+        quantise(2, 15, three_series[15])
+        store(1, 2, vcopy)
+        product(2, last)
+        quantise(1, 12, two_series[12])
+        quantise(1, 13, two_series[13])
+        store(2, last, vcopy)
+        quantise(1, 14, two_series[14])
+        quantise(1, 15, two_series[15])
+        product(1, 3)
+        store(1, 3, vcopy)

@@ -54,45 +54,51 @@ def tile_anomalyattention_pa_kernel(tc, q_plus, key_plus, retrieval, out):
             room = work.tile([P, len(pairs), PASSES, PACK, E], BF16, tag=tag, bufs=bufs, name="raw", align_bytes=64)
             return {pair: (room[:, i, :, :, :], source[0, pair].rearrange("(g p t) e -> p g t e", g=PASSES, t=PACK)) for i, pair in enumerate(pairs)}
 
+        def load(raws, pair):
+            nc.sync.dma_start(out=raws[pair][0], in_=raws[pair][1])
+
         q_raw = work.tile([P, CHUNKS, 3, E], BF16, tag="codes3", bufs=1, name="q_raw", align_bytes=64)
-        nc.sync.dma_start(out=q_raw[:], in_=q_view)
         k_raw = {}
         r_raw = {}
-        for pair in range(5, 9):
-            k_raw.update(raw("three_series", 4, (pair,), key_plus))
-        k_raw.update(raw("codes2", 1, (2, 3, 4), key_plus))
-        k_raw.update(raw("four_series", 2, (0, 1), key_plus))
+        k_raw.update(raw("three_series", 2, (5, 6, 7), key_plus))
+        k_raw.update(raw("three_series", 2, (8, 3, 4), key_plus))
+        k_raw.update(raw("codes2", 1, (2, 0, 1), key_plus))
         r_raw.update(raw("four_series", 2, (5, 6), retrieval))
-        for pair in (5, 6, 7, 8, 3, 4, 2, 0, 1):
-            nc.sync.dma_start(out=k_raw[pair][0], in_=k_raw[pair][1])
+        r_raw.update(raw("four_series", 2, (7, 8), retrieval))
+        load(k_raw, 5)
+        nc.sync.dma_start(out=q_raw[:, 0:PACK, :, :], in_=q_view[:, 0:PACK, :, :])
+        for pair in (6, 7, 8, 3, 4, 2):
+            load(k_raw, pair)
+        nc.sync.dma_start(out=q_raw[:, PACK:CHUNKS, :, :], in_=q_view[:, PACK:CHUNKS, :, :])
+        load(k_raw, 0)
+        load(k_raw, 1)
         value_order = (5, 6, 7, 8, 2, 3, 4, 0, 1)
         for pair in value_order:
             if pair not in r_raw:
-                r_raw.update(raw("r_raw", 3, (pair,), retrieval))
-            nc.sync.dma_start(out=r_raw[pair][0], in_=r_raw[pair][1])
+                r_raw.update(raw("r_raw", 2, (pair,), retrieval))
+            load(r_raw, pair)
 
-        def four_bank(shape, dtype, name):
-            return psum.tile(shape, dtype, tag="four", bufs=5, name=name)
+        def bank(shape, dtype, name):
+            return psum.tile(shape, dtype, tag="bank", bufs=8, name=name)
 
-        def pair_bank(shape, dtype, name):
-            return psum.tile(shape, dtype, tag="pair", bufs=2, name=name)
+        vcopy = nc.vector.tensor_copy
+        scopy = nc.scalar.copy
 
-        def late_bank(shape, dtype, name):
-            return psum.tile(shape, dtype, tag="late", bufs=1, name=name)
-
-        def flip(sources, bank):
+        def flip(sources):
             flipped = bank([P, PACK, P], BF16, "flipped")
             for i, source in enumerate(sources):
                 nc.tensor.transpose(flipped[:, i, :], source, ident[:])
             return flipped
 
-        def ready_queries(x, half, bank, copy):
-            flipped = flip([q_raw[:, c, x - 1, :] for c in range(half * PACK, (half + 1) * PACK)], bank)
+        def ready_queries(x, half, copy):
+            flipped = flip([q_raw[:, c, x - 1, :] for c in range(half * PACK, (half + 1) * PACK)])
             copy(out=q_t[:, x - 1, half * PACK : (half + 1) * PACK, :], in_=flipped[:])
 
-        def ready_keys(pair, g, bank, copy):
-            flipped = flip([k_raw[pair][0][:, g, t, :] for t in range(PACK)], bank)
-            if pair in NEGATED_PAIRS:
+        def ready_keys(pair, g, copy):
+            flipped = flip([k_raw[pair][0][:, g, t, :] for t in range(PACK)])
+            if pair in NEGATED_PAIRS and copy is vcopy:
+                nc.vector.tensor_scalar_mul(out=k_t[:, pair, g, :, :], in0=flipped[:], scalar1=-1.0)
+            elif pair in NEGATED_PAIRS:
                 nc.scalar.activation(out=k_t[:, pair, g, :, :], in_=flipped[:], func=ACT.Copy, scale=-1.0)
             else:
                 copy(out=k_t[:, pair, g, :, :], in_=flipped[:])
@@ -134,38 +140,40 @@ def tile_anomalyattention_pa_kernel(tc, q_plus, key_plus, retrieval, out):
 
         packed = {}
 
-        def quantise(x, step, series):
-            block, j = divmod(step, STEPS)
-            n = x + 1
-            if (x, block) not in packed:
-                packed[x, block] = (
-                    work.tile([P, STEPS, n, P], U32, tag="codes%d" % x, bufs=1, name="codes", align_bytes=64),
-                    work.tile([P, STEPS, n, P], U8, tag="scales%d" % x, bufs=1, name="scales", align_bytes=64),
+        def room_for_codes(x, chunk):
+            key = (x, chunk // BLOCK_CHUNKS)
+            if key not in packed:
+                packed[key] = (
+                    work.tile([P, BLOCK_CHUNKS, PASSES * (x + 1), P], U32, tag="codes%d" % x, bufs=1, name="codes", align_bytes=64),
+                    work.tile([P, BLOCK_CHUNKS, PASSES * (x + 1), P], U8, tag="scales%d" % x, bufs=1, name="scales", align_bytes=64),
                 )
-            codes, scales = packed[x, block]
-            y = 0
-            for run in (4, 2, 1):
-                if n - y >= run:
-                    nc.vector.quantize_mx(
-                        out=codes[:, j, y : y + run, :].rearrange("p y l -> p (y l)").bitcast(FP8X4),
-                        scales=scales[:, j, y : y + run, :].rearrange("p y l -> p (y l)"),
-                        in_=series[:, y : y + run, :, :].rearrange("p y l t -> p (y l t)"),
-                    )
-                    y += run
+            return packed[key]
+
+        def quantise(x, chunk, at, n, series):
+            codes, scales = room_for_codes(x, chunk)
+            c = chunk % BLOCK_CHUNKS
+            nc.vector.quantize_mx(
+                out=codes[:, c, at : at + n, :].rearrange("p y l -> p (y l)").bitcast(FP8X4),
+                scales=scales[:, c, at : at + n, :].rearrange("p y l -> p (y l)"),
+                in_=series,
+            )
+
+        def row_of(x, g, y):
+            return g * (x + 1) + y if x == 3 else y * PASSES + g
 
         sums = {}
 
         def product(x, block):
             codes, scales = packed[x, block]
-            acc = late_bank([P, BLOCK_CHUNKS, E], F32, "acc")
+            acc = bank([P, BLOCK_CHUNKS, E], F32, "acc")
             sums[x] = acc
             terms = [(g, y) for g in range(PASSES) for y in range(x + 1)]
             for c in range(BLOCK_CHUNKS):
                 for g, y in terms:
                     nc.tensor.matmul_mx(
                         out=acc[:, c, :],
-                        lhsT=codes[:, c * PASSES + g, y, :].bitcast(FP8X4),
-                        lhsT_scale=scales[:, c * PASSES + g, y, :],
+                        lhsT=codes[:, c, row_of(x, g, y), :].bitcast(FP8X4),
+                        lhsT_scale=scales[:, c, row_of(x, g, y), :],
                         rhs=r_codes[:, first_pair(x) + y, g, :].bitcast(FP8X4),
                         rhs_scale=r_scales[:, first_pair(x) + y, g, :],
                         start=((g, y) == terms[0]),
@@ -180,12 +188,22 @@ def tile_anomalyattention_pa_kernel(tc, q_plus, key_plus, retrieval, out):
 
         two_series = {}
 
+        differences = {}
+
+        def two_scores(step):
+            differences[1, step] = bank([P, PACK, P], F32, "difference")
+            score(differences[1, step], 1, step, (0, 1))
+
         def two_sigmoids(step):
-            difference = pair_bank([P, PACK, P], F32, "difference")
-            score(difference, 1, step, (0, 1))
-            two_series[step] = work.tile([P, 2, P, PACK], BF16, tag="two_series", bufs=4, name="two_series", align_bytes=64)
-            nc.scalar.activation(out=two_series[step][:, 0, :, :], in_=by_query(difference), func=ACT.Sigmoid, scale=SCALE)
-            nc.scalar.activation(out=two_series[step][:, 1, :, :], in_=by_query(difference), func=ACT.Sigmoid, scale=-SCALE)
+            difference = differences[1, step]
+            chunk, g = divmod(step, PASSES)
+            if g == 0:
+                two_series[chunk] = work.tile([P, 2, PASSES, P, PACK], BF16, tag="two_series", bufs=2, name="two_series", align_bytes=64)
+            nc.scalar.activation(out=two_series[chunk][:, 0, g, :, :], in_=by_query(difference), func=ACT.Sigmoid, scale=SCALE)
+            nc.scalar.activation(out=two_series[chunk][:, 1, g, :, :], in_=by_query(difference), func=ACT.Sigmoid, scale=-SCALE)
+
+        def two_quantise(chunk):
+            quantise(1, chunk, 0, 4, two_series[chunk][:].rearrange("p y g l t -> p (y g l t)"))
 
         lower = {}
         minus_one = {}
@@ -193,67 +211,86 @@ def tile_anomalyattention_pa_kernel(tc, q_plus, key_plus, retrieval, out):
         odds = {}
         three_series = {}
 
+        def two_planes(name):
+            return work.tile([P, PASSES, P, PACK], F32, tag="two_planes", bufs=6, name=name)
+
         def is_long(step):
             return step // PASSES == LONG_CHUNK
 
         def long_one(step):
-            one = late_bank([P, PACK, P], F32, "one")
+            one = bank([P, PACK, P], F32, "one")
             score(one, 2, step, (3,))
-            minus_one[step] = work.tile([P, P, PACK], F32, tag="plane", bufs=14, name="minus_one")
+            minus_one[step] = work.tile([P, P, PACK], F32, tag="plane", bufs=6, name="minus_one")
             nc.scalar.copy(out=minus_one[step][:], in_=by_query(one))
 
         def long_two(step):
-            two = late_bank([P, PACK, P], F32, "two")
+            two = bank([P, PACK, P], F32, "two")
             score(two, 2, step, (4,))
-            lower[step] = work.tile([P, P, PACK], F32, tag="plane", bufs=14, name="lower")
-            nc.vector.tensor_tensor(out=lower[step][:], in0=by_query(two), in1=minus_one[step][:], op=ALU.add)
+            chunk, g = divmod(step, PASSES)
+            if g == 0:
+                lower[chunk] = two_planes("lower")
+            nc.vector.tensor_tensor(out=lower[chunk][:, g, :, :], in0=by_query(two), in1=minus_one[step][:], op=ALU.add)
+
+        def three_scores(step):
+            if not is_long(step):
+                differences[2, step] = bank([P, PACK, P], F32, "difference")
+                score(differences[2, step], 2, step, (4, 3))
 
         def three_sigmoids(step):
-            halves[step] = work.tile([P, 2, P, PACK], F32, tag="halves", bufs=8, name="halves")
+            chunk, g = divmod(step, PASSES)
+            if g == 0:
+                halves[chunk] = work.tile([P, 2, PASSES, P, PACK], F32, tag="halves", bufs=4, name="halves")
             if is_long(step):
-                source = lower[step][:]
+                source = lower[chunk][:, g, :, :]
             else:
-                difference = pair_bank([P, PACK, P], F32, "difference")
-                score(difference, 2, step, (4, 3))
-                source = by_query(difference)
-            nc.scalar.activation(out=halves[step][:, 0, :, :], in_=source, func=ACT.Sigmoid, scale=-SCALE)
-            nc.scalar.activation(out=halves[step][:, 1, :, :], in_=source, func=ACT.Sigmoid, scale=SCALE)
+                source = by_query(differences[2, step])
+                if g == 0:
+                    lower[chunk] = two_planes("lower")
+            nc.scalar.activation(out=halves[chunk][:, 0, g, :, :], in_=source, func=ACT.Sigmoid, scale=-SCALE)
+            nc.scalar.activation(out=halves[chunk][:, 1, g, :, :], in_=source, func=ACT.Sigmoid, scale=SCALE)
             if not is_long(step):
-                lower[step] = work.tile([P, P, PACK], F32, tag="plane", bufs=14, name="lower")
-                nc.scalar.copy(out=lower[step][:], in_=source)
+                nc.scalar.copy(out=lower[chunk][:, g, :, :], in_=source)
 
-        def three_ln(step):
-            odds[step] = work.tile([P, P, PACK], F32, tag="plane", bufs=14, name="odds")
-            nc.scalar.activation(out=odds[step][:], in_=halves[step][:, 0, :, :], func=ACT.Ln, bias=tiny[:])
+        def three_ln(chunk):
+            odds[chunk] = two_planes("odds")
+            nc.scalar.activation(out=odds[chunk][:], in_=halves[chunk][:, 0, :, :, :], func=ACT.Ln, bias=tiny[:])
 
-        def three_guard(step):
+        def three_guard(chunk):
             nc.vector.scalar_tensor_tensor(
-                out=odds[step][:], in0=lower[step][:], scalar=-SCALE, in1=odds[step][:], op0=ALU.mult, op1=ALU.min
+                out=odds[chunk][:], in0=lower[chunk][:], scalar=-SCALE, in1=odds[chunk][:], op0=ALU.mult, op1=ALU.min
             )
+
+        upper = {}
+
+        def three_upper(step):
+            upper[step] = bank([P, PACK, P], F32, "upper")
+            score(upper[step], 2, step, (2,) if is_long(step) else (2, 3))
 
         def three_z(step):
-            bank = pair_bank([P, PACK, P], F32, "upper")
+            chunk, g = divmod(step, PASSES)
+            source = by_query(upper[step])
             if is_long(step):
-                score(bank, 2, step, (2,))
-                nc.vector.tensor_tensor(out=minus_one[step][:], in0=by_query(bank), in1=minus_one[step][:], op=ALU.add)
+                nc.vector.tensor_tensor(out=minus_one[step][:], in0=source, in1=minus_one[step][:], op=ALU.add)
                 source = minus_one[step][:]
-            else:
-                score(bank, 2, step, (2, 3))
-                source = by_query(bank)
-            nc.vector.scalar_tensor_tensor(out=odds[step][:], in0=source, scalar=SCALE, in1=odds[step][:], op0=ALU.mult, op1=ALU.add)
+            here = odds[chunk][:, g, :, :]
+            nc.vector.scalar_tensor_tensor(out=here, in0=source, scalar=SCALE, in1=here, op0=ALU.mult, op1=ALU.add)
 
-        def three_split(step):
-            three_series[step] = work.tile([P, 3, P, PACK], BF16, tag="three_series", bufs=4, name="three_series", align_bytes=64)
-            nc.scalar.activation(out=three_series[step][:, 0, :, :], in_=odds[step][:], func=ACT.Sigmoid)
-            nc.scalar.activation(out=odds[step][:], in_=odds[step][:], func=ACT.Sigmoid, scale=-1.0)
+        def three_split(chunk):
+            three_series[chunk] = work.tile([P, 3, PASSES, P, PACK], BF16, tag="three_series", bufs=2, name="three_series", align_bytes=64)
+            nc.scalar.activation(out=three_series[chunk][:, 0, :, :, :], in_=odds[chunk][:], func=ACT.Sigmoid)
+            nc.scalar.activation(out=odds[chunk][:], in_=odds[chunk][:], func=ACT.Sigmoid, scale=-1.0)
 
-        def three_multiply(step):
+        def three_multiply(chunk):
             nc.vector.tensor_tensor(
-                out=three_series[step][:, 1:3, :, :],
-                in0=halves[step][:],
-                in1=odds[step][:].unsqueeze(1).to_broadcast([P, 2, P, PACK]),
+                out=three_series[chunk][:, 1:3, :, :, :],
+                in0=halves[chunk][:],
+                in1=odds[chunk][:].unsqueeze(1).to_broadcast([P, 2, PASSES, P, PACK]),
                 op=ALU.mult,
             )
+
+        def three_quantise(chunk):
+            quantise(2, chunk, 0, 4, three_series[chunk][:, 0:2, :, :, :].rearrange("p y g l t -> p (y g l t)"))
+            quantise(2, chunk, 4, 2, three_series[chunk][:, 2, :, :, :].rearrange("p g l t -> p (g l t)"))
 
         banks = {}
         top = {}
@@ -263,12 +300,12 @@ def tile_anomalyattention_pa_kernel(tc, q_plus, key_plus, retrieval, out):
 
         def four_score(step, y):
             if step < HEAD_STEPS:
-                banks[step, y] = four_bank([P, PACK, P], F32, "scores")
+                banks[step, y] = bank([P, PACK, P], F32, "scores")
                 score(banks[step, y], 3, step, (first_pair(3) + y,))
 
         def four_copy(step):
             if step < HEAD_STEPS:
-                top[step] = work.tile([P, P, PACK], F32, tag="plane", bufs=14, name="top")
+                top[step] = work.tile([P, P, PACK], F32, tag="plane", bufs=6, name="top")
                 nc.scalar.copy(out=top[step][:], in_=by_query(banks[step, 0]))
 
         def raise_top(step, y):
@@ -280,26 +317,30 @@ def tile_anomalyattention_pa_kernel(tc, q_plus, key_plus, retrieval, out):
                 expo[step] = work.tile([P, 4, P, PACK], F32, tag="expo", bufs=8, name="expo")
             nc.vector.tensor_tensor(out=expo[step][:, y, :, :], in0=by_query(banks[step, y]), in1=top[step][:], op=ALU.subtract)
 
-        def four_unit(step, fill=()):
-            subtract_top(step, 0)
+        def four_unit(step, before=(), after=()):
+            jobs = list(before)
+
+            def one_job():
+                if jobs:
+                    jobs.pop(0)()
+
             four_score(step + 1, 1)
-            for job in fill[0:1]:
-                job()
-            subtract_top(step, 1)
-            raise_top(step + 1, 1)
+            subtract_top(step, 0)
             four_score(step + 1, 2)
-            for job in fill[1:2]:
-                job()
-            subtract_top(step, 2)
-            raise_top(step + 1, 2)
+            raise_top(step + 1, 1)
+            one_job()
+            subtract_top(step, 1)
             four_score(step + 1, 3)
-            for job in fill[2:3]:
-                job()
-            subtract_top(step, 3)
-            raise_top(step + 1, 3)
+            raise_top(step + 1, 2)
+            one_job()
+            subtract_top(step, 2)
             four_score(step + 2, 0)
+            while jobs:
+                one_job()
             four_copy(step + 2)
-            for job in fill[3:]:
+            raise_top(step + 1, 3)
+            subtract_top(step, 3)
+            for job in after:
                 job()
 
         def four_exp(step):
@@ -308,7 +349,7 @@ def tile_anomalyattention_pa_kernel(tc, q_plus, key_plus, retrieval, out):
         def four_add(step):
             adder = nc.gpsimd if step < HEAD_STEPS - STEPS else nc.vector
             here = den[:, step % STEPS, :, :]
-            half_sum = work.tile([P, P, PACK], F32, tag="plane", bufs=14, name="half_sum")
+            half_sum = work.tile([P, P, PACK], F32, tag="plane", bufs=6, name="half_sum")
             adder.tensor_tensor(out=here, in0=expo[step][:, 0, :, :], in1=expo[step][:, 1, :, :], op=ALU.add)
             adder.tensor_tensor(out=half_sum[:], in0=expo[step][:, 2, :, :], in1=expo[step][:, 3, :, :], op=ALU.add)
             adder.tensor_tensor(out=here, in0=here, in1=half_sum[:], op=ALU.add)
@@ -329,47 +370,70 @@ def tile_anomalyattention_pa_kernel(tc, q_plus, key_plus, retrieval, out):
                 op=ALU.mult,
             )
 
+        def four_quantise(step):
+            chunk, g = divmod(step, PASSES)
+            quantise(3, chunk, 4 * g, 4, four_series[step][:].rearrange("p y l t -> p (y l t)"))
+
         tiny = keep.tile([P, 1], F32, name="tiny")
         nc.vector.memset(tiny[:], TINY)
 
-        vcopy = nc.vector.tensor_copy
-        scopy = nc.scalar.copy
-        ready_queries(3, 0, four_bank, vcopy)
-        for pair in range(5, 9):
-            ready_keys(pair, 0, four_bank, vcopy)
+        ready_keys(5, 0, vcopy)
+        ready_queries(3, 0, vcopy)
+        for pair in range(6, 9):
+            ready_keys(pair, 0, vcopy)
         for y in range(4):
             four_score(0, y)
         four_copy(0)
         for pair, y in zip(range(5, 9), (1, 2, 3, 4)):
-            ready_keys(pair, 1, late_bank, vcopy)
             if y < 4:
                 raise_top(0, y)
+            ready_keys(pair, 1, vcopy)
         four_score(1, 0)
         four_copy(1)
 
-        def queries(x, half):
-            return lambda: ready_queries(x, half, pair_bank, scopy)
+        def queries(x, half, copy):
+            return lambda: ready_queries(x, half, copy)
 
-        def keys(pair, g):
-            return lambda: ready_keys(pair, g, pair_bank, scopy)
+        def keys(pair, g, copy):
+            return lambda: ready_keys(pair, g, copy)
 
-        def two(step):
-            return lambda: two_sigmoids(step)
+        ahead = []
+        begun = []
+        done = []
 
-        def three(step):
-            return lambda: three_sigmoids(step)
+        def scores_ahead():
+            if len(begun) < len(ahead):
+                begun.append(ahead[len(begun)])
+                begun[-1][0](begun[-1][2])
 
-        def split(step):
-            return lambda: three_split(step)
+        def sigmoids_next():
+            done.append(ahead[len(done)])
+            done[-1][1](done[-1][2])
+            scores_ahead()
+
+        def phase(two_block, three_block):
+            ahead.extend([(two_scores, two_sigmoids, step) for step in steps_of(two_block)])
+            ahead.extend([(three_scores, three_sigmoids, step) for step in steps_of(three_block)])
+
+        def split(chunk):
+            return lambda: three_split(chunk)
 
         def steps_of(block):
             return range(block * STEPS, (block + 1) * STEPS) if 0 <= block < BLOCKS else range(0)
+
+        def chunks_of(block):
+            return range(block * BLOCK_CHUNKS, (block + 1) * BLOCK_CHUNKS) if 0 <= block < BLOCKS else range(0)
 
         def at(block, j):
             return steps_of(block)[j : j + 1] if j >= 0 else ()
 
         def blocks(block):
             return (block,) if 0 <= block < BLOCKS else ()
+
+        def logarithms(block):
+            for chunk in chunks_of(block):
+                three_ln(chunk)
+            four_ln(block)
 
         values_ready = []
 
@@ -382,134 +446,148 @@ def tile_anomalyattention_pa_kernel(tc, q_plus, key_plus, retrieval, out):
 
         next_values()
         flips = [
-            [queries(2, 0), keys(3, 0), keys(4, 0)],
-            [keys(3, 1), keys(4, 1)],
-            [keys(2, 0), keys(2, 1)],
-            [queries(1, 0), keys(0, 0), keys(1, 0)],
+            [queries(2, 0, scopy), keys(3, 0, scopy), keys(4, 0, scopy)],
+            [keys(3, 1, scopy), keys(4, 1, scopy)],
+            [keys(2, 0, scopy), keys(2, 1, scopy)],
+            [],
         ]
         for step in range(STEPS):
-            four_unit(step, flips[step])
-            next_values()
+            four_unit(step, flips[step][:2], flips[step][2:])
+            if step:
+                next_values()
             four_exp(step)
             four_add(step)
 
+        twos_at = {1: 0, 2: 1}
+
         for w in range(BLOCKS):
             long = [step for step in steps_of(w) if is_long(step)]
-            twos = {1: (0,), 2: (1,)}.get(w, ())
-            for block in blocks(w - 1):
-                four_reciprocal(block)
-            for step in steps_of(w - 1):
-                three_guard(step)
-            for block in blocks(w - 2):
-                store(2, block, vcopy)
-            for step in steps_of(w - 1):
+            two_block = twos_at.get(w, -1)
+            z_steps = steps_of(w - 1)
+            due = [(3, b) for b in blocks(w - 2)] + [(2, b) for b in blocks(w - 2)] + [(1, b) for b in blocks(twos_at.get(w - 1, -1))]
+            n_twos = len(steps_of(two_block))
+
+            if w > 1:
+                four_reciprocal(w - 1)
+            for chunk in chunks_of(w - 1):
+                three_guard(chunk)
+            for step in z_steps[0:2]:
                 three_z(step)
+            for step in z_steps[2:4]:
+                three_upper(step)
             for step in steps_of(w) if w else ():
                 four_exp(step)
-            fills = {row: [] for row in range(STEPS)}
-            for j in range(STEPS):
-                fills[1 + j // 2] += [split(step) for step in at(w - 1, j)]
-                for block in twos:
-                    fills[1 + j // 2] += [two(step) for step in at(block, j)]
-                if w:
-                    fills[3] += [three(step) for step in at(w, j)]
+            if w == 1:
+                for i in range(2):
+                    next_values()
+
+            for step in long:
+                long_one(step)
+            phase(two_block, w)
+            if w:
+                splits = [split(chunk) for chunk in chunks_of(w - 1)]
+                n = [sigmoids_next]
+                if n_twos:
+                    fills = [([], []), ([splits[0]] + n * 2 + [splits[1]], []), (n * 3, n), (n * 2, n * 0)]
                 else:
-                    fills[j // 2] += [three(step) for step in at(w, j)]
-            if w == 0:
-                fills[1] += [queries(3, 1)]
-                fills[2] = [keys(0, 1), keys(1, 1)]
-                fills[3] = [queries(2, 1), queries(1, 1)]
+                    fills = [([], []), ([splits[0]], [splits[1]]), (n, n), (n * 2, [])]
+                fills[3] = (fills[3][0] + n * (STEPS + n_twos - sum(a.count(sigmoids_next) + b.count(sigmoids_next) for a, b in fills)), [])
+            else:
+                scores_ahead()
+                scores_ahead()
+                fills = [
+                    ([sigmoids_next, sigmoids_next], [queries(3, 1, scopy)]),
+                    ([sigmoids_next, sigmoids_next], [lambda: three_ln(0), lambda: three_ln(1)]),
+                    ([lambda: four_ln(0), queries(1, 0, scopy)], [keys(0, 0, scopy), keys(1, 0, scopy)]),
+                    ([lambda: four_reciprocal(0), keys(0, 1, scopy)], [keys(1, 1, scopy), queries(2, 1, scopy), queries(1, 1, scopy)]),
+                ]
             for row in range(STEPS):
-                for step in at(w - 1, row - 1):
-                    quantise(3, step, four_series[step])
                 for step in at(w - 1, row):
                     four_multiply(step)
+                if row == 0:
+                    for step in z_steps[2:4]:
+                        three_z(step)
+                else:
+                    for step in at(w - 1, row - 1):
+                        four_quantise(step)
+                    for x, block in due[row - 1 : row]:
+                        store(x, block, vcopy)
                 for step in at(w, row) if w else ():
                     four_add(step)
-                if row == 2 and long:
-                    long_two(long[0])
-                    long_one(long[1])
-                if row == 3 and long:
-                    long_two(long[1])
+                if row == 2:
+                    for step in long:
+                        long_two(step)
                 for step in at(w + 1, row):
-                    four_unit(step, fills[row])
+                    four_unit(step, fills[row][0], fills[row][1])
                 if w + 1 >= BLOCKS:
-                    for job in fills[row]:
+                    for job in fills[row][0] + fills[row][1]:
                         job()
-                if row == 0 and long:
-                    long_one(long[0])
+                for x, block in due[row : row + 1]:
+                    product(x, block)
+                if row == 0 and w:
+                    scores_ahead()
+                    scores_ahead()
                 if w == 0:
                     next_values()
-            for step in steps_of(w):
-                three_ln(step)
-            for block in blocks(w):
-                four_ln(block)
-            if w == 0:
-                next_values()
+            if w:
+                logarithms(w)
+            for step in steps_of(w)[0:2]:
+                three_upper(step)
             for step in at(w - 1, STEPS - 1):
-                quantise(3, step, four_series[step])
-            for block in blocks(w - 1):
-                product(3, block)
-            for j in range(STEPS):
-                for step in at(w - 1, j):
-                    three_multiply(step)
-                for block in twos:
-                    for step in at(block, j):
-                        quantise(1, step, two_series[step])
-                for step in at(w - 1, j - 1):
-                    quantise(2, step, three_series[step])
-                if j == 1:
-                    for block in blocks(w - 1):
-                        store(3, block, vcopy)
-            for step in at(w - 1, STEPS - 1):
-                quantise(2, step, three_series[step])
-            for block in twos:
-                product(1, block)
-                store(1, block, vcopy)
-            for block in blocks(w - 1):
-                product(2, block)
+                four_quantise(step)
+            for j in range(BLOCK_CHUNKS):
+                for chunk in chunks_of(w - 1)[j : j + 1]:
+                    three_multiply(chunk)
+                for chunk in chunks_of(two_block)[j : j + 1]:
+                    two_quantise(chunk)
+                for chunk in chunks_of(w - 1)[j : j + 1]:
+                    three_quantise(chunk)
 
         last = BLOCKS - 1
         four_reciprocal(last)
-        for step in steps_of(last):
-            three_guard(step)
-        store(2, last - 1, vcopy)
-        for step in steps_of(last):
-            three_z(step)
-        for step in steps_of(last):
-            three_split(step)
-        for block in (2, 3):
-            for step in steps_of(block):
-                two_sigmoids(step)
+        for chunk in chunks_of(last):
+            three_guard(chunk)
+        three_z(12)
+        three_z(13)
+        three_upper(14)
+        three_upper(15)
+        phase(2, -1)
+        phase(3, -1)
+        scores_ahead()
+        scores_ahead()
+        three_split(6)
         four_multiply(12)
+        three_z(14)
+        three_z(15)
+        three_split(7)
+        product(3, last - 1)
+        product(2, last - 1)
+        for i in range(STEPS):
+            sigmoids_next()
         four_multiply(13)
-        quantise(3, 12, four_series[12])
-        three_multiply(12)
-        quantise(3, 13, four_series[13])
+        four_quantise(12)
+        store(3, last - 1, vcopy)
+        store(2, last - 1, vcopy)
+        three_multiply(6)
+        four_quantise(13)
         four_multiply(14)
-        quantise(2, 12, three_series[12])
-        three_multiply(13)
-        quantise(3, 14, four_series[14])
-        quantise(1, 8, two_series[8])
+        three_quantise(6)
+        two_quantise(4)
+        for i in range(STEPS):
+            sigmoids_next()
+        three_multiply(7)
+        four_quantise(14)
+        two_quantise(5)
         four_multiply(15)
-        quantise(2, 13, three_series[13])
-        quantise(1, 9, two_series[9])
-        three_multiply(14)
-        quantise(3, 15, four_series[15])
-        product(3, last)
-        quantise(1, 10, two_series[10])
-        quantise(1, 11, two_series[11])
-        three_multiply(15)
-        quantise(2, 14, three_series[14])
-        store(3, last, vcopy)
+        three_quantise(7)
         product(1, 2)
-        quantise(2, 15, three_series[15])
-        store(1, 2, vcopy)
         product(2, last)
-        quantise(1, 12, two_series[12])
-        quantise(1, 13, two_series[13])
+        four_quantise(15)
+        store(1, 2, vcopy)
+        two_quantise(6)
         store(2, last, vcopy)
-        quantise(1, 14, two_series[14])
-        quantise(1, 15, two_series[15])
+        product(3, last)
+        two_quantise(7)
         product(1, 3)
+        store(3, last, vcopy)
         store(1, 3, vcopy)

@@ -60,8 +60,7 @@ def tile_anomalyattention_pa_kernel(tc, q_plus, key_plus, retrieval, out):
         q_raw = work.tile([P, CHUNKS, 3, E], BF16, tag="codes3", bufs=1, name="q_raw", align_bytes=64)
         k_raw = {}
         r_raw = {}
-        k_raw.update(raw("three_series", 2, (5, 6, 7), key_plus))
-        k_raw.update(raw("three_series", 2, (8, 3, 4), key_plus))
+        k_raw.update(raw("three_series", 1, (5, 6, 7, 8, 3, 4), key_plus))
         k_raw.update(raw("codes2", 1, (2, 0, 1), key_plus))
         r_raw.update(raw("four_series", 2, (5, 6), retrieval))
         r_raw.update(raw("four_series", 2, (7, 8), retrieval))
@@ -106,7 +105,7 @@ def tile_anomalyattention_pa_kernel(tc, q_plus, key_plus, retrieval, out):
         grouped = {}
 
         def group_values(pair):
-            grouped[pair] = work.tile([P, PASSES, E, PACK], BF16, tag="grouped", name="grouped", align_bytes=64)
+            grouped[pair] = work.tile([P, PASSES, E, PACK], BF16, tag="grouped", bufs=3, name="grouped", align_bytes=64)
             nc.gpsimd.tensor_scalar(
                 out=grouped[pair][:],
                 in0=r_raw[pair][0].rearrange("p g t e -> p g e t"),
@@ -126,8 +125,14 @@ def tile_anomalyattention_pa_kernel(tc, q_plus, key_plus, retrieval, out):
         def by_query(scores):
             return scores[:].rearrange("p t l -> p l t")
 
+        def place(x, step):
+            if x < 3:
+                return divmod(step, PASSES)
+            block, j = divmod(step, STEPS)
+            return block * BLOCK_CHUNKS + j % BLOCK_CHUNKS, j // BLOCK_CHUNKS
+
         def score(bank, x, step, pairs):
-            c, g = divmod(step, PASSES)
+            c, g = place(x, step)
             for t in range(PACK):
                 for pair in pairs:
                     nc.tensor.matmul(
@@ -140,26 +145,26 @@ def tile_anomalyattention_pa_kernel(tc, q_plus, key_plus, retrieval, out):
 
         packed = {}
 
-        def room_for_codes(x, chunk):
-            key = (x, chunk // BLOCK_CHUNKS)
-            if key not in packed:
-                packed[key] = (
-                    work.tile([P, BLOCK_CHUNKS, PASSES * (x + 1), P], U32, tag="codes%d" % x, bufs=1, name="codes", align_bytes=64),
-                    work.tile([P, BLOCK_CHUNKS, PASSES * (x + 1), P], U8, tag="scales%d" % x, bufs=1, name="scales", align_bytes=64),
+        def room_for_codes(x, block):
+            if (x, block) not in packed:
+                shape = [P, STEPS * (x + 1), P]
+                packed[x, block] = (
+                    work.tile(shape, U32, tag="codes%d" % x, bufs=1, name="codes", align_bytes=64),
+                    work.tile(shape, U8, tag="scales%d" % x, bufs=1, name="scales", align_bytes=64),
                 )
-            return packed[key]
+            return packed[x, block]
 
-        def quantise(x, chunk, at, n, series):
-            codes, scales = room_for_codes(x, chunk)
-            c = chunk % BLOCK_CHUNKS
+        def quantise(x, block, first, n, series):
+            codes, scales = room_for_codes(x, block)
             nc.vector.quantize_mx(
-                out=codes[:, c, at : at + n, :].rearrange("p y l -> p (y l)").bitcast(FP8X4),
-                scales=scales[:, c, at : at + n, :].rearrange("p y l -> p (y l)"),
+                out=codes[:, first : first + n, :].rearrange("p y l -> p (y l)").bitcast(FP8X4),
+                scales=scales[:, first : first + n, :].rearrange("p y l -> p (y l)"),
                 in_=series,
             )
 
-        def row_of(x, g, y):
-            return g * (x + 1) + y if x == 3 else y * PASSES + g
+        def row_of(x, c, g, y):
+            step = c * PASSES + g
+            return step * (x + 1) + y if x == 3 else y * STEPS + step
 
         sums = {}
 
@@ -172,8 +177,8 @@ def tile_anomalyattention_pa_kernel(tc, q_plus, key_plus, retrieval, out):
                 for g, y in terms:
                     nc.tensor.matmul_mx(
                         out=acc[:, c, :],
-                        lhsT=codes[:, c, row_of(x, g, y), :].bitcast(FP8X4),
-                        lhsT_scale=scales[:, c, row_of(x, g, y), :],
+                        lhsT=codes[:, row_of(x, c, g, y), :].bitcast(FP8X4),
+                        lhsT_scale=scales[:, row_of(x, c, g, y), :],
                         rhs=r_codes[:, first_pair(x) + y, g, :].bitcast(FP8X4),
                         rhs_scale=r_scales[:, first_pair(x) + y, g, :],
                         start=((g, y) == terms[0]),
@@ -196,14 +201,14 @@ def tile_anomalyattention_pa_kernel(tc, q_plus, key_plus, retrieval, out):
 
         def two_sigmoids(step):
             difference = differences[1, step]
-            chunk, g = divmod(step, PASSES)
-            if g == 0:
-                two_series[chunk] = work.tile([P, 2, PASSES, P, PACK], BF16, tag="two_series", bufs=2, name="two_series", align_bytes=64)
-            nc.scalar.activation(out=two_series[chunk][:, 0, g, :, :], in_=by_query(difference), func=ACT.Sigmoid, scale=SCALE)
-            nc.scalar.activation(out=two_series[chunk][:, 1, g, :, :], in_=by_query(difference), func=ACT.Sigmoid, scale=-SCALE)
+            block, j = divmod(step, STEPS)
+            if j == 0:
+                two_series[block] = work.tile([P, 2, STEPS, P, PACK], BF16, tag="big", bufs=9, name="two_series", align_bytes=64)
+            nc.scalar.activation(out=two_series[block][:, 0, j, :, :], in_=by_query(difference), func=ACT.Sigmoid, scale=SCALE)
+            nc.scalar.activation(out=two_series[block][:, 1, j, :, :], in_=by_query(difference), func=ACT.Sigmoid, scale=-SCALE)
 
-        def two_quantise(chunk):
-            quantise(1, chunk, 0, 4, two_series[chunk][:].rearrange("p y g l t -> p (y g l t)"))
+        def two_quantise(block):
+            quantise(1, block, 0, 2 * STEPS, two_series[block][:].rearrange("p y j l t -> p (y j l t)"))
 
         lower = {}
         minus_one = {}
@@ -211,8 +216,8 @@ def tile_anomalyattention_pa_kernel(tc, q_plus, key_plus, retrieval, out):
         odds = {}
         three_series = {}
 
-        def two_planes(name):
-            return work.tile([P, PASSES, P, PACK], F32, tag="two_planes", bufs=6, name=name)
+        def planes(name):
+            return work.tile([P, STEPS, P, PACK], F32, tag="planes", bufs=3, name=name)
 
         def is_long(step):
             return step // PASSES == LONG_CHUNK
@@ -220,16 +225,16 @@ def tile_anomalyattention_pa_kernel(tc, q_plus, key_plus, retrieval, out):
         def long_one(step):
             one = bank([P, PACK, P], F32, "one")
             score(one, 2, step, (3,))
-            minus_one[step] = work.tile([P, P, PACK], F32, tag="plane", bufs=6, name="minus_one")
+            minus_one[step] = work.tile([P, P, PACK], F32, tag="plane", bufs=5, name="minus_one")
             nc.scalar.copy(out=minus_one[step][:], in_=by_query(one))
 
         def long_two(step):
             two = bank([P, PACK, P], F32, "two")
             score(two, 2, step, (4,))
-            chunk, g = divmod(step, PASSES)
-            if g == 0:
-                lower[chunk] = two_planes("lower")
-            nc.vector.tensor_tensor(out=lower[chunk][:, g, :, :], in0=by_query(two), in1=minus_one[step][:], op=ALU.add)
+            block, j = divmod(step, STEPS)
+            if j == 0:
+                lower[block] = planes("lower")
+            nc.vector.tensor_tensor(out=lower[block][:, j, :, :], in0=by_query(two), in1=minus_one[step][:], op=ALU.add)
 
         def three_scores(step):
             if not is_long(step):
@@ -237,27 +242,27 @@ def tile_anomalyattention_pa_kernel(tc, q_plus, key_plus, retrieval, out):
                 score(differences[2, step], 2, step, (4, 3))
 
         def three_sigmoids(step):
-            chunk, g = divmod(step, PASSES)
-            if g == 0:
-                halves[chunk] = work.tile([P, 2, PASSES, P, PACK], F32, tag="halves", bufs=4, name="halves")
+            block, j = divmod(step, STEPS)
+            if j == 0:
+                halves[block] = work.tile([P, 2, STEPS, P, PACK], F32, tag="halves", bufs=2, name="halves")
             if is_long(step):
-                source = lower[chunk][:, g, :, :]
+                source = lower[block][:, j, :, :]
             else:
                 source = by_query(differences[2, step])
-                if g == 0:
-                    lower[chunk] = two_planes("lower")
-            nc.scalar.activation(out=halves[chunk][:, 0, g, :, :], in_=source, func=ACT.Sigmoid, scale=-SCALE)
-            nc.scalar.activation(out=halves[chunk][:, 1, g, :, :], in_=source, func=ACT.Sigmoid, scale=SCALE)
+                if j == 0:
+                    lower[block] = planes("lower")
+            nc.scalar.activation(out=halves[block][:, 0, j, :, :], in_=source, func=ACT.Sigmoid, scale=-SCALE)
+            nc.scalar.activation(out=halves[block][:, 1, j, :, :], in_=source, func=ACT.Sigmoid, scale=SCALE)
             if not is_long(step):
-                nc.scalar.copy(out=lower[chunk][:, g, :, :], in_=source)
+                nc.scalar.copy(out=lower[block][:, j, :, :], in_=source)
 
-        def three_ln(chunk):
-            odds[chunk] = two_planes("odds")
-            nc.scalar.activation(out=odds[chunk][:], in_=halves[chunk][:, 0, :, :, :], func=ACT.Ln, bias=tiny[:])
+        def three_ln(block):
+            odds[block] = planes("odds")
+            nc.scalar.activation(out=odds[block][:], in_=halves[block][:, 0, :, :, :], func=ACT.Ln, bias=tiny[:])
 
-        def three_guard(chunk):
+        def three_guard(block):
             nc.vector.scalar_tensor_tensor(
-                out=odds[chunk][:], in0=lower[chunk][:], scalar=-SCALE, in1=odds[chunk][:], op0=ALU.mult, op1=ALU.min
+                out=odds[block][:], in0=lower[block][:], scalar=-SCALE, in1=odds[block][:], op0=ALU.mult, op1=ALU.min
             )
 
         upper = {}
@@ -267,30 +272,34 @@ def tile_anomalyattention_pa_kernel(tc, q_plus, key_plus, retrieval, out):
             score(upper[step], 2, step, (2,) if is_long(step) else (2, 3))
 
         def three_z(step):
-            chunk, g = divmod(step, PASSES)
+            block, j = divmod(step, STEPS)
             source = by_query(upper[step])
             if is_long(step):
                 nc.vector.tensor_tensor(out=minus_one[step][:], in0=source, in1=minus_one[step][:], op=ALU.add)
                 source = minus_one[step][:]
-            here = odds[chunk][:, g, :, :]
+            here = odds[block][:, j, :, :]
             nc.vector.scalar_tensor_tensor(out=here, in0=source, scalar=SCALE, in1=here, op0=ALU.mult, op1=ALU.add)
 
         def three_split(chunk):
-            three_series[chunk] = work.tile([P, 3, PASSES, P, PACK], BF16, tag="three_series", bufs=2, name="three_series", align_bytes=64)
-            nc.scalar.activation(out=three_series[chunk][:, 0, :, :, :], in_=odds[chunk][:], func=ACT.Sigmoid)
-            nc.scalar.activation(out=odds[chunk][:], in_=odds[chunk][:], func=ACT.Sigmoid, scale=-1.0)
+            block, c = divmod(chunk, BLOCK_CHUNKS)
+            if c == 0:
+                three_series[block] = work.tile([P, 3, STEPS, P, PACK], BF16, tag="three_series", bufs=1, name="three_series", align_bytes=64)
+            steps = slice(c * PASSES, (c + 1) * PASSES)
+            z = odds[block][:, steps, :, :]
+            nc.scalar.activation(out=three_series[block][:, 0, steps, :, :], in_=z, func=ACT.Sigmoid)
+            nc.scalar.activation(out=z, in_=z, func=ACT.Sigmoid, scale=-1.0)
 
-        def three_multiply(chunk):
+        def three_multiply(block):
             nc.vector.tensor_tensor(
-                out=three_series[chunk][:, 1:3, :, :, :],
-                in0=halves[chunk][:],
-                in1=odds[chunk][:].unsqueeze(1).to_broadcast([P, 2, PASSES, P, PACK]),
+                out=three_series[block][:, 1:3, :, :, :],
+                in0=halves[block][:],
+                in1=odds[block][:].unsqueeze(1).to_broadcast([P, 2, STEPS, P, PACK]),
                 op=ALU.mult,
             )
 
-        def three_quantise(chunk):
-            quantise(2, chunk, 0, 4, three_series[chunk][:, 0:2, :, :, :].rearrange("p y g l t -> p (y g l t)"))
-            quantise(2, chunk, 4, 2, three_series[chunk][:, 2, :, :, :].rearrange("p g l t -> p (g l t)"))
+        def three_quantise(block):
+            quantise(2, block, 0, 2 * STEPS, three_series[block][:, 0:2, :, :, :].rearrange("p y j l t -> p (y j l t)"))
+            quantise(2, block, 2 * STEPS, STEPS, three_series[block][:, 2, :, :, :].rearrange("p j l t -> p (j l t)"))
 
         banks = {}
         top = {}
@@ -305,7 +314,7 @@ def tile_anomalyattention_pa_kernel(tc, q_plus, key_plus, retrieval, out):
 
         def four_copy(step):
             if step < HEAD_STEPS:
-                top[step] = work.tile([P, P, PACK], F32, tag="plane", bufs=6, name="top")
+                top[step] = work.tile([P, P, PACK], F32, tag="plane", bufs=5, name="top")
                 nc.scalar.copy(out=top[step][:], in_=by_query(banks[step, 0]))
 
         def raise_top(step, y):
@@ -314,7 +323,7 @@ def tile_anomalyattention_pa_kernel(tc, q_plus, key_plus, retrieval, out):
 
         def subtract_top(step, y):
             if y == 0:
-                expo[step] = work.tile([P, 4, P, PACK], F32, tag="expo", bufs=8, name="expo")
+                expo[step] = work.tile([P, 4, P, PACK], F32, tag="big", bufs=9, name="expo", align_bytes=64)
             nc.vector.tensor_tensor(out=expo[step][:, y, :, :], in0=by_query(banks[step, y]), in1=top[step][:], op=ALU.subtract)
 
         def four_unit(step, before=(), after=()):
@@ -349,7 +358,7 @@ def tile_anomalyattention_pa_kernel(tc, q_plus, key_plus, retrieval, out):
         def four_add(step):
             adder = nc.gpsimd if step < HEAD_STEPS - STEPS else nc.vector
             here = den[:, step % STEPS, :, :]
-            half_sum = work.tile([P, P, PACK], F32, tag="plane", bufs=6, name="half_sum")
+            half_sum = work.tile([P, P, PACK], F32, tag="plane", bufs=5, name="half_sum")
             adder.tensor_tensor(out=here, in0=expo[step][:, 0, :, :], in1=expo[step][:, 1, :, :], op=ALU.add)
             adder.tensor_tensor(out=half_sum[:], in0=expo[step][:, 2, :, :], in1=expo[step][:, 3, :, :], op=ALU.add)
             adder.tensor_tensor(out=here, in0=here, in1=half_sum[:], op=ALU.add)
@@ -371,8 +380,9 @@ def tile_anomalyattention_pa_kernel(tc, q_plus, key_plus, retrieval, out):
             )
 
         def four_quantise(step):
-            chunk, g = divmod(step, PASSES)
-            quantise(3, chunk, 4 * g, 4, four_series[step][:].rearrange("p y l t -> p (y l t)"))
+            c, g = place(3, step)
+            block, c = divmod(c, BLOCK_CHUNKS)
+            quantise(3, block, row_of(3, c, g, 0), 4, four_series[step][:].rearrange("p y l t -> p (y l t)"))
 
         tiny = keep.tile([P, 1], F32, name="tiny")
         nc.vector.memset(tiny[:], TINY)
@@ -384,11 +394,9 @@ def tile_anomalyattention_pa_kernel(tc, q_plus, key_plus, retrieval, out):
         for y in range(4):
             four_score(0, y)
         four_copy(0)
-        for pair, y in zip(range(5, 9), (1, 2, 3, 4)):
-            if y < 4:
-                raise_top(0, y)
-            ready_keys(pair, 1, vcopy)
         four_score(1, 0)
+        for y in range(1, 4):
+            raise_top(0, y)
         four_copy(1)
 
         def queries(x, half, copy):
@@ -431,30 +439,34 @@ def tile_anomalyattention_pa_kernel(tc, q_plus, key_plus, retrieval, out):
             return (block,) if 0 <= block < BLOCKS else ()
 
         def logarithms(block):
-            for chunk in chunks_of(block):
-                three_ln(chunk)
+            three_ln(block)
             four_ln(block)
 
-        values_ready = []
+        in_groups = []
+        in_codes = []
+
+        def next_group():
+            if len(in_groups) < PAIRS:
+                in_groups.append(value_order[len(in_groups)])
+                group_values(in_groups[-1])
 
         def next_values():
-            if values_ready:
-                quantise_values(values_ready[-1])
-            if len(values_ready) < PAIRS:
-                values_ready.append(value_order[len(values_ready)])
-                group_values(values_ready[-1])
+            if len(in_codes) < PAIRS:
+                in_codes.append(value_order[len(in_codes)])
+                quantise_values(in_codes[-1])
+                next_group()
 
-        next_values()
+        for i in range(3):
+            next_group()
         flips = [
+            [keys(5, 1, vcopy), keys(6, 1, vcopy), keys(7, 1, vcopy), keys(8, 1, vcopy)],
             [queries(2, 0, scopy), keys(3, 0, scopy), keys(4, 0, scopy)],
             [keys(3, 1, scopy), keys(4, 1, scopy)],
             [keys(2, 0, scopy), keys(2, 1, scopy)],
-            [],
         ]
         for step in range(STEPS):
             four_unit(step, flips[step][:2], flips[step][2:])
-            if step:
-                next_values()
+            next_values()
             four_exp(step)
             four_add(step)
 
@@ -469,8 +481,8 @@ def tile_anomalyattention_pa_kernel(tc, q_plus, key_plus, retrieval, out):
 
             if w > 1:
                 four_reciprocal(w - 1)
-            for chunk in chunks_of(w - 1):
-                three_guard(chunk)
+            for block in blocks(w - 1):
+                three_guard(block)
             for step in z_steps[0:2]:
                 three_z(step)
             for step in z_steps[2:4]:
@@ -478,8 +490,7 @@ def tile_anomalyattention_pa_kernel(tc, q_plus, key_plus, retrieval, out):
             for step in steps_of(w) if w else ():
                 four_exp(step)
             if w == 1:
-                for i in range(2):
-                    next_values()
+                next_values()
 
             for step in long:
                 long_one(step)
@@ -497,7 +508,7 @@ def tile_anomalyattention_pa_kernel(tc, q_plus, key_plus, retrieval, out):
                 scores_ahead()
                 fills = [
                     ([sigmoids_next, sigmoids_next], [queries(3, 1, scopy)]),
-                    ([sigmoids_next, sigmoids_next], [lambda: three_ln(0), lambda: three_ln(1)]),
+                    ([sigmoids_next, sigmoids_next], [lambda: three_ln(0)]),
                     ([lambda: four_ln(0), queries(1, 0, scopy)], [keys(0, 0, scopy), keys(1, 0, scopy)]),
                     ([lambda: four_reciprocal(0), keys(0, 1, scopy)], [keys(1, 1, scopy), queries(2, 1, scopy), queries(1, 1, scopy)]),
                 ]
@@ -535,18 +546,16 @@ def tile_anomalyattention_pa_kernel(tc, q_plus, key_plus, retrieval, out):
                 three_upper(step)
             for step in at(w - 1, STEPS - 1):
                 four_quantise(step)
-            for j in range(BLOCK_CHUNKS):
-                for chunk in chunks_of(w - 1)[j : j + 1]:
-                    three_multiply(chunk)
-                for chunk in chunks_of(two_block)[j : j + 1]:
-                    two_quantise(chunk)
-                for chunk in chunks_of(w - 1)[j : j + 1]:
-                    three_quantise(chunk)
+            for block in blocks(w - 1):
+                three_multiply(block)
+            for block in blocks(two_block):
+                two_quantise(block)
+            for block in blocks(w - 1):
+                three_quantise(block)
 
         last = BLOCKS - 1
         four_reciprocal(last)
-        for chunk in chunks_of(last):
-            three_guard(chunk)
+        three_guard(last)
         three_z(12)
         three_z(13)
         three_upper(14)
@@ -562,32 +571,26 @@ def tile_anomalyattention_pa_kernel(tc, q_plus, key_plus, retrieval, out):
         three_split(7)
         product(3, last - 1)
         product(2, last - 1)
-        for i in range(STEPS):
+        for i in range(2 * STEPS):
             sigmoids_next()
         four_multiply(13)
         four_quantise(12)
-        store(3, last - 1, vcopy)
-        store(2, last - 1, vcopy)
-        three_multiply(6)
-        four_quantise(13)
+        store(3, last - 1, scopy)
+        store(2, last - 1, scopy)
         four_multiply(14)
-        three_quantise(6)
-        two_quantise(4)
-        for i in range(STEPS):
-            sigmoids_next()
-        three_multiply(7)
-        four_quantise(14)
-        two_quantise(5)
+        four_quantise(13)
         four_multiply(15)
-        three_quantise(7)
+        four_quantise(14)
+        two_quantise(2)
         product(1, 2)
-        product(2, last)
+        three_multiply(last)
         four_quantise(15)
-        store(1, 2, vcopy)
-        two_quantise(6)
-        store(2, last, vcopy)
         product(3, last)
-        two_quantise(7)
-        product(1, 3)
+        three_quantise(last)
+        store(1, 2, vcopy)
+        product(2, last)
+        two_quantise(3)
         store(3, last, vcopy)
+        product(1, 3)
+        store(2, last, vcopy)
         store(1, 3, vcopy)

@@ -62,8 +62,7 @@ def tile_anomalyattention_pa_kernel(tc, q_plus, key_plus, retrieval, out):
         r_raw = {}
         k_raw.update(raw("three_series", 1, (5, 6, 7, 8, 3, 4), key_plus))
         k_raw.update(raw("codes2", 1, (2, 0, 1), key_plus))
-        r_raw.update(raw("four_series", 2, (5, 6), retrieval))
-        r_raw.update(raw("four_series", 2, (7, 8), retrieval))
+        r_raw.update(raw("four_series", 1, (5, 6, 7, 8), retrieval))
         load(k_raw, 5)
         nc.sync.dma_start(out=q_raw[:, 0:PACK, :, :], in_=q_view[:, 0:PACK, :, :])
         for pair in (6, 7, 8, 3, 4, 2):
@@ -71,7 +70,7 @@ def tile_anomalyattention_pa_kernel(tc, q_plus, key_plus, retrieval, out):
         nc.sync.dma_start(out=q_raw[:, PACK:CHUNKS, :, :], in_=q_view[:, PACK:CHUNKS, :, :])
         load(k_raw, 0)
         load(k_raw, 1)
-        value_order = (5, 6, 7, 8, 2, 3, 4, 0, 1)
+        value_order = (5, 6, 7, 8, 0, 1, 2, 3, 4)
         for pair in value_order:
             if pair not in r_raw:
                 r_raw.update(raw("r_raw", 2, (pair,), retrieval))
@@ -102,24 +101,31 @@ def tile_anomalyattention_pa_kernel(tc, q_plus, key_plus, retrieval, out):
             else:
                 copy(out=k_t[:, pair, g, :, :], in_=flipped[:])
 
+        value_runs = ((5, 4), (0, 4), (4, 1))
         grouped = {}
 
-        def group_values(pair):
-            grouped[pair] = work.tile([P, PASSES, E, PACK], BF16, tag="grouped", bufs=3, name="grouped", align_bytes=64)
-            nc.gpsimd.tensor_scalar(
-                out=grouped[pair][:],
-                in0=r_raw[pair][0].rearrange("p g t e -> p g e t"),
-                scalar1=1.0,
-                scalar2=0.0,
-                op0=ALU.mult,
-                op1=ALU.add,
-            )
+        def group_values():
+            room = work.tile([P, 8, PASSES, E, PACK], BF16, tag="halves", bufs=2, name="room", align_bytes=64)
+            rest = keep.tile([P, 1, PASSES, E, PACK], BF16, name="rest", align_bytes=64)
+            grouped[5] = room[:, 0:4, :, :, :]
+            grouped[0] = room[:, 4:8, :, :, :]
+            grouped[4] = rest[:]
+            for first, n in value_runs:
+                for i in range(n):
+                    nc.gpsimd.tensor_scalar(
+                        out=grouped[first][:, i, :, :, :],
+                        in0=r_raw[first + i][0].rearrange("p g t e -> p g e t"),
+                        scalar1=1.0,
+                        scalar2=0.0,
+                        op0=ALU.mult,
+                        op1=ALU.add,
+                    )
 
-        def quantise_values(pair):
+        def quantise_values(first, n):
             nc.vector.quantize_mx(
-                out=r_codes[:, pair, :, :].rearrange("p g e -> p (g e)").bitcast(FP8X4),
-                scales=r_scales[:, pair, :, :].rearrange("p g e -> p (g e)"),
-                in_=grouped[pair][:].rearrange("p g e t -> p (g e t)"),
+                out=r_codes[:, first : first + n, :, :].rearrange("p a g e -> p (a g e)").bitcast(FP8X4),
+                scales=r_scales[:, first : first + n, :, :].rearrange("p a g e -> p (a g e)"),
+                in_=grouped[first].rearrange("p a g e t -> p (a g e t)"),
             )
 
         def by_query(scores):
@@ -163,8 +169,7 @@ def tile_anomalyattention_pa_kernel(tc, q_plus, key_plus, retrieval, out):
             )
 
         def row_of(x, c, g, y):
-            step = c * PASSES + g
-            return step * (x + 1) + y if x == 3 else y * STEPS + step
+            return (g * BLOCK_CHUNKS + c) * (x + 1) + y if x == 3 else y * STEPS + c * PASSES + g
 
         sums = {}
 
@@ -203,7 +208,7 @@ def tile_anomalyattention_pa_kernel(tc, q_plus, key_plus, retrieval, out):
             difference = differences[1, step]
             block, j = divmod(step, STEPS)
             if j == 0:
-                two_series[block] = work.tile([P, 2, STEPS, P, PACK], BF16, tag="big", bufs=9, name="two_series", align_bytes=64)
+                two_series[block] = work.tile([P, 2, STEPS, P, PACK], BF16, tag="two_series", bufs=1, name="two_series", align_bytes=64)
             nc.scalar.activation(out=two_series[block][:, 0, j, :, :], in_=by_query(difference), func=ACT.Sigmoid, scale=SCALE)
             nc.scalar.activation(out=two_series[block][:, 1, j, :, :], in_=by_query(difference), func=ACT.Sigmoid, scale=-SCALE)
 
@@ -225,7 +230,7 @@ def tile_anomalyattention_pa_kernel(tc, q_plus, key_plus, retrieval, out):
         def long_one(step):
             one = bank([P, PACK, P], F32, "one")
             score(one, 2, step, (3,))
-            minus_one[step] = work.tile([P, P, PACK], F32, tag="plane", bufs=5, name="minus_one")
+            minus_one[step] = work.tile([P, P, PACK], F32, tag="plane", bufs=3, name="minus_one")
             nc.scalar.copy(out=minus_one[step][:], in_=by_query(one))
 
         def long_two(step):
@@ -244,7 +249,7 @@ def tile_anomalyattention_pa_kernel(tc, q_plus, key_plus, retrieval, out):
         def three_sigmoids(step):
             block, j = divmod(step, STEPS)
             if j == 0:
-                halves[block] = work.tile([P, 2, STEPS, P, PACK], F32, tag="halves", bufs=2, name="halves")
+                halves[block] = work.tile([P, 2, STEPS, P, PACK], F32, tag="halves", bufs=2, name="halves", align_bytes=64)
             if is_long(step):
                 source = lower[block][:, j, :, :]
             else:
@@ -314,7 +319,7 @@ def tile_anomalyattention_pa_kernel(tc, q_plus, key_plus, retrieval, out):
 
         def four_copy(step):
             if step < HEAD_STEPS:
-                top[step] = work.tile([P, P, PACK], F32, tag="plane", bufs=5, name="top")
+                top[step] = work.tile([P, P, PACK], F32, tag="plane", bufs=3, name="top")
                 nc.scalar.copy(out=top[step][:], in_=by_query(banks[step, 0]))
 
         def raise_top(step, y):
@@ -322,9 +327,10 @@ def tile_anomalyattention_pa_kernel(tc, q_plus, key_plus, retrieval, out):
                 nc.vector.tensor_tensor(out=top[step][:], in0=by_query(banks[step, y]), in1=top[step][:], op=ALU.max)
 
         def subtract_top(step, y):
-            if y == 0:
-                expo[step] = work.tile([P, 4, P, PACK], F32, tag="big", bufs=9, name="expo", align_bytes=64)
-            nc.vector.tensor_tensor(out=expo[step][:, y, :, :], in0=by_query(banks[step, y]), in1=top[step][:], op=ALU.subtract)
+            pair, i = divmod(step, 2)
+            if y == 0 and i == 0:
+                expo[pair] = work.tile([P, 2, 4, P, PACK], F32, tag="expo", bufs=4, name="expo")
+            nc.vector.tensor_tensor(out=expo[pair][:, i, y, :, :], in0=by_query(banks[step, y]), in1=top[step][:], op=ALU.subtract)
 
         def four_unit(step, before=(), after=()):
             jobs = list(before)
@@ -352,16 +358,18 @@ def tile_anomalyattention_pa_kernel(tc, q_plus, key_plus, retrieval, out):
             for job in after:
                 job()
 
+        def exponentials(step):
+            return expo[step // 2][:, step % 2, :, :, :]
+
         def four_exp(step):
-            nc.scalar.activation(out=expo[step][:], in_=expo[step][:], func=ACT.Exp, scale=SCALE)
+            nc.scalar.activation(out=exponentials(step), in_=exponentials(step), func=ACT.Exp, scale=SCALE)
 
         def four_add(step):
             adder = nc.gpsimd if step < HEAD_STEPS - STEPS else nc.vector
-            here = den[:, step % STEPS, :, :]
-            half_sum = work.tile([P, P, PACK], F32, tag="plane", bufs=5, name="half_sum")
-            adder.tensor_tensor(out=here, in0=expo[step][:, 0, :, :], in1=expo[step][:, 1, :, :], op=ALU.add)
-            adder.tensor_tensor(out=half_sum[:], in0=expo[step][:, 2, :, :], in1=expo[step][:, 3, :, :], op=ALU.add)
-            adder.tensor_tensor(out=here, in0=here, in1=half_sum[:], op=ALU.add)
+            e = exponentials(step)
+            half_sums = work.tile([P, 2, P, PACK], F32, tag="half_sums", bufs=1, name="half_sums")
+            adder.tensor_tensor(out=half_sums[:], in0=e[:, 0:2, :, :], in1=e[:, 2:4, :, :], op=ALU.add)
+            adder.tensor_tensor(out=den[:, step % STEPS, :, :], in0=half_sums[:, 0, :, :], in1=half_sums[:, 1, :, :], op=ALU.add)
 
         def four_ln(block):
             nc.scalar.activation(out=den[:], in_=den[:], func=ACT.Ln)
@@ -369,20 +377,19 @@ def tile_anomalyattention_pa_kernel(tc, q_plus, key_plus, retrieval, out):
         def four_reciprocal(block):
             nc.scalar.activation(out=den[:], in_=den[:], func=ACT.Exp, scale=-1.0)
 
-        def four_multiply(step):
-            block, j = divmod(step, STEPS)
-            four_series[step] = work.tile([P, 4, P, PACK], BF16, tag="four_series", bufs=2, name="four_series", align_bytes=64)
+        def four_multiply(pair):
+            four_series[pair] = work.tile([P, 2, 4, P, PACK], BF16, tag="four_series", bufs=1, name="four_series", align_bytes=64)
+            first = (2 * pair) % STEPS
             nc.vector.tensor_tensor(
-                out=four_series[step][:],
-                in0=expo[step][:],
-                in1=den[:, j, :, :].unsqueeze(1).to_broadcast([P, 4, P, PACK]),
+                out=four_series[pair][:],
+                in0=expo[pair][:],
+                in1=den[:, first : first + 2, :, :].unsqueeze(2).to_broadcast([P, 2, 4, P, PACK]),
                 op=ALU.mult,
             )
 
-        def four_quantise(step):
-            c, g = place(3, step)
-            block, c = divmod(c, BLOCK_CHUNKS)
-            quantise(3, block, row_of(3, c, g, 0), 4, four_series[step][:].rearrange("p y l t -> p (y l t)"))
+        def four_quantise(pair):
+            block, i = divmod(pair, STEPS // 2)
+            quantise(3, block, 8 * i, 8, four_series[pair][:].rearrange("p i y l t -> p (i y l t)"))
 
         tiny = keep.tile([P, 1], F32, name="tiny")
         nc.vector.memset(tiny[:], TINY)
@@ -442,22 +449,7 @@ def tile_anomalyattention_pa_kernel(tc, q_plus, key_plus, retrieval, out):
             three_ln(block)
             four_ln(block)
 
-        in_groups = []
-        in_codes = []
-
-        def next_group():
-            if len(in_groups) < PAIRS:
-                in_groups.append(value_order[len(in_groups)])
-                group_values(in_groups[-1])
-
-        def next_values():
-            if len(in_codes) < PAIRS:
-                in_codes.append(value_order[len(in_codes)])
-                quantise_values(in_codes[-1])
-                next_group()
-
-        for i in range(3):
-            next_group()
+        group_values()
         flips = [
             [keys(5, 1, vcopy), keys(6, 1, vcopy), keys(7, 1, vcopy), keys(8, 1, vcopy)],
             [queries(2, 0, scopy), keys(3, 0, scopy), keys(4, 0, scopy)],
@@ -466,19 +458,23 @@ def tile_anomalyattention_pa_kernel(tc, q_plus, key_plus, retrieval, out):
         ]
         for step in range(STEPS):
             four_unit(step, flips[step][:2], flips[step][2:])
-            next_values()
             four_exp(step)
             four_add(step)
 
         twos_at = {1: 0, 2: 1}
 
+        def pairs_of(block):
+            return range(2 * block, 2 * block + 2) if 0 <= block < BLOCKS else ()
+
         for w in range(BLOCKS):
             long = [step for step in steps_of(w) if is_long(step)]
             two_block = twos_at.get(w, -1)
             z_steps = steps_of(w - 1)
-            due = [(3, b) for b in blocks(w - 2)] + [(2, b) for b in blocks(w - 2)] + [(1, b) for b in blocks(twos_at.get(w - 1, -1))]
             n_twos = len(steps_of(two_block))
+            n = [sigmoids_next]
 
+            for block in blocks(w - 2):
+                product(3, block)
             if w > 1:
                 four_reciprocal(w - 1)
             for block in blocks(w - 1):
@@ -490,107 +486,108 @@ def tile_anomalyattention_pa_kernel(tc, q_plus, key_plus, retrieval, out):
             for step in steps_of(w) if w else ():
                 four_exp(step)
             if w == 1:
-                next_values()
-
+                for first, count in value_runs:
+                    quantise_values(first, count)
+                for flip_job in (keys(0, 1, vcopy), keys(1, 1, vcopy), queries(2, 1, vcopy), queries(1, 1, vcopy)):
+                    flip_job()
             for step in long:
                 long_one(step)
             phase(two_block, w)
             if w:
                 splits = [split(chunk) for chunk in chunks_of(w - 1)]
-                n = [sigmoids_next]
                 if n_twos:
-                    fills = [([], []), ([splits[0]] + n * 2 + [splits[1]], []), (n * 3, n), (n * 2, n * 0)]
+                    fills = [([], []), ([splits[0]] + n * 2 + [splits[1]], []), (n * 3, n), (n * 2, [])]
                 else:
                     fills = [([], []), ([splits[0]], [splits[1]]), (n, n), (n * 2, [])]
-                fills[3] = (fills[3][0] + n * (STEPS + n_twos - sum(a.count(sigmoids_next) + b.count(sigmoids_next) for a, b in fills)), [])
             else:
                 scores_ahead()
                 scores_ahead()
                 fills = [
-                    ([sigmoids_next, sigmoids_next], [queries(3, 1, scopy)]),
-                    ([sigmoids_next, sigmoids_next], [lambda: three_ln(0)]),
-                    ([lambda: four_ln(0), queries(1, 0, scopy)], [keys(0, 0, scopy), keys(1, 0, scopy)]),
-                    ([lambda: four_reciprocal(0), keys(0, 1, scopy)], [keys(1, 1, scopy), queries(2, 1, scopy), queries(1, 1, scopy)]),
+                    (n * 2, [queries(3, 1, scopy)]),
+                    (n * 2, [lambda: three_ln(0)]),
+                    ([], [lambda: four_ln(0), queries(1, 0, scopy)]),
+                    ([lambda: four_reciprocal(0)], [keys(0, 0, scopy), keys(1, 0, scopy)]),
                 ]
-            for row in range(STEPS):
-                for step in at(w - 1, row):
-                    four_multiply(step)
-                if row == 0:
+            for half in range(2):
+                for pair in pairs_of(w - 1)[half : half + 1]:
+                    four_multiply(pair)
+                if half == 0:
                     for step in z_steps[2:4]:
                         three_z(step)
+                    for block in blocks(w - 2):
+                        store(3, block, vcopy)
                 else:
-                    for step in at(w - 1, row - 1):
-                        four_quantise(step)
-                    for x, block in due[row - 1 : row]:
-                        store(x, block, vcopy)
-                for step in at(w, row) if w else ():
-                    four_add(step)
-                if row == 2:
                     for step in long:
                         long_two(step)
-                for step in at(w + 1, row):
-                    four_unit(step, fills[row][0], fills[row][1])
-                if w + 1 >= BLOCKS:
-                    for job in fills[row][0] + fills[row][1]:
-                        job()
-                for x, block in due[row : row + 1]:
-                    product(x, block)
-                if row == 0 and w:
-                    scores_ahead()
-                    scores_ahead()
-                if w == 0:
-                    next_values()
+                    for block in blocks(w - 2):
+                        store(2, block, vcopy)
+                for step in steps_of(w)[2 * half : 2 * half + 2] if w else ():
+                    four_add(step)
+                for row in (2 * half, 2 * half + 1):
+                    if (w, row) == (0, 3):
+                        three_upper(0)
+                        three_upper(1)
+                    for step in at(w + 1, row):
+                        four_unit(step, fills[row][0], fills[row][1])
+                    if row == 0 and w:
+                        scores_ahead()
+                        scores_ahead()
+                    if w + 1 >= BLOCKS:
+                        for job in fills[row][0] + fills[row][1]:
+                            job()
+                if half == 0:
+                    for block in blocks(w - 2):
+                        product(2, block)
+                else:
+                    for block in blocks(twos_at.get(w - 1, -1)):
+                        product(1, block)
+                for pair in pairs_of(w - 1)[half : half + 1]:
+                    four_quantise(pair)
             if w:
                 logarithms(w)
-            for step in steps_of(w)[0:2]:
+            for step in steps_of(w)[0 : 2 if w + 1 < BLOCKS else STEPS] if w else ():
                 three_upper(step)
-            for step in at(w - 1, STEPS - 1):
-                four_quantise(step)
             for block in blocks(w - 1):
                 three_multiply(block)
+            for block in blocks(twos_at.get(w - 1, -1)):
+                store(1, block, vcopy)
             for block in blocks(two_block):
                 two_quantise(block)
             for block in blocks(w - 1):
                 three_quantise(block)
 
         last = BLOCKS - 1
+        product(3, last - 1)
+        product(2, last - 1)
         four_reciprocal(last)
         three_guard(last)
-        three_z(12)
-        three_z(13)
-        three_upper(14)
-        three_upper(15)
+        for step in steps_of(last):
+            three_z(step)
         phase(2, -1)
         phase(3, -1)
         scores_ahead()
         scores_ahead()
         three_split(6)
-        four_multiply(12)
-        three_z(14)
-        three_z(15)
         three_split(7)
-        product(3, last - 1)
-        product(2, last - 1)
-        for i in range(2 * STEPS):
+        four_multiply(6)
+        for i in range(STEPS):
             sigmoids_next()
-        four_multiply(13)
-        four_quantise(12)
         store(3, last - 1, scopy)
         store(2, last - 1, scopy)
-        four_multiply(14)
-        four_quantise(13)
-        four_multiply(15)
-        four_quantise(14)
+        four_quantise(6)
+        four_multiply(7)
         two_quantise(2)
         product(1, 2)
+        for i in range(STEPS):
+            sigmoids_next()
         three_multiply(last)
-        four_quantise(15)
+        four_quantise(7)
         product(3, last)
         three_quantise(last)
-        store(1, 2, vcopy)
         product(2, last)
-        two_quantise(3)
         store(3, last, vcopy)
-        product(1, 3)
+        store(1, 2, vcopy)
+        two_quantise(3)
         store(2, last, vcopy)
+        product(1, 3)
         store(1, 3, vcopy)

@@ -479,24 +479,22 @@ def tile_anomalyattention_pa_kernel(tc, q_plus, key_plus, retrieval, out):
                 four_reciprocal(w - 1)
             for block in blocks(w - 1):
                 three_guard(block)
+            if w == 1:
+                for run in value_runs:
+                    quantise_values(*run)
             for step in z_steps[0:2]:
                 three_z(step)
             for step in z_steps[2:4]:
                 three_upper(step)
             for step in steps_of(w) if w else ():
                 four_exp(step)
-            if w == 1:
-                for first, count in value_runs:
-                    quantise_values(first, count)
-                for flip_job in (keys(0, 1, vcopy), keys(1, 1, vcopy), queries(2, 1, vcopy), queries(1, 1, vcopy)):
-                    flip_job()
             for step in long:
                 long_one(step)
             phase(two_block, w)
             if w:
                 splits = [split(chunk) for chunk in chunks_of(w - 1)]
                 if n_twos:
-                    fills = [([], []), ([splits[0]] + n * 2 + [splits[1]], []), (n * 3, n), (n * 2, [])]
+                    fills = [([], []), ([splits[0]] + n * 2 + [splits[1]], []), (n * 3, []), (n * 3, [])]
                 else:
                     fills = [([], []), ([splits[0]], [splits[1]]), (n, n), (n * 2, [])]
             else:
@@ -505,8 +503,8 @@ def tile_anomalyattention_pa_kernel(tc, q_plus, key_plus, retrieval, out):
                 fills = [
                     (n * 2, [queries(3, 1, scopy)]),
                     (n * 2, [lambda: three_ln(0)]),
-                    ([], [lambda: four_ln(0), queries(1, 0, scopy)]),
-                    ([lambda: four_reciprocal(0)], [keys(0, 0, scopy), keys(1, 0, scopy)]),
+                    ([], [lambda: four_ln(0)]),
+                    ([lambda: four_reciprocal(0)], [queries(1, 0, scopy), keys(0, 0, scopy), keys(1, 0, scopy), keys(0, 1, scopy), keys(1, 1, scopy), queries(2, 1, scopy), queries(1, 1, scopy)]),
                 ]
             for half in range(2):
                 for pair in pairs_of(w - 1)[half : half + 1]:
@@ -567,11 +565,11 @@ def tile_anomalyattention_pa_kernel(tc, q_plus, key_plus, retrieval, out):
         phase(3, -1)
         scores_ahead()
         scores_ahead()
+        for i in range(STEPS):
+            sigmoids_next()
         three_split(6)
         three_split(7)
         four_multiply(6)
-        for i in range(STEPS):
-            sigmoids_next()
         store(3, last - 1, scopy)
         store(2, last - 1, scopy)
         four_quantise(6)

@@ -309,7 +309,7 @@ def tile_anomalyattention_pa_kernel(tc, q_plus, key_plus, retrieval, out):
         banks = {}
         top = {}
         expo = {}
-        den = keep.tile([P, STEPS, P, PACK], F32, name="den")
+        den = keep.tile([P, STEPS, 2, P, PACK], F32, name="den")
         four_series = {}
 
         def four_score(step, y):
@@ -367,15 +367,15 @@ def tile_anomalyattention_pa_kernel(tc, q_plus, key_plus, retrieval, out):
         def four_add(step):
             adder = nc.gpsimd if step < HEAD_STEPS - STEPS else nc.vector
             e = exponentials(step)
-            half_sums = work.tile([P, 2, P, PACK], F32, tag="half_sums", bufs=1, name="half_sums")
-            adder.tensor_tensor(out=half_sums[:], in0=e[:, 0:2, :, :], in1=e[:, 2:4, :, :], op=ALU.add)
-            adder.tensor_tensor(out=den[:, step % STEPS, :, :], in0=half_sums[:, 0, :, :], in1=half_sums[:, 1, :, :], op=ALU.add)
+            here = den[:, step % STEPS, :, :, :]
+            adder.tensor_tensor(out=here, in0=e[:, 0:2, :, :], in1=e[:, 2:4, :, :], op=ALU.add)
+            adder.tensor_tensor(out=here[:, 0, :, :], in0=here[:, 0, :, :], in1=here[:, 1, :, :], op=ALU.add)
 
         def four_ln(block):
-            nc.scalar.activation(out=den[:], in_=den[:], func=ACT.Ln)
+            nc.scalar.activation(out=den[:, :, 0, :, :], in_=den[:, :, 0, :, :], func=ACT.Ln)
 
         def four_reciprocal(block):
-            nc.scalar.activation(out=den[:], in_=den[:], func=ACT.Exp, scale=-1.0)
+            nc.scalar.activation(out=den[:, :, 0, :, :], in_=den[:, :, 0, :, :], func=ACT.Exp, scale=-1.0)
 
         def four_multiply(pair):
             four_series[pair] = work.tile([P, 2, 4, P, PACK], BF16, tag="four_series", bufs=1, name="four_series", align_bytes=64)
@@ -383,7 +383,7 @@ def tile_anomalyattention_pa_kernel(tc, q_plus, key_plus, retrieval, out):
             nc.vector.tensor_tensor(
                 out=four_series[pair][:],
                 in0=expo[pair][:],
-                in1=den[:, first : first + 2, :, :].unsqueeze(2).to_broadcast([P, 2, 4, P, PACK]),
+                in1=den[:, first : first + 2, 0, :, :].unsqueeze(2).to_broadcast([P, 2, 4, P, PACK]),
                 op=ALU.mult,
             )
 
@@ -512,13 +512,9 @@ def tile_anomalyattention_pa_kernel(tc, q_plus, key_plus, retrieval, out):
                 if half == 0:
                     for step in z_steps[2:4]:
                         three_z(step)
-                    for block in blocks(w - 2):
-                        store(3, block, vcopy)
                 else:
                     for step in long:
                         long_two(step)
-                    for block in blocks(w - 2):
-                        store(2, block, vcopy)
                 for step in steps_of(w)[2 * half : 2 * half + 2] if w else ():
                     four_add(step)
                 for row in (2 * half, 2 * half + 1):
@@ -530,6 +526,12 @@ def tile_anomalyattention_pa_kernel(tc, q_plus, key_plus, retrieval, out):
                     if row == 0 and w:
                         scores_ahead()
                         scores_ahead()
+                    if row == 0:
+                        for block in blocks(w - 2):
+                            store(3, block, scopy)
+                    if row == 2:
+                        for block in blocks(w - 2):
+                            store(2, block, scopy)
                     if w + 1 >= BLOCKS:
                         for job in fills[row][0] + fills[row][1]:
                             job()
@@ -543,12 +545,12 @@ def tile_anomalyattention_pa_kernel(tc, q_plus, key_plus, retrieval, out):
                     four_quantise(pair)
             if w:
                 logarithms(w)
+            for block in blocks(twos_at.get(w - 1, -1)):
+                store(1, block, scopy)
             for step in steps_of(w)[0 : 2 if w + 1 < BLOCKS else STEPS] if w else ():
                 three_upper(step)
             for block in blocks(w - 1):
                 three_multiply(block)
-            for block in blocks(twos_at.get(w - 1, -1)):
-                store(1, block, vcopy)
             for block in blocks(two_block):
                 two_quantise(block)
             for block in blocks(w - 1):

@@ -364,6 +364,9 @@ def tile_anomalyattention_pa_kernel(tc, q_plus, key_plus, retrieval, out):
         def four_exp(step):
             nc.scalar.activation(out=exponentials(step), in_=exponentials(step), func=ACT.Exp, scale=SCALE)
 
+        def four_exp_pair(pair):
+            nc.scalar.activation(out=expo[pair][:], in_=expo[pair][:], func=ACT.Exp, scale=SCALE)
+
         def four_add(step):
             adder = nc.gpsimd if step < HEAD_STEPS - STEPS else nc.vector
             e = exponentials(step)
@@ -451,7 +454,7 @@ def tile_anomalyattention_pa_kernel(tc, q_plus, key_plus, retrieval, out):
 
         group_values()
         flips = [
-            [keys(5, 1, vcopy), keys(6, 1, vcopy), keys(7, 1, vcopy), keys(8, 1, vcopy)],
+            [keys(5, 1, scopy), keys(6, 1, scopy), keys(7, 1, vcopy), keys(8, 1, vcopy)],
             [queries(2, 0, scopy), keys(3, 0, scopy), keys(4, 0, scopy)],
             [keys(3, 1, scopy), keys(4, 1, scopy)],
             [keys(2, 0, scopy), keys(2, 1, scopy)],
@@ -486,8 +489,8 @@ def tile_anomalyattention_pa_kernel(tc, q_plus, key_plus, retrieval, out):
                 three_z(step)
             for step in z_steps[2:4]:
                 three_upper(step)
-            for step in steps_of(w) if w else ():
-                four_exp(step)
+            for pair in pairs_of(w) if w else ():
+                four_exp_pair(pair)
             for step in long:
                 long_one(step)
             phase(two_block, w)
@@ -528,10 +531,10 @@ def tile_anomalyattention_pa_kernel(tc, q_plus, key_plus, retrieval, out):
                         scores_ahead()
                     if row == 0:
                         for block in blocks(w - 2):
-                            store(3, block, scopy)
+                            store(3, block, vcopy if w == 2 else scopy)
                     if row == 2:
                         for block in blocks(w - 2):
-                            store(2, block, scopy)
+                            store(2, block, vcopy if w == 2 else scopy)
                     if w + 1 >= BLOCKS:
                         for job in fills[row][0] + fills[row][1]:
                             job()
@@ -546,7 +549,7 @@ def tile_anomalyattention_pa_kernel(tc, q_plus, key_plus, retrieval, out):
             if w:
                 logarithms(w)
             for block in blocks(twos_at.get(w - 1, -1)):
-                store(1, block, scopy)
+                store(1, block, vcopy if w == 2 else scopy)
             for step in steps_of(w)[0 : 2 if w + 1 < BLOCKS else STEPS] if w else ():
                 three_upper(step)
             for block in blocks(w - 1):
@@ -585,9 +588,9 @@ def tile_anomalyattention_pa_kernel(tc, q_plus, key_plus, retrieval, out):
         product(3, last)
         three_quantise(last)
         product(2, last)
-        store(3, last, vcopy)
-        store(1, 2, vcopy)
+        store(3, last, scopy)
+        store(1, 2, scopy)
         two_quantise(3)
-        store(2, last, vcopy)
+        store(2, last, scopy)
         product(1, 3)
         store(1, 3, vcopy)

@@ -26,6 +26,7 @@ BLOCK_CHUNKS = 2
 STEPS = BLOCK_CHUNKS * PASSES
 HEAD_STEPS = CHUNKS * PASSES
 BLOCKS = HEAD_STEPS // STEPS
+COUPLE = 2
 LONG_CHUNK = 6
 
 FLOPS = 2 * 2 * PAIRS * L * L * E
@@ -37,6 +38,8 @@ def first_pair(x):
 
 def tile_anomalyattention_pa_kernel(tc, q_plus, key_plus, retrieval, out):
     nc = tc.nc
+    vcopy = nc.vector.tensor_copy
+    scopy = nc.scalar.copy
     q_view = q_plus[0].rearrange("(p c) x e -> p c x e", c=CHUNKS)
     out_view = out[0].rearrange("(p c) x e -> p c x e", c=CHUNKS)
 
@@ -49,20 +52,24 @@ def tile_anomalyattention_pa_kernel(tc, q_plus, key_plus, retrieval, out):
         k_t = keep.tile([P, PAIRS, PASSES, PACK, P], BF16, name="k_t")
         r_codes = keep.tile([P, PAIRS, PASSES, E], U32, name="r_codes", align_bytes=64)
         r_scales = keep.tile([P, PAIRS, PASSES, E], U8, name="r_scales", align_bytes=64)
+        den = keep.tile([P, STEPS, 2, P, PACK], F32, name="den")
+        tiny = keep.tile([P, 1], F32, name="tiny")
+        nc.vector.memset(tiny[:], TINY)
 
         def raw(tag, bufs, pairs, source):
             room = work.tile([P, len(pairs), PASSES, PACK, E], BF16, tag=tag, bufs=bufs, name="raw", align_bytes=64)
-            return {pair: (room[:, i, :, :, :], source[0, pair].rearrange("(g p t) e -> p g t e", g=PASSES, t=PACK)) for i, pair in enumerate(pairs)}
+            return {
+                pair: (room[:, i, :, :, :], source[0, pair].rearrange("(g p t) e -> p g t e", g=PASSES, t=PACK))
+                for i, pair in enumerate(pairs)
+            }
 
         def load(raws, pair):
             nc.sync.dma_start(out=raws[pair][0], in_=raws[pair][1])
 
         q_raw = work.tile([P, CHUNKS, 3, E], BF16, tag="codes3", bufs=1, name="q_raw", align_bytes=64)
-        k_raw = {}
-        r_raw = {}
-        k_raw.update(raw("three_series", 1, (5, 6, 7, 8, 3, 4), key_plus))
+        k_raw = raw("three_series", 1, (5, 6, 7, 8, 3, 4), key_plus)
         k_raw.update(raw("codes2", 1, (2, 0, 1), key_plus))
-        r_raw.update(raw("four_series", 1, (5, 6, 7, 8), retrieval))
+        r_raw = raw("four_series", 1, (5, 6, 7, 8), retrieval)
         load(k_raw, 5)
         nc.sync.dma_start(out=q_raw[:, 0:PACK, :, :], in_=q_view[:, 0:PACK, :, :])
         for pair in (6, 7, 8, 3, 4, 2):
@@ -70,17 +77,13 @@ def tile_anomalyattention_pa_kernel(tc, q_plus, key_plus, retrieval, out):
         nc.sync.dma_start(out=q_raw[:, PACK:CHUNKS, :, :], in_=q_view[:, PACK:CHUNKS, :, :])
         load(k_raw, 0)
         load(k_raw, 1)
-        value_order = (5, 6, 7, 8, 0, 1, 2, 3, 4)
-        for pair in value_order:
+        for pair in (5, 6, 7, 8, 0, 1, 2, 3, 4):
             if pair not in r_raw:
                 r_raw.update(raw("r_raw", 2, (pair,), retrieval))
             load(r_raw, pair)
 
         def bank(shape, dtype, name):
             return psum.tile(shape, dtype, tag="bank", bufs=8, name=name)
-
-        vcopy = nc.vector.tensor_copy
-        scopy = nc.scalar.copy
 
         def flip(sources):
             flipped = bank([P, PACK, P], BF16, "flipped")
@@ -89,14 +92,13 @@ def tile_anomalyattention_pa_kernel(tc, q_plus, key_plus, retrieval, out):
             return flipped
 
         def ready_queries(x, half, copy):
-            flipped = flip([q_raw[:, c, x - 1, :] for c in range(half * PACK, (half + 1) * PACK)])
-            copy(out=q_t[:, x - 1, half * PACK : (half + 1) * PACK, :], in_=flipped[:])
+            chunks = range(half * PACK, (half + 1) * PACK)
+            flipped = flip([q_raw[:, c, x - 1, :] for c in chunks])
+            copy(out=q_t[:, x - 1, chunks[0] : chunks[-1] + 1, :], in_=flipped[:])
 
         def ready_keys(pair, g, copy):
             flipped = flip([k_raw[pair][0][:, g, t, :] for t in range(PACK)])
-            if pair in NEGATED_PAIRS and copy is vcopy:
-                nc.vector.tensor_scalar_mul(out=k_t[:, pair, g, :, :], in0=flipped[:], scalar1=-1.0)
-            elif pair in NEGATED_PAIRS:
+            if pair in NEGATED_PAIRS:
                 nc.scalar.activation(out=k_t[:, pair, g, :, :], in_=flipped[:], func=ACT.Copy, scale=-1.0)
             else:
                 copy(out=k_t[:, pair, g, :, :], in_=flipped[:])
@@ -121,47 +123,47 @@ def tile_anomalyattention_pa_kernel(tc, q_plus, key_plus, retrieval, out):
                         op1=ALU.add,
                     )
 
-        def quantise_values(first, n):
-            nc.vector.quantize_mx(
-                out=r_codes[:, first : first + n, :, :].rearrange("p a g e -> p (a g e)").bitcast(FP8X4),
-                scales=r_scales[:, first : first + n, :, :].rearrange("p a g e -> p (a g e)"),
-                in_=grouped[first].rearrange("p a g e t -> p (a g e t)"),
-            )
+        def quantise_values():
+            for first, n in value_runs:
+                nc.vector.quantize_mx(
+                    out=r_codes[:, first : first + n, :, :].rearrange("p a g e -> p (a g e)").bitcast(FP8X4),
+                    scales=r_scales[:, first : first + n, :, :].rearrange("p a g e -> p (a g e)"),
+                    in_=grouped[first].rearrange("p a g e t -> p (a g e t)"),
+                )
 
         def by_query(scores):
             return scores[:].rearrange("p t l -> p l t")
 
-        def place(x, step):
+        def chunk_and_pass(x, step):
             if x < 3:
                 return divmod(step, PASSES)
             block, j = divmod(step, STEPS)
             return block * BLOCK_CHUNKS + j % BLOCK_CHUNKS, j // BLOCK_CHUNKS
 
-        def score(bank, x, step, pairs):
-            c, g = place(x, step)
+        def score(x, step, pairs, name):
+            c, g = chunk_and_pass(x, step)
+            scores = bank([P, PACK, P], F32, name)
             for t in range(PACK):
                 for pair in pairs:
                     nc.tensor.matmul(
-                        bank[:, t, :],
+                        scores[:, t, :],
                         lhsT=k_t[:, pair, g, t, :],
                         rhs=q_t[:, x - 1, c, :],
                         start=(pair == pairs[0]),
                         stop=(pair == pairs[-1]),
                     )
+            return scores
 
         packed = {}
 
-        def room_for_codes(x, block):
+        def quantise(x, block, first, n, series):
             if (x, block) not in packed:
                 shape = [P, STEPS * (x + 1), P]
                 packed[x, block] = (
                     work.tile(shape, U32, tag="codes%d" % x, bufs=1, name="codes", align_bytes=64),
                     work.tile(shape, U8, tag="scales%d" % x, bufs=1, name="scales", align_bytes=64),
                 )
-            return packed[x, block]
-
-        def quantise(x, block, first, n, series):
-            codes, scales = room_for_codes(x, block)
+            codes, scales = packed[x, block]
             nc.vector.quantize_mx(
                 out=codes[:, first : first + n, :].rearrange("p y l -> p (y l)").bitcast(FP8X4),
                 scales=scales[:, first : first + n, :].rearrange("p y l -> p (y l)"),
@@ -175,13 +177,12 @@ def tile_anomalyattention_pa_kernel(tc, q_plus, key_plus, retrieval, out):
 
         def product(x, block):
             codes, scales = packed[x, block]
-            acc = bank([P, BLOCK_CHUNKS, E], F32, "acc")
-            sums[x] = acc
+            sums[x, block] = bank([P, BLOCK_CHUNKS, E], F32, "sums")
             terms = [(g, y) for g in range(PASSES) for y in range(x + 1)]
             for c in range(BLOCK_CHUNKS):
                 for g, y in terms:
                     nc.tensor.matmul_mx(
-                        out=acc[:, c, :],
+                        out=sums[x, block][:, c, :],
                         lhsT=codes[:, row_of(x, c, g, y), :].bitcast(FP8X4),
                         lhsT_scale=scales[:, row_of(x, c, g, y), :],
                         rhs=r_codes[:, first_pair(x) + y, g, :].bitcast(FP8X4),
@@ -192,33 +193,34 @@ def tile_anomalyattention_pa_kernel(tc, q_plus, key_plus, retrieval, out):
 
         def store(x, block, copy):
             result = work.tile([P, BLOCK_CHUNKS, E], F32, name="result")
-            copy(out=result[:], in_=sums[x][:])
+            copy(out=result[:], in_=sums[x, block][:])
             chunks = slice(block * BLOCK_CHUNKS, (block + 1) * BLOCK_CHUNKS)
             nc.sync.dma_start(out=out_view[:, chunks, x - 1, :], in_=result[:])
 
+        differences = {}
         two_series = {}
 
-        differences = {}
-
         def two_scores(step):
-            differences[1, step] = bank([P, PACK, P], F32, "difference")
-            score(differences[1, step], 1, step, (0, 1))
+            differences[1, step] = score(1, step, (0, 1), "difference")
 
         def two_sigmoids(step):
-            difference = differences[1, step]
+            source = by_query(differences[1, step])
             block, j = divmod(step, STEPS)
             if j == 0:
-                two_series[block] = work.tile([P, 2, STEPS, P, PACK], BF16, tag="two_series", bufs=1, name="two_series", align_bytes=64)
-            nc.scalar.activation(out=two_series[block][:, 0, j, :, :], in_=by_query(difference), func=ACT.Sigmoid, scale=SCALE)
-            nc.scalar.activation(out=two_series[block][:, 1, j, :, :], in_=by_query(difference), func=ACT.Sigmoid, scale=-SCALE)
+                two_series[block] = work.tile(
+                    [P, 2, STEPS, P, PACK], BF16, tag="two_series", bufs=1, name="two_series", align_bytes=64
+                )
+            nc.scalar.activation(out=two_series[block][:, 0, j, :, :], in_=source, func=ACT.Sigmoid, scale=SCALE)
+            nc.scalar.activation(out=two_series[block][:, 1, j, :, :], in_=source, func=ACT.Sigmoid, scale=-SCALE)
 
         def two_quantise(block):
             quantise(1, block, 0, 2 * STEPS, two_series[block][:].rearrange("p y j l t -> p (y j l t)"))
 
         lower = {}
-        minus_one = {}
         halves = {}
         odds = {}
+        upper = {}
+        minus_one = {}
         three_series = {}
 
         def planes(name):
@@ -228,28 +230,29 @@ def tile_anomalyattention_pa_kernel(tc, q_plus, key_plus, retrieval, out):
             return step // PASSES == LONG_CHUNK
 
         def long_one(step):
-            one = bank([P, PACK, P], F32, "one")
-            score(one, 2, step, (3,))
+            one = score(2, step, (3,), "one")
             minus_one[step] = work.tile([P, P, PACK], F32, tag="plane", bufs=3, name="minus_one")
             nc.scalar.copy(out=minus_one[step][:], in_=by_query(one))
 
         def long_two(step):
-            two = bank([P, PACK, P], F32, "two")
-            score(two, 2, step, (4,))
+            two = score(2, step, (4,), "two")
             block, j = divmod(step, STEPS)
             if j == 0:
                 lower[block] = planes("lower")
-            nc.vector.tensor_tensor(out=lower[block][:, j, :, :], in0=by_query(two), in1=minus_one[step][:], op=ALU.add)
+            nc.vector.tensor_tensor(
+                out=lower[block][:, j, :, :], in0=by_query(two), in1=minus_one[step][:], op=ALU.add
+            )
 
         def three_scores(step):
             if not is_long(step):
-                differences[2, step] = bank([P, PACK, P], F32, "difference")
-                score(differences[2, step], 2, step, (4, 3))
+                differences[2, step] = score(2, step, (4, 3), "difference")
 
         def three_sigmoids(step):
             block, j = divmod(step, STEPS)
             if j == 0:
-                halves[block] = work.tile([P, 2, STEPS, P, PACK], F32, tag="halves", bufs=2, name="halves", align_bytes=64)
+                halves[block] = work.tile(
+                    [P, 2, STEPS, P, PACK], F32, tag="halves", bufs=2, name="halves", align_bytes=64
+                )
             if is_long(step):
                 source = lower[block][:, j, :, :]
             else:
@@ -270,11 +273,8 @@ def tile_anomalyattention_pa_kernel(tc, q_plus, key_plus, retrieval, out):
                 out=odds[block][:], in0=lower[block][:], scalar=-SCALE, in1=odds[block][:], op0=ALU.mult, op1=ALU.min
             )
 
-        upper = {}
-
         def three_upper(step):
-            upper[step] = bank([P, PACK, P], F32, "upper")
-            score(upper[step], 2, step, (2,) if is_long(step) else (2, 3))
+            upper[step] = score(2, step, (2,) if is_long(step) else (2, 3), "upper")
 
         def three_z(step):
             block, j = divmod(step, STEPS)
@@ -288,7 +288,9 @@ def tile_anomalyattention_pa_kernel(tc, q_plus, key_plus, retrieval, out):
         def three_split(chunk):
             block, c = divmod(chunk, BLOCK_CHUNKS)
             if c == 0:
-                three_series[block] = work.tile([P, 3, STEPS, P, PACK], BF16, tag="three_series", bufs=1, name="three_series", align_bytes=64)
+                three_series[block] = work.tile(
+                    [P, 3, STEPS, P, PACK], BF16, tag="three_series", bufs=1, name="three_series", align_bytes=64
+                )
             steps = slice(c * PASSES, (c + 1) * PASSES)
             z = odds[block][:, steps, :, :]
             nc.scalar.activation(out=three_series[block][:, 0, steps, :, :], in_=z, func=ACT.Sigmoid)
@@ -303,34 +305,37 @@ def tile_anomalyattention_pa_kernel(tc, q_plus, key_plus, retrieval, out):
             )
 
         def three_quantise(block):
-            quantise(2, block, 0, 2 * STEPS, three_series[block][:, 0:2, :, :, :].rearrange("p y j l t -> p (y j l t)"))
-            quantise(2, block, 2 * STEPS, STEPS, three_series[block][:, 2, :, :, :].rearrange("p j l t -> p (j l t)"))
+            series = three_series[block]
+            quantise(2, block, 0, 2 * STEPS, series[:, 0:2, :, :, :].rearrange("p y j l t -> p (y j l t)"))
+            quantise(2, block, 2 * STEPS, STEPS, series[:, 2, :, :, :].rearrange("p j l t -> p (j l t)"))
 
-        banks = {}
+        scores_of = {}
         top = {}
         expo = {}
-        den = keep.tile([P, STEPS, 2, P, PACK], F32, name="den")
         four_series = {}
 
         def four_score(step, y):
             if step < HEAD_STEPS:
-                banks[step, y] = bank([P, PACK, P], F32, "scores")
-                score(banks[step, y], 3, step, (first_pair(3) + y,))
+                scores_of[step, y] = score(3, step, (first_pair(3) + y,), "scores")
 
         def four_copy(step):
             if step < HEAD_STEPS:
                 top[step] = work.tile([P, P, PACK], F32, tag="plane", bufs=3, name="top")
-                nc.scalar.copy(out=top[step][:], in_=by_query(banks[step, 0]))
+                nc.scalar.copy(out=top[step][:], in_=by_query(scores_of[step, 0]))
 
         def raise_top(step, y):
             if step < HEAD_STEPS:
-                nc.vector.tensor_tensor(out=top[step][:], in0=by_query(banks[step, y]), in1=top[step][:], op=ALU.max)
+                nc.vector.tensor_tensor(
+                    out=top[step][:], in0=by_query(scores_of[step, y]), in1=top[step][:], op=ALU.max
+                )
 
         def subtract_top(step, y):
-            pair, i = divmod(step, 2)
+            couple, i = divmod(step, COUPLE)
             if y == 0 and i == 0:
-                expo[pair] = work.tile([P, 2, 4, P, PACK], F32, tag="expo", bufs=4, name="expo")
-            nc.vector.tensor_tensor(out=expo[pair][:, i, y, :, :], in0=by_query(banks[step, y]), in1=top[step][:], op=ALU.subtract)
+                expo[couple] = work.tile([P, COUPLE, 4, P, PACK], F32, tag="expo", bufs=4, name="expo")
+            nc.vector.tensor_tensor(
+                out=expo[couple][:, i, y, :, :], in0=by_query(scores_of[step, y]), in1=top[step][:], op=ALU.subtract
+            )
 
         def four_unit(step, before=(), after=()):
             jobs = list(before)
@@ -355,51 +360,86 @@ def tile_anomalyattention_pa_kernel(tc, q_plus, key_plus, retrieval, out):
             four_copy(step + 2)
             raise_top(step + 1, 3)
             subtract_top(step, 3)
-            for job in after:
-                job()
+            for one in after:
+                one()
+
+        def four_exp(these):
+            nc.scalar.activation(out=these, in_=these, func=ACT.Exp, scale=SCALE)
 
         def exponentials(step):
-            return expo[step // 2][:, step % 2, :, :, :]
+            couple, i = divmod(step, COUPLE)
+            return expo[couple][:, i, :, :, :]
 
-        def four_exp(step):
-            nc.scalar.activation(out=exponentials(step), in_=exponentials(step), func=ACT.Exp, scale=SCALE)
+        def four_add(couple):
+            adder = nc.gpsimd if couple < couples_of(BLOCKS - 1)[0] else nc.vector
+            e = expo[couple]
+            first = COUPLE * couple % STEPS
+            here = den[:, first : first + COUPLE, :, :, :]
+            adder.tensor_tensor(out=here, in0=e[:, :, 0:2, :, :], in1=e[:, :, 2:4, :, :], op=ALU.add)
+            adder.tensor_tensor(
+                out=here[:, :, 0, :, :], in0=here[:, :, 0, :, :], in1=here[:, :, 1, :, :], op=ALU.add
+            )
 
-        def four_exp_pair(pair):
-            nc.scalar.activation(out=expo[pair][:], in_=expo[pair][:], func=ACT.Exp, scale=SCALE)
-
-        def four_add(step):
-            adder = nc.gpsimd if step < HEAD_STEPS - STEPS else nc.vector
-            e = exponentials(step)
-            here = den[:, step % STEPS, :, :, :]
-            adder.tensor_tensor(out=here, in0=e[:, 0:2, :, :], in1=e[:, 2:4, :, :], op=ALU.add)
-            adder.tensor_tensor(out=here[:, 0, :, :], in0=here[:, 0, :, :], in1=here[:, 1, :, :], op=ALU.add)
-
-        def four_ln(block):
+        def four_ln():
             nc.scalar.activation(out=den[:, :, 0, :, :], in_=den[:, :, 0, :, :], func=ACT.Ln)
 
-        def four_reciprocal(block):
+        def four_reciprocal():
             nc.scalar.activation(out=den[:, :, 0, :, :], in_=den[:, :, 0, :, :], func=ACT.Exp, scale=-1.0)
 
-        def four_multiply(pair):
-            four_series[pair] = work.tile([P, 2, 4, P, PACK], BF16, tag="four_series", bufs=1, name="four_series", align_bytes=64)
-            first = (2 * pair) % STEPS
+        def four_multiply(couple):
+            four_series[couple] = work.tile(
+                [P, COUPLE, 4, P, PACK], BF16, tag="four_series", bufs=1, name="four_series", align_bytes=64
+            )
+            first = COUPLE * couple % STEPS
             nc.vector.tensor_tensor(
-                out=four_series[pair][:],
-                in0=expo[pair][:],
-                in1=den[:, first : first + 2, 0, :, :].unsqueeze(2).to_broadcast([P, 2, 4, P, PACK]),
+                out=four_series[couple][:],
+                in0=expo[couple][:],
+                in1=den[:, first : first + COUPLE, 0, :, :].unsqueeze(2).to_broadcast([P, COUPLE, 4, P, PACK]),
                 op=ALU.mult,
             )
 
-        def four_quantise(pair):
-            block, i = divmod(pair, STEPS // 2)
-            quantise(3, block, 8 * i, 8, four_series[pair][:].rearrange("p i y l t -> p (i y l t)"))
+        def four_quantise(couple):
+            block, i = divmod(couple, STEPS // COUPLE)
+            rows = COUPLE * 4
+            quantise(3, block, rows * i, rows, four_series[couple][:].rearrange("p i y l t -> p (i y l t)"))
 
-        tiny = keep.tile([P, 1], F32, name="tiny")
-        nc.vector.memset(tiny[:], TINY)
+        def job(function, *arguments):
+            return lambda: function(*arguments)
+
+        def steps_of(block):
+            return range(block * STEPS, (block + 1) * STEPS)
+
+        def chunks_of(block):
+            return range(block * BLOCK_CHUNKS, (block + 1) * BLOCK_CHUNKS)
+
+        def couples_of(block):
+            return range(block * STEPS // COUPLE, (block + 1) * STEPS // COUPLE)
+
+        items = []
+        asked = []
+        done = []
+
+        def scores_ahead():
+            if len(asked) < len(items):
+                asked.append(items[len(asked)])
+                scores, _, step = asked[-1]
+                scores(step)
+
+        def sigmoids_next():
+            done.append(items[len(done)])
+            _, sigmoids, step = done[-1]
+            sigmoids(step)
+            scores_ahead()
+
+        def open_phase(two_blocks, three_blocks):
+            for block in two_blocks:
+                items.extend([(two_scores, two_sigmoids, step) for step in steps_of(block)])
+            for block in three_blocks:
+                items.extend([(three_scores, three_sigmoids, step) for step in steps_of(block)])
 
         ready_keys(5, 0, vcopy)
         ready_queries(3, 0, vcopy)
-        for pair in range(6, 9):
+        for pair in (6, 7, 8):
             ready_keys(pair, 0, vcopy)
         for y in range(4):
             four_score(0, y)
@@ -408,189 +448,147 @@ def tile_anomalyattention_pa_kernel(tc, q_plus, key_plus, retrieval, out):
         for y in range(1, 4):
             raise_top(0, y)
         four_copy(1)
-
-        def queries(x, half, copy):
-            return lambda: ready_queries(x, half, copy)
-
-        def keys(pair, g, copy):
-            return lambda: ready_keys(pair, g, copy)
-
-        ahead = []
-        begun = []
-        done = []
-
-        def scores_ahead():
-            if len(begun) < len(ahead):
-                begun.append(ahead[len(begun)])
-                begun[-1][0](begun[-1][2])
-
-        def sigmoids_next():
-            done.append(ahead[len(done)])
-            done[-1][1](done[-1][2])
-            scores_ahead()
-
-        def phase(two_block, three_block):
-            ahead.extend([(two_scores, two_sigmoids, step) for step in steps_of(two_block)])
-            ahead.extend([(three_scores, three_sigmoids, step) for step in steps_of(three_block)])
-
-        def split(chunk):
-            return lambda: three_split(chunk)
-
-        def steps_of(block):
-            return range(block * STEPS, (block + 1) * STEPS) if 0 <= block < BLOCKS else range(0)
-
-        def chunks_of(block):
-            return range(block * BLOCK_CHUNKS, (block + 1) * BLOCK_CHUNKS) if 0 <= block < BLOCKS else range(0)
-
-        def at(block, j):
-            return steps_of(block)[j : j + 1] if j >= 0 else ()
-
-        def blocks(block):
-            return (block,) if 0 <= block < BLOCKS else ()
-
-        def logarithms(block):
-            three_ln(block)
-            four_ln(block)
-
         group_values()
         flips = [
-            [keys(5, 1, scopy), keys(6, 1, scopy), keys(7, 1, vcopy), keys(8, 1, vcopy)],
-            [queries(2, 0, scopy), keys(3, 0, scopy), keys(4, 0, scopy)],
-            [keys(3, 1, scopy), keys(4, 1, scopy)],
-            [keys(2, 0, scopy), keys(2, 1, scopy)],
+            [
+                job(ready_keys, 5, 1, scopy),
+                job(ready_keys, 6, 1, scopy),
+                job(ready_keys, 7, 1, vcopy),
+                job(ready_keys, 8, 1, vcopy),
+            ],
+            [job(ready_queries, 2, 0, scopy), job(ready_keys, 3, 0, scopy), job(ready_keys, 4, 0, scopy)],
+            [job(ready_keys, 3, 1, scopy), job(ready_keys, 4, 1, scopy)],
+            [job(ready_keys, 2, 0, scopy), job(ready_keys, 2, 1, scopy)],
         ]
-        for step in range(STEPS):
+        for step in steps_of(0):
             four_unit(step, flips[step][:2], flips[step][2:])
-            four_exp(step)
-            four_add(step)
+            four_exp(exponentials(step))
+            if step % COUPLE == COUPLE - 1:
+                four_add(step // COUPLE)
 
-        twos_at = {1: 0, 2: 1}
+        open_phase((), (0,))
+        scores_ahead()
+        scores_ahead()
+        four_unit(4, [sigmoids_next, sigmoids_next], [job(ready_queries, 3, 1, scopy)])
+        four_unit(5, [sigmoids_next, sigmoids_next], [job(three_ln, 0)])
+        four_unit(6, [], [four_ln])
+        three_upper(0)
+        three_upper(1)
+        four_unit(
+            7,
+            [four_reciprocal],
+            [
+                job(ready_queries, 1, 0, scopy),
+                job(ready_keys, 0, 0, scopy),
+                job(ready_keys, 1, 0, scopy),
+                job(ready_keys, 0, 1, scopy),
+                job(ready_keys, 1, 1, scopy),
+                job(ready_queries, 2, 1, scopy),
+                job(ready_queries, 1, 1, scopy),
+            ],
+        )
 
-        def pairs_of(block):
-            return range(2 * block, 2 * block + 2) if 0 <= block < BLOCKS else ()
-
-        for w in range(BLOCKS):
-            long = [step for step in steps_of(w) if is_long(step)]
-            two_block = twos_at.get(w, -1)
+        two_at = {1: (0,), 2: (1,), 3: ()}
+        for w in range(1, BLOCKS):
+            copy = vcopy if w == 2 else scopy
+            finished = [w - 2] if w > 1 else []
+            long_steps = [step for step in steps_of(w) if is_long(step)]
             z_steps = steps_of(w - 1)
-            n_twos = len(steps_of(two_block))
-            n = [sigmoids_next]
 
-            for block in blocks(w - 2):
+            for block in finished:
                 product(3, block)
-            if w > 1:
-                four_reciprocal(w - 1)
-            for block in blocks(w - 1):
-                three_guard(block)
+                four_reciprocal()
+            three_guard(w - 1)
             if w == 1:
-                for run in value_runs:
-                    quantise_values(*run)
-            for step in z_steps[0:2]:
+                quantise_values()
+            for step in z_steps[:2]:
                 three_z(step)
-            for step in z_steps[2:4]:
+            for step in z_steps[2:]:
                 three_upper(step)
-            for pair in pairs_of(w) if w else ():
-                four_exp_pair(pair)
-            for step in long:
+            for couple in couples_of(w):
+                four_exp(expo[couple][:])
+            for step in long_steps:
                 long_one(step)
-            phase(two_block, w)
-            if w:
-                splits = [split(chunk) for chunk in chunks_of(w - 1)]
-                if n_twos:
-                    fills = [([], []), ([splits[0]] + n * 2 + [splits[1]], []), (n * 3, []), (n * 3, [])]
-                else:
-                    fills = [([], []), ([splits[0]], [splits[1]]), (n, n), (n * 2, [])]
+
+            open_phase(two_at[w], (w,))
+            first_split, last_split = [job(three_split, chunk) for chunk in chunks_of(w - 1)]
+            if two_at[w]:
+                jobs = [[], [first_split, sigmoids_next, sigmoids_next, last_split], [sigmoids_next] * 3, [sigmoids_next] * 3]
             else:
-                scores_ahead()
-                scores_ahead()
-                fills = [
-                    (n * 2, [queries(3, 1, scopy)]),
-                    (n * 2, [lambda: three_ln(0)]),
-                    ([], [lambda: four_ln(0)]),
-                    ([lambda: four_reciprocal(0)], [queries(1, 0, scopy), keys(0, 0, scopy), keys(1, 0, scopy), keys(0, 1, scopy), keys(1, 1, scopy), queries(2, 1, scopy), queries(1, 1, scopy)]),
-                ]
-            for half in range(2):
-                for pair in pairs_of(w - 1)[half : half + 1]:
-                    four_multiply(pair)
+                jobs = [[], [first_split, last_split], [sigmoids_next] * 2, [sigmoids_next] * 2]
+            for half, couple in enumerate(couples_of(w - 1)):
+                four_multiply(couple)
                 if half == 0:
-                    for step in z_steps[2:4]:
+                    for step in z_steps[2:]:
                         three_z(step)
                 else:
-                    for step in long:
+                    for step in long_steps:
                         long_two(step)
-                for step in steps_of(w)[2 * half : 2 * half + 2] if w else ():
-                    four_add(step)
-                for row in (2 * half, 2 * half + 1):
-                    if (w, row) == (0, 3):
-                        three_upper(0)
-                        three_upper(1)
-                    for step in at(w + 1, row):
-                        four_unit(step, fills[row][0], fills[row][1])
-                    if row == 0 and w:
-                        scores_ahead()
-                        scores_ahead()
+                four_add(couples_of(w)[half])
+                for row in (COUPLE * half, COUPLE * half + 1):
+                    if w + 1 < BLOCKS:
+                        four_unit(steps_of(w + 1)[row], jobs[row])
                     if row == 0:
-                        for block in blocks(w - 2):
-                            store(3, block, vcopy if w == 2 else scopy)
-                    if row == 2:
-                        for block in blocks(w - 2):
-                            store(2, block, vcopy if w == 2 else scopy)
-                    if w + 1 >= BLOCKS:
-                        for job in fills[row][0] + fills[row][1]:
-                            job()
+                        scores_ahead()
+                        scores_ahead()
+                    for block in finished:
+                        if row == 0:
+                            store(3, block, copy)
+                        if row == 2:
+                            store(2, block, copy)
+                    if w + 1 == BLOCKS:
+                        for one in jobs[row]:
+                            one()
                 if half == 0:
-                    for block in blocks(w - 2):
+                    for block in finished:
                         product(2, block)
                 else:
-                    for block in blocks(twos_at.get(w - 1, -1)):
+                    for block in finished:
                         product(1, block)
-                for pair in pairs_of(w - 1)[half : half + 1]:
-                    four_quantise(pair)
-            if w:
-                logarithms(w)
-            for block in blocks(twos_at.get(w - 1, -1)):
-                store(1, block, vcopy if w == 2 else scopy)
-            for step in steps_of(w)[0 : 2 if w + 1 < BLOCKS else STEPS] if w else ():
+                four_quantise(couple)
+            three_ln(w)
+            four_ln()
+            for block in finished:
+                store(1, block, copy)
+            for step in steps_of(w)[: 2 if w + 1 < BLOCKS else STEPS]:
                 three_upper(step)
-            for block in blocks(w - 1):
-                three_multiply(block)
-            for block in blocks(two_block):
+            three_multiply(w - 1)
+            for block in two_at[w]:
                 two_quantise(block)
-            for block in blocks(w - 1):
-                three_quantise(block)
+            three_quantise(w - 1)
 
         last = BLOCKS - 1
+        first_couple, last_couple = couples_of(last)
         product(3, last - 1)
         product(2, last - 1)
-        four_reciprocal(last)
+        four_reciprocal()
         three_guard(last)
         for step in steps_of(last):
             three_z(step)
-        phase(2, -1)
-        phase(3, -1)
+        open_phase((last - 1, last), ())
         scores_ahead()
         scores_ahead()
-        for i in range(STEPS):
+        for _ in range(STEPS):
             sigmoids_next()
-        three_split(6)
-        three_split(7)
-        four_multiply(6)
+        for chunk in chunks_of(last):
+            three_split(chunk)
+        four_multiply(first_couple)
         store(3, last - 1, scopy)
         store(2, last - 1, scopy)
-        four_quantise(6)
-        four_multiply(7)
-        two_quantise(2)
-        product(1, 2)
-        for i in range(STEPS):
+        four_quantise(first_couple)
+        four_multiply(last_couple)
+        two_quantise(last - 1)
+        product(1, last - 1)
+        for _ in range(STEPS):
             sigmoids_next()
         three_multiply(last)
-        four_quantise(7)
+        four_quantise(last_couple)
         product(3, last)
         three_quantise(last)
         product(2, last)
         store(3, last, scopy)
-        store(1, 2, scopy)
-        two_quantise(3)
+        store(1, last - 1, scopy)
+        two_quantise(last)
         store(2, last, scopy)
-        product(1, 3)
-        store(1, 3, vcopy)
+        product(1, last)
+        store(1, last, vcopy)

import math

import concourse.masks as masks
import concourse.mybir as mybir

F32 = mybir.dt.float32
BF16 = mybir.dt.bfloat16
U32 = mybir.dt.uint32
U8 = mybir.dt.uint8
FP8X4 = mybir.dt.float8_e4m3fn_x4
ACT = mybir.ActivationFunctionType
ALU = mybir.AluOpType

P = 128
PACK = 4
L = 1024
E = 128
PASSES = L // (P * PACK)
CHUNKS = L // P
SCALE = 1.0 / math.sqrt(E)
PAIRS = 9
NEGATED_PAIRS = (1, 3)
TINY = 2.0**-62

BLOCK_CHUNKS = 2
STEPS = BLOCK_CHUNKS * PASSES
HEAD_STEPS = CHUNKS * PASSES
BLOCKS = HEAD_STEPS // STEPS
COUPLE = 2
LONG_CHUNK = 6

FLOPS = 2 * 2 * PAIRS * L * L * E


def first_pair(x):
    return x * (x + 1) // 2 - 1


def tile_anomalyattention_pa_kernel(tc, q_plus, key_plus, retrieval, out):
    nc = tc.nc
    vcopy = nc.vector.tensor_copy
    scopy = nc.scalar.copy
    q_view = q_plus[0].rearrange("(p c) x e -> p c x e", c=CHUNKS)
    out_view = out[0].rearrange("(p c) x e -> p c x e", c=CHUNKS)

    with tc.manual_schedule(), tc.tile_pool(name="keep", bufs=1) as keep, tc.tile_pool(
        name="work", bufs=2
    ) as work, tc.psum_pool(name="psum", bufs=1) as psum:
        ident = keep.tile([P, P], BF16, name="ident")
        masks.make_identity(nc, ident[:])
        q_t = keep.tile([P, 3, CHUNKS, P], BF16, name="q_t")
        k_t = keep.tile([P, PAIRS, PASSES, PACK, P], BF16, name="k_t")
        r_codes = keep.tile([P, PAIRS, PASSES, E], U32, name="r_codes", align_bytes=64)
        r_scales = keep.tile([P, PAIRS, PASSES, E], U8, name="r_scales", align_bytes=64)
        den = keep.tile([P, STEPS, 2, P, PACK], F32, name="den")
        tiny = keep.tile([P, 1], F32, name="tiny")
        nc.vector.memset(tiny[:], TINY)

        def raw(tag, bufs, pairs, source):
            room = work.tile([P, len(pairs), PASSES, PACK, E], BF16, tag=tag, bufs=bufs, name="raw", align_bytes=64)
            return {
                pair: (room[:, i, :, :, :], source[0, pair].rearrange("(g p t) e -> p g t e", g=PASSES, t=PACK))
                for i, pair in enumerate(pairs)
            }

        def load(raws, pair):
            nc.sync.dma_start(out=raws[pair][0], in_=raws[pair][1])

        q_raw = work.tile([P, CHUNKS, 3, E], BF16, tag="codes3", bufs=1, name="q_raw", align_bytes=64)
        k_raw = raw("three_series", 1, (5, 6, 7, 8, 3, 4), key_plus)
        k_raw.update(raw("codes2", 1, (2, 0, 1), key_plus))
        r_raw = raw("four_series", 1, (5, 6, 7, 8), retrieval)
        load(k_raw, 5)
        nc.sync.dma_start(out=q_raw[:, 0:PACK, :, :], in_=q_view[:, 0:PACK, :, :])
        for pair in (6, 7, 8, 3, 4, 2):
            load(k_raw, pair)
        nc.sync.dma_start(out=q_raw[:, PACK:CHUNKS, :, :], in_=q_view[:, PACK:CHUNKS, :, :])
        load(k_raw, 0)
        load(k_raw, 1)
        for pair in (5, 6, 7, 8, 0, 1, 2, 3, 4):
            if pair not in r_raw:
                r_raw.update(raw("r_raw", 2, (pair,), retrieval))
            load(r_raw, pair)

        def bank(shape, dtype, name):
            return psum.tile(shape, dtype, tag="bank", bufs=8, name=name)

        def flip(sources):
            flipped = bank([P, PACK, P], BF16, "flipped")
            for i, source in enumerate(sources):
                nc.tensor.transpose(flipped[:, i, :], source, ident[:])
            return flipped

        def ready_queries(x, half, copy):
            chunks = range(half * PACK, (half + 1) * PACK)
            flipped = flip([q_raw[:, c, x - 1, :] for c in chunks])
            copy(out=q_t[:, x - 1, chunks[0] : chunks[-1] + 1, :], in_=flipped[:])

        def ready_keys(pair, g, copy):
            flipped = flip([k_raw[pair][0][:, g, t, :] for t in range(PACK)])
            if pair in NEGATED_PAIRS:
                nc.scalar.activation(out=k_t[:, pair, g, :, :], in_=flipped[:], func=ACT.Copy, scale=-1.0)
            else:
                copy(out=k_t[:, pair, g, :, :], in_=flipped[:])

        value_runs = ((5, 4), (0, 4), (4, 1))
        grouped = {}

        def group_values():
            room = work.tile([P, 8, PASSES, E, PACK], BF16, tag="halves", bufs=2, name="room", align_bytes=64)
            rest = keep.tile([P, 1, PASSES, E, PACK], BF16, name="rest", align_bytes=64)
            grouped[5] = room[:, 0:4, :, :, :]
            grouped[0] = room[:, 4:8, :, :, :]
            grouped[4] = rest[:]
            for first, n in value_runs:
                for i in range(n):
                    nc.gpsimd.tensor_scalar(
                        out=grouped[first][:, i, :, :, :],
                        in0=r_raw[first + i][0].rearrange("p g t e -> p g e t"),
                        scalar1=1.0,
                        scalar2=0.0,
                        op0=ALU.mult,
                        op1=ALU.add,
                    )

        def quantise_values():
            for first, n in value_runs:
                nc.vector.quantize_mx(
                    out=r_codes[:, first : first + n, :, :].rearrange("p a g e -> p (a g e)").bitcast(FP8X4),
                    scales=r_scales[:, first : first + n, :, :].rearrange("p a g e -> p (a g e)"),
                    in_=grouped[first].rearrange("p a g e t -> p (a g e t)"),
                )

        def by_query(scores):
            return scores[:].rearrange("p t l -> p l t")

        def chunk_and_pass(x, step):
            if x < 3:
                return divmod(step, PASSES)
            block, j = divmod(step, STEPS)
            return block * BLOCK_CHUNKS + j % BLOCK_CHUNKS, j // BLOCK_CHUNKS

        def score(x, step, pairs, name):
            c, g = chunk_and_pass(x, step)
            scores = bank([P, PACK, P], F32, name)
            for t in range(PACK):
                for pair in pairs:
                    nc.tensor.matmul(
                        scores[:, t, :],
                        lhsT=k_t[:, pair, g, t, :],
                        rhs=q_t[:, x - 1, c, :],
                        start=(pair == pairs[0]),
                        stop=(pair == pairs[-1]),
                    )
            return scores

        packed = {}

        def quantise(x, block, first, n, series):
            if (x, block) not in packed:
                shape = [P, STEPS * (x + 1), P]
                packed[x, block] = (
                    work.tile(shape, U32, tag="codes%d" % x, bufs=1, name="codes", align_bytes=64),
                    work.tile(shape, U8, tag="scales%d" % x, bufs=1, name="scales", align_bytes=64),
                )
            codes, scales = packed[x, block]
            nc.vector.quantize_mx(
                out=codes[:, first : first + n, :].rearrange("p y l -> p (y l)").bitcast(FP8X4),
                scales=scales[:, first : first + n, :].rearrange("p y l -> p (y l)"),
                in_=series,
            )

        def row_of(x, c, g, y):
            return (g * BLOCK_CHUNKS + c) * (x + 1) + y if x == 3 else y * STEPS + c * PASSES + g

        sums = {}

        def product(x, block):
            codes, scales = packed[x, block]
            sums[x, block] = bank([P, BLOCK_CHUNKS, E], F32, "sums")
            terms = [(g, y) for g in range(PASSES) for y in range(x + 1)]
            for c in range(BLOCK_CHUNKS):
                for g, y in terms:
                    nc.tensor.matmul_mx(
                        out=sums[x, block][:, c, :],
                        lhsT=codes[:, row_of(x, c, g, y), :].bitcast(FP8X4),
                        lhsT_scale=scales[:, row_of(x, c, g, y), :],
                        rhs=r_codes[:, first_pair(x) + y, g, :].bitcast(FP8X4),
                        rhs_scale=r_scales[:, first_pair(x) + y, g, :],
                        start=((g, y) == terms[0]),
                        stop=((g, y) == terms[-1]),
                    )

        def store(x, block, copy):
            result = work.tile([P, BLOCK_CHUNKS, E], F32, name="result")
            copy(out=result[:], in_=sums[x, block][:])
            chunks = slice(block * BLOCK_CHUNKS, (block + 1) * BLOCK_CHUNKS)
            nc.sync.dma_start(out=out_view[:, chunks, x - 1, :], in_=result[:])

        differences = {}
        two_series = {}

        def two_scores(step):
            differences[1, step] = score(1, step, (0, 1), "difference")

        def two_sigmoids(step):
            source = by_query(differences[1, step])
            block, j = divmod(step, STEPS)
            if j == 0:
                two_series[block] = work.tile(
                    [P, 2, STEPS, P, PACK], BF16, tag="two_series", bufs=1, name="two_series", align_bytes=64
                )
            nc.scalar.activation(out=two_series[block][:, 0, j, :, :], in_=source, func=ACT.Sigmoid, scale=SCALE)
            nc.scalar.activation(out=two_series[block][:, 1, j, :, :], in_=source, func=ACT.Sigmoid, scale=-SCALE)

        def two_quantise(block):
            quantise(1, block, 0, 2 * STEPS, two_series[block][:].rearrange("p y j l t -> p (y j l t)"))

        lower = {}
        halves = {}
        odds = {}
        upper = {}
        minus_one = {}
        three_series = {}

        def planes(name):
            return work.tile([P, STEPS, P, PACK], F32, tag="planes", bufs=3, name=name)

        def is_long(step):
            return step // PASSES == LONG_CHUNK

        def long_one(step):
            one = score(2, step, (3,), "one")
            minus_one[step] = work.tile([P, P, PACK], F32, tag="plane", bufs=3, name="minus_one")
            nc.scalar.copy(out=minus_one[step][:], in_=by_query(one))

        def long_two(step):
            two = score(2, step, (4,), "two")
            block, j = divmod(step, STEPS)
            if j == 0:
                lower[block] = planes("lower")
            nc.vector.tensor_tensor(
                out=lower[block][:, j, :, :], in0=by_query(two), in1=minus_one[step][:], op=ALU.add
            )

        def three_scores(step):
            if not is_long(step):
                differences[2, step] = score(2, step, (4, 3), "difference")

        def three_sigmoids(step):
            block, j = divmod(step, STEPS)
            if j == 0:
                halves[block] = work.tile(
                    [P, 2, STEPS, P, PACK], F32, tag="halves", bufs=2, name="halves", align_bytes=64
                )
            if is_long(step):
                source = lower[block][:, j, :, :]
            else:
                source = by_query(differences[2, step])
                if j == 0:
                    lower[block] = planes("lower")
            nc.scalar.activation(out=halves[block][:, 0, j, :, :], in_=source, func=ACT.Sigmoid, scale=-SCALE)
            nc.scalar.activation(out=halves[block][:, 1, j, :, :], in_=source, func=ACT.Sigmoid, scale=SCALE)
            if not is_long(step):
                nc.scalar.copy(out=lower[block][:, j, :, :], in_=source)

        def three_ln(block):
            odds[block] = planes("odds")
            nc.scalar.activation(out=odds[block][:], in_=halves[block][:, 0, :, :, :], func=ACT.Ln, bias=tiny[:])

        def three_guard(block):
            nc.vector.scalar_tensor_tensor(
                out=odds[block][:], in0=lower[block][:], scalar=-SCALE, in1=odds[block][:], op0=ALU.mult, op1=ALU.min
            )

        def three_upper(step):
            upper[step] = score(2, step, (2,) if is_long(step) else (2, 3), "upper")

        def three_z(step):
            block, j = divmod(step, STEPS)
            source = by_query(upper[step])
            if is_long(step):
                nc.vector.tensor_tensor(out=minus_one[step][:], in0=source, in1=minus_one[step][:], op=ALU.add)
                source = minus_one[step][:]
            here = odds[block][:, j, :, :]
            nc.vector.scalar_tensor_tensor(out=here, in0=source, scalar=SCALE, in1=here, op0=ALU.mult, op1=ALU.add)

        def three_split(chunk):
            block, c = divmod(chunk, BLOCK_CHUNKS)
            if c == 0:
                three_series[block] = work.tile(
                    [P, 3, STEPS, P, PACK], BF16, tag="three_series", bufs=1, name="three_series", align_bytes=64
                )
            steps = slice(c * PASSES, (c + 1) * PASSES)
            z = odds[block][:, steps, :, :]
            nc.scalar.activation(out=three_series[block][:, 0, steps, :, :], in_=z, func=ACT.Sigmoid)
            nc.scalar.activation(out=z, in_=z, func=ACT.Sigmoid, scale=-1.0)

        def three_multiply(block):
            nc.vector.tensor_tensor(
                out=three_series[block][:, 1:3, :, :, :],
                in0=halves[block][:],
                in1=odds[block][:].unsqueeze(1).to_broadcast([P, 2, STEPS, P, PACK]),
                op=ALU.mult,
            )

        def three_quantise(block):
            series = three_series[block]
            quantise(2, block, 0, 2 * STEPS, series[:, 0:2, :, :, :].rearrange("p y j l t -> p (y j l t)"))
            quantise(2, block, 2 * STEPS, STEPS, series[:, 2, :, :, :].rearrange("p j l t -> p (j l t)"))

        scores_of = {}
        top = {}
        expo = {}
        four_series = {}

        def four_score(step, y):
            if step < HEAD_STEPS:
                scores_of[step, y] = score(3, step, (first_pair(3) + y,), "scores")

        def four_copy(step):
            if step < HEAD_STEPS:
                top[step] = work.tile([P, P, PACK], F32, tag="plane", bufs=3, name="top")
                nc.scalar.copy(out=top[step][:], in_=by_query(scores_of[step, 0]))

        def raise_top(step, y):
            if step < HEAD_STEPS:
                nc.vector.tensor_tensor(
                    out=top[step][:], in0=by_query(scores_of[step, y]), in1=top[step][:], op=ALU.max
                )

        def subtract_top(step, y):
            couple, i = divmod(step, COUPLE)
            if y == 0 and i == 0:
                expo[couple] = work.tile([P, COUPLE, 4, P, PACK], F32, tag="expo", bufs=4, name="expo")
            nc.vector.tensor_tensor(
                out=expo[couple][:, i, y, :, :], in0=by_query(scores_of[step, y]), in1=top[step][:], op=ALU.subtract
            )

        def four_unit(step, before=(), after=()):
            jobs = list(before)

            def one_job():
                if jobs:
                    jobs.pop(0)()

            four_score(step + 1, 1)
            subtract_top(step, 0)
            four_score(step + 1, 2)
            raise_top(step + 1, 1)
            one_job()
            subtract_top(step, 1)
            four_score(step + 1, 3)
            raise_top(step + 1, 2)
            one_job()
            subtract_top(step, 2)
            four_score(step + 2, 0)
            while jobs:
                one_job()
            four_copy(step + 2)
            raise_top(step + 1, 3)
            subtract_top(step, 3)
            for one in after:
                one()

        def four_exp(these):
            nc.scalar.activation(out=these, in_=these, func=ACT.Exp, scale=SCALE)

        def exponentials(step):
            couple, i = divmod(step, COUPLE)
            return expo[couple][:, i, :, :, :]

        def four_add(couple):
            adder = nc.gpsimd if couple < couples_of(BLOCKS - 1)[0] else nc.vector
            e = expo[couple]
            first = COUPLE * couple % STEPS
            here = den[:, first : first + COUPLE, :, :, :]
            adder.tensor_tensor(out=here, in0=e[:, :, 0:2, :, :], in1=e[:, :, 2:4, :, :], op=ALU.add)
            adder.tensor_tensor(
                out=here[:, :, 0, :, :], in0=here[:, :, 0, :, :], in1=here[:, :, 1, :, :], op=ALU.add
            )

        def four_ln():
            nc.scalar.activation(out=den[:, :, 0, :, :], in_=den[:, :, 0, :, :], func=ACT.Ln)

        def four_reciprocal():
            nc.scalar.activation(out=den[:, :, 0, :, :], in_=den[:, :, 0, :, :], func=ACT.Exp, scale=-1.0)

        def four_multiply(couple):
            four_series[couple] = work.tile(
                [P, COUPLE, 4, P, PACK], BF16, tag="four_series", bufs=1, name="four_series", align_bytes=64
            )
            first = COUPLE * couple % STEPS
            nc.vector.tensor_tensor(
                out=four_series[couple][:],
                in0=expo[couple][:],
                in1=den[:, first : first + COUPLE, 0, :, :].unsqueeze(2).to_broadcast([P, COUPLE, 4, P, PACK]),
                op=ALU.mult,
            )

        def four_quantise(couple):
            block, i = divmod(couple, STEPS // COUPLE)
            rows = COUPLE * 4
            quantise(3, block, rows * i, rows, four_series[couple][:].rearrange("p i y l t -> p (i y l t)"))

        def job(function, *arguments):
            return lambda: function(*arguments)

        def steps_of(block):
            return range(block * STEPS, (block + 1) * STEPS)

        def chunks_of(block):
            return range(block * BLOCK_CHUNKS, (block + 1) * BLOCK_CHUNKS)

        def couples_of(block):
            return range(block * STEPS // COUPLE, (block + 1) * STEPS // COUPLE)

        items = []
        asked = []
        done = []

        def scores_ahead():
            if len(asked) < len(items):
                asked.append(items[len(asked)])
                scores, _, step = asked[-1]
                scores(step)

        def sigmoids_next():
            done.append(items[len(done)])
            _, sigmoids, step = done[-1]
            sigmoids(step)
            scores_ahead()

        def open_phase(two_blocks, three_blocks):
            for block in two_blocks:
                items.extend([(two_scores, two_sigmoids, step) for step in steps_of(block)])
            for block in three_blocks:
                items.extend([(three_scores, three_sigmoids, step) for step in steps_of(block)])

        ready_keys(5, 0, vcopy)
        ready_queries(3, 0, vcopy)
        for pair in (6, 7, 8):
            ready_keys(pair, 0, vcopy)
        for y in range(4):
            four_score(0, y)
        four_copy(0)
        four_score(1, 0)
        for y in range(1, 4):
            raise_top(0, y)
        four_copy(1)
        group_values()
        flips = [
            [
                job(ready_keys, 5, 1, scopy),
                job(ready_keys, 6, 1, scopy),
                job(ready_keys, 7, 1, vcopy),
                job(ready_keys, 8, 1, vcopy),
            ],
            [job(ready_queries, 2, 0, scopy), job(ready_keys, 3, 0, scopy), job(ready_keys, 4, 0, scopy)],
            [job(ready_keys, 3, 1, scopy), job(ready_keys, 4, 1, scopy)],
            [job(ready_keys, 2, 0, scopy), job(ready_keys, 2, 1, scopy)],
        ]
        for step in steps_of(0):
            four_unit(step, flips[step][:2], flips[step][2:])
            four_exp(exponentials(step))
            if step % COUPLE == COUPLE - 1:
                four_add(step // COUPLE)

        open_phase((), (0,))
        scores_ahead()
        scores_ahead()
        four_unit(4, [sigmoids_next, sigmoids_next], [job(ready_queries, 3, 1, scopy)])
        four_unit(5, [sigmoids_next, sigmoids_next], [job(three_ln, 0)])
        four_unit(6, [], [four_ln])
        three_upper(0)
        three_upper(1)
        four_unit(
            7,
            [four_reciprocal],
            [
                job(ready_queries, 1, 0, scopy),
                job(ready_keys, 0, 0, scopy),
                job(ready_keys, 1, 0, scopy),
                job(ready_keys, 0, 1, scopy),
                job(ready_keys, 1, 1, scopy),
                job(ready_queries, 2, 1, scopy),
                job(ready_queries, 1, 1, scopy),
            ],
        )

        two_at = {1: (0,), 2: (1,), 3: ()}
        for w in range(1, BLOCKS):
            copy = vcopy if w == 2 else scopy
            finished = [w - 2] if w > 1 else []
            long_steps = [step for step in steps_of(w) if is_long(step)]
            z_steps = steps_of(w - 1)

            for block in finished:
                product(3, block)
                four_reciprocal()
            three_guard(w - 1)
            if w == 1:
                quantise_values()
            for step in z_steps[:2]:
                three_z(step)
            for step in z_steps[2:]:
                three_upper(step)
            for couple in couples_of(w):
                four_exp(expo[couple][:])
            for step in long_steps:
                long_one(step)

            open_phase(two_at[w], (w,))
            first_split, last_split = [job(three_split, chunk) for chunk in chunks_of(w - 1)]
            if two_at[w]:
                jobs = [[], [first_split, sigmoids_next, sigmoids_next, last_split], [sigmoids_next] * 3, [sigmoids_next] * 3]
            else:
                jobs = [[], [first_split, last_split], [sigmoids_next] * 2, [sigmoids_next] * 2]
            for half, couple in enumerate(couples_of(w - 1)):
                four_multiply(couple)
                if half == 0:
                    for step in z_steps[2:]:
                        three_z(step)
                else:
                    for step in long_steps:
                        long_two(step)
                four_add(couples_of(w)[half])
                for row in (COUPLE * half, COUPLE * half + 1):
                    if w + 1 < BLOCKS:
                        four_unit(steps_of(w + 1)[row], jobs[row])
                    if row == 0:
                        scores_ahead()
                        scores_ahead()
                    for block in finished:
                        if row == 0:
                            store(3, block, copy)
                        if row == 2:
                            store(2, block, copy)
                    if w + 1 == BLOCKS:
                        for one in jobs[row]:
                            one()
                if half == 0:
                    for block in finished:
                        product(2, block)
                else:
                    for block in finished:
                        product(1, block)
                four_quantise(couple)
            three_ln(w)
            four_ln()
            for block in finished:
                store(1, block, copy)
            for step in steps_of(w)[: 2 if w + 1 < BLOCKS else STEPS]:
                three_upper(step)
            three_multiply(w - 1)
            for block in two_at[w]:
                two_quantise(block)
            three_quantise(w - 1)

        last = BLOCKS - 1
        first_couple, last_couple = couples_of(last)
        product(3, last - 1)
        product(2, last - 1)
        four_reciprocal()
        three_guard(last)
        for step in steps_of(last):
            three_z(step)
        open_phase((last - 1, last), ())
        scores_ahead()
        scores_ahead()
        for _ in range(STEPS):
            sigmoids_next()
        for chunk in chunks_of(last):
            three_split(chunk)
        four_multiply(first_couple)
        store(3, last - 1, scopy)
        store(2, last - 1, scopy)
        four_quantise(first_couple)
        four_multiply(last_couple)
        two_quantise(last - 1)
        product(1, last - 1)
        for _ in range(STEPS):
            sigmoids_next()
        three_multiply(last)
        four_quantise(last_couple)
        product(3, last)
        three_quantise(last)
        product(2, last)
        store(3, last, scopy)
        store(1, last - 1, scopy)
        two_quantise(last)
        store(2, last, scopy)
        product(1, last)
        store(1, last, vcopy)
